import numpy as np
import ml_dtypes


def mxq(x, axis, fmt="e4m3"):
    dtype, down = {"e4m3": (ml_dtypes.float8_e4m3fn, 7), "e5m2": (ml_dtypes.float8_e5m2, 14)}[fmt]
    v = np.moveaxis(np.asarray(x, np.float32).astype(ml_dtypes.bfloat16).astype(np.float64), axis, -1)
    blocks = v.reshape(v.shape[:-1] + (-1, 32))
    amax = np.abs(blocks).max(-1, keepdims=True)
    byte = np.maximum(np.where(amax > 0, np.frexp(amax)[1] - 1 + 127, 0) - down, 1)
    scale = np.exp2(byte - 127.0)
    codes = (blocks / scale).astype(np.float32).astype(dtype).astype(np.float64)
    return np.moveaxis((codes * scale).reshape(v.shape), -1, axis)


WIDE = False


def mx_kscale(k):
    if not WIDE:
        return np.ones(k)
    levels = np.array([10, -10, 5, -5, 0])
    a = np.random.permutation(np.resize(levels, k // 512 * 4)).reshape(k // 512, 4)
    idx = np.arange(k)
    return np.exp2(a[idx // 512, idx % 128 // 32])


BF16 = ml_dtypes.bfloat16


def bf(x):
    return np.asarray(x, np.float32).astype(BF16)


def f64(x):
    return np.asarray(x).astype(np.float64)


B, S, D, F, G, K = 2, 256, 512, 2048, 5, 3
N = B * S
NB = G + K
C = F * NB


def silu(v):
    e = np.exp(-np.abs(v))
    return v * np.where(v >= 0, 1.0, e) / (1.0 + e)


def b_splines(x, grid, k):
    x = x[..., None]
    bases = np.where((x >= grid[:-1]) & (x < grid[1:]), 1.0, 0.0)
    for j in range(1, k + 1):
        left = (x - grid[: -(j + 1)]) / (grid[j:-1] - grid[: -(j + 1)])
        right = (grid[j + 1:] - x) / (grid[j + 1:] - grid[1:-j])
        bases = left * bases[..., :-1] + right * bases[..., 1:]
    return bases


def setup_inputs():
    t = np.maximum(mx_kscale(F), 1.0) ** 2
    return {"h": bf(np.random.standard_normal((N, F)) * 0.9 * t),
            "grid": bf(np.arange(-K, G + K + 1) * (2.0 / G) - 1.0),
            "w2_base": bf(np.random.standard_normal((D, F)) / np.sqrt(F) / t),
            "w2_spline": bf(np.random.standard_normal((D, F, NB)) / np.sqrt(F))}


def reference(h, grid, w2_base, w2_spline):
    hf = f64(h)
    base = mxq(silu(hf), 1, "e4m3") @ mxq(f64(w2_base), 1, "e4m3").T
    bases = b_splines(hf, f64(grid), K).reshape(N, C)
    spline = mxq(bases, 1, "e4m3") @ mxq(f64(w2_spline).reshape(D, C), 1, "e4m3").T
    return (base + spline).reshape(B, S, D)

@@ -1,0 +1,286 @@
+from contextlib import ExitStack
+
+import concourse.masks as masks
+import concourse.mybir as mybir
+
+F32 = mybir.dt.float32
+BF16 = mybir.dt.bfloat16
+U32 = mybir.dt.uint32
+U8 = mybir.dt.uint8
+FP8X4 = mybir.dt.float8_e4m3fn_x4
+ALU = mybir.AluOpType
+ACT = mybir.ActivationFunctionType
+
+P = 128
+PACK = 4
+TOKENS = 512
+FEATURES = 2048
+OUTPUTS = 512
+BASES = 8
+KNOTS = 12
+TOKEN_TILES = TOKENS // P
+OUTPUT_TILES = OUTPUTS // P
+FEATURE_TILES = FEATURES // P
+BASE_PASSES = FEATURES // (P * PACK)
+BASIS_GROUPS = BASES // PACK
+TILES_PER_BATCH = 2
+BATCHES = FEATURE_TILES // TILES_PER_BATCH
+BATCH_COLS = TILES_PER_BATCH * TOKENS
+LAST_UP = 8
+FIRST_DOWN = 3
+WORDS_PER_FEATURE = BASES // 2
+
+FLOPS = 2 * TOKENS * OUTPUTS * (FEATURES + FEATURES * BASES)
+
+
+def knot_constants(nc, consts, grid):
+    knots_bf = consts.tile([P, KNOTS], BF16)
+    nc.sync.dma_start(out=knots_bf[:], in_=grid.partition_broadcast(P))
+    knots = consts.tile([P, KNOTS], F32)
+    nc.vector.tensor_copy(out=knots[:], in_=knots_bf[:])
+    neg_knots = consts.tile([P, KNOTS], F32)
+    nc.vector.tensor_scalar_mul(out=neg_knots[:], in0=knots[:], scalar1=-1.0)
+
+    span = {}
+    for k in range(1, 5):
+        span[k] = consts.tile([P, KNOTS - k], F32, name="span%d" % k)
+        nc.vector.tensor_sub(out=span[k][:], in0=knots[:, k:KNOTS], in1=knots[:, 0 : KNOTS - k])
+
+    n_up = LAST_UP + 1
+    up_two = consts.tile([P, n_up], F32)
+    nc.vector.tensor_mul(out=up_two[:], in0=span[1][:, 0:n_up], in1=span[2][:, 0:n_up])
+    up_three = consts.tile([P, n_up], F32)
+    nc.vector.tensor_mul(out=up_three[:], in0=up_two[:], in1=span[3][:, 0:n_up])
+    up_scale = consts.tile([P, n_up], F32)
+    nc.vector.reciprocal(out=up_scale[:], in_=up_three[:])
+
+    n_down = KNOTS - FIRST_DOWN
+    down_two = consts.tile([P, n_down], F32)
+    nc.vector.tensor_mul(out=down_two[:], in0=span[1][:, 2 : 2 + n_down], in1=span[2][:, 1 : 1 + n_down])
+    down_three = consts.tile([P, n_down], F32)
+    nc.vector.tensor_mul(out=down_three[:], in0=down_two[:], in1=span[3][:, 0:n_down])
+    down_scale = consts.tile([P, n_down], F32)
+    nc.vector.reciprocal(out=down_scale[:], in_=down_three[:])
+    neg_down_scale = consts.tile([P, n_down], F32)
+    nc.vector.tensor_scalar_mul(out=neg_down_scale[:], in0=down_scale[:], scalar1=-1.0)
+
+    inv_span1 = consts.tile([P, KNOTS - 1], F32)
+    nc.vector.reciprocal(out=inv_span1[:], in_=span[1][:])
+    neg_rise_ratio = consts.tile([P, BASES], F32)
+    nc.vector.scalar_tensor_tensor(
+        out=neg_rise_ratio[:], in0=span[4][:], scalar=-1.0, in1=inv_span1[:, 0:BASES],
+        op0=ALU.mult, op1=ALU.mult,
+    )
+    neg_fall_ratio = consts.tile([P, BASES], F32)
+    nc.vector.scalar_tensor_tensor(
+        out=neg_fall_ratio[:], in0=span[4][:], scalar=-1.0, in1=inv_span1[:, 3 : 3 + BASES],
+        op0=ALU.mult, op1=ALU.mult,
+    )
+    return {
+        "knots": knots,
+        "neg_knots": neg_knots,
+        "up_scale": up_scale,
+        "neg_down_scale": neg_down_scale,
+        "neg_rise_ratio": neg_rise_ratio,
+        "neg_fall_ratio": neg_fall_ratio,
+    }
+
+
+def quantise_128_rows(nc, turn, stage, ident_bf, rows_sb, codes, scales, first_col):
+    cols = slice(first_col, first_col + P)
+    for c in range(BASE_PASSES):
+        turned = turn.tile([P, PACK, P], BF16, tag="turn")
+        for t in range(PACK):
+            first = (c * PACK + t) * P
+            nc.tensor.transpose(turned[:, t, :], rows_sb[:, first : first + P], ident_bf[:])
+        grouped = stage.tile([P, P, PACK], BF16, align_bytes=64, tag="rows_grouped")
+        nc.vector.tensor_copy(out=grouped[:], in_=turned[:].rearrange("p t r -> p r t"))
+        nc.vector.quantize_mx(
+            out=codes[:, c, cols].bitcast(FP8X4),
+            scales=scales[:, c, cols],
+            in_=grouped[:].rearrange("p r t -> p (r t)"),
+        )
+
+
+def tile_kanblock_pb_kernel(tc, h, grid, w2_base, w2_spline, out):
+    nc = tc.nc
+    out_rows = out.flatten_outer_dims()
+    spline_rows = w2_spline.rearrange("(dt p) i g -> p dt (i g)", p=P)
+
+    with ExitStack() as ctx:
+        consts = ctx.enter_context(tc.tile_pool(name="consts", bufs=1))
+        keep = ctx.enter_context(tc.tile_pool(name="keep", bufs=1))
+        rows = ctx.enter_context(tc.tile_pool(name="rows", bufs=2))
+        stage = ctx.enter_context(tc.tile_pool(name="stage", bufs=2))
+        work = ctx.enter_context(tc.tile_pool(name="work", bufs=2))
+        cubes = ctx.enter_context(tc.tile_pool(name="cubes", bufs=3))
+        operands = ctx.enter_context(tc.tile_pool(name="operands", bufs=2))
+        sums = ctx.enter_context(tc.psum_pool(name="sums", bufs=1))
+        turn = ctx.enter_context(tc.psum_pool(name="turn", bufs=4))
+
+        ident_bf = consts.tile([P, P], BF16)
+        masks.make_identity(nc, ident_bf[:])
+        ident_f32 = consts.tile([P, P], F32)
+        masks.make_identity(nc, ident_f32[:])
+        k = knot_constants(nc, consts, grid)
+
+        acc = [sums.tile([P, OUTPUTS], F32, name="acc%d" % tt) for tt in range(TOKEN_TILES)]
+
+        x_all = keep.tile([P, FEATURE_TILES, TOKENS], BF16)
+        silu_codes = keep.tile([P, BASE_PASSES, TOKENS], U32, align_bytes=64)
+        silu_scales = keep.tile([P, BASE_PASSES, TOKENS], U8, align_bytes=64)
+        base_codes = keep.tile([P, BASE_PASSES, OUTPUTS], U32, align_bytes=64)
+        base_scales = keep.tile([P, BASE_PASSES, OUTPUTS], U8, align_bytes=64)
+
+        for tt in range(TOKEN_TILES):
+            h_sb = rows.tile([P, FEATURES], BF16)
+            nc.sync.dma_start(out=h_sb[:], in_=h[tt * P : (tt + 1) * P, :])
+            for q in range(FEATURE_TILES // PACK):
+                turned = turn.tile([P, PACK, P], BF16, tag="turn")
+                for t in range(PACK):
+                    first = (q * PACK + t) * P
+                    nc.tensor.transpose(turned[:, t, :], h_sb[:, first : first + P], ident_bf[:])
+                nc.vector.tensor_scalar(
+                    out=x_all[:, q * PACK : (q + 1) * PACK, tt * P : (tt + 1) * P],
+                    in0=turned[:],
+                    scalar1=k["knots"][:, 0:1],
+                    scalar2=k["knots"][:, KNOTS - 1 : KNOTS],
+                    op0=ALU.max,
+                    op1=ALU.min,
+                )
+            silu_sb = rows.tile([P, FEATURES], BF16)
+            nc.scalar.activation(out=silu_sb[:], in_=h_sb[:], func=ACT.Silu)
+            quantise_128_rows(nc, turn, stage, ident_bf, silu_sb, silu_codes, silu_scales, tt * P)
+
+        for dt in range(OUTPUT_TILES):
+            base_sb = rows.tile([P, FEATURES], BF16)
+            nc.sync.dma_start(out=base_sb[:], in_=w2_base[dt * P : (dt + 1) * P, :])
+            quantise_128_rows(nc, turn, stage, ident_bf, base_sb, base_codes, base_scales, dt * P)
+
+        for c in range(BASE_PASSES):
+            for tt in range(TOKEN_TILES):
+                token_cols = slice(tt * P, (tt + 1) * P)
+                nc.tensor.matmul_mx(
+                    out=acc[tt][:],
+                    lhsT=silu_codes[:, c, token_cols].bitcast(FP8X4),
+                    lhsT_scale=silu_scales[:, c, token_cols],
+                    rhs=base_codes[:, c, :].bitcast(FP8X4),
+                    rhs_scale=base_scales[:, c, :],
+                    start=(c == 0),
+                    stop=False,
+                )
+
+        for b in range(BATCHES):
+            row_len = TILES_PER_BATCH * P * BASES
+            w_sb = rows.tile([P, OUTPUT_TILES, row_len], BF16)
+            nc.sync.dma_start(out=w_sb[:], in_=spline_rows[:, :, b * row_len : (b + 1) * row_len])
+            w_words = w_sb[:].bitcast(F32).rearrange(
+                "p dt (f i q) -> p dt f i q", f=TILES_PER_BATCH, q=WORDS_PER_FEATURE
+            )
+            w_codes = {}
+            w_scales = {}
+            for f in range(TILES_PER_BATCH):
+                for a in range(BASIS_GROUPS):
+                    w_grouped = stage.tile([P, OUTPUTS, 2], F32, align_bytes=64)
+                    for half in range(2):
+                        turned = turn.tile([P, 2, 2 * P], F32, tag="turn")
+                        for u in range(2):
+                            for s in range(2):
+                                nc.tensor.transpose(
+                                    turned[:, u, s * P : (s + 1) * P],
+                                    w_words[:, 2 * half + s, f, :, 2 * a + u],
+                                    ident_f32[:],
+                                )
+                        nc.scalar.copy(
+                            out=w_grouped[:, half * 2 * P : (half + 1) * 2 * P, :],
+                            in_=turned[:].rearrange("p u d -> p d u"),
+                        )
+                    w_codes[f, a] = operands.tile(
+                        [P, OUTPUTS], U32, align_bytes=64, name="w_codes", tag="w_codes", bufs=6
+                    )
+                    w_scales[f, a] = operands.tile(
+                        [P, OUTPUTS], U8, align_bytes=64, name="w_scales", tag="w_scales", bufs=6
+                    )
+                    nc.vector.quantize_mx(
+                        out=w_codes[f, a][:].bitcast(FP8X4),
+                        scales=w_scales[f, a][:],
+                        in_=w_grouped[:].rearrange("p d u -> p (d u)").bitcast(BF16),
+                    )
+
+            x = x_all[:, b * TILES_PER_BATCH : (b + 1) * TILES_PER_BATCH, :].rearrange("p f n -> p (f n)")
+            up = {}
+            down = {}
+            rise = {}
+            fall = {}
+            for a in range(BASIS_GROUPS):
+                rise[a] = work.tile([P, PACK, BATCH_COLS], BF16, name="rise", tag="rise")
+                fall[a] = work.tile([P, PACK, BATCH_COLS], BF16, name="fall", tag="fall")
+            for j in range(KNOTS):
+                square = work.tile([P, BATCH_COLS], F32)
+                nc.scalar.activation(
+                    out=square[:], in_=x, func=ACT.Square, bias=k["neg_knots"][:, j : j + 1], scale=1.0
+                )
+                cube = work.tile([P, BATCH_COLS], F32)
+                nc.vector.scalar_tensor_tensor(
+                    out=cube[:], in0=x, scalar=k["knots"][:, j : j + 1], in1=square[:],
+                    op0=ALU.subtract, op1=ALU.mult,
+                )
+                if j <= LAST_UP:
+                    up[j] = cubes.tile([P, BATCH_COLS], F32, name="up", tag="up")
+                    nc.scalar.activation(
+                        out=up[j][:], in_=cube[:], func=ACT.Relu, scale=k["up_scale"][:, j : j + 1]
+                    )
+                if j >= FIRST_DOWN:
+                    down[j] = cubes.tile([P, BATCH_COLS], F32, name="down", tag="down")
+                    nc.scalar.activation(
+                        out=down[j][:], in_=cube[:], func=ACT.Relu,
+                        scale=k["neg_down_scale"][:, j - FIRST_DOWN : j - FIRST_DOWN + 1],
+                    )
+                if 1 <= j <= LAST_UP:
+                    g = j - 1
+                    nc.vector.scalar_tensor_tensor(
+                        out=rise[g // PACK][:, g % PACK, :], in0=up[g + 1][:],
+                        scalar=k["neg_rise_ratio"][:, g : g + 1], in1=up[g][:],
+                        op0=ALU.mult, op1=ALU.add,
+                    )
+                if j >= FIRST_DOWN + 1:
+                    g = j - 4
+                    nc.vector.scalar_tensor_tensor(
+                        out=fall[g // PACK][:, g % PACK, :], in0=down[g + 3][:],
+                        scalar=k["neg_fall_ratio"][:, g : g + 1], in1=down[g + 4][:],
+                        op0=ALU.mult, op1=ALU.add,
+                    )
+                    if g % PACK == PACK - 1:
+                        a = g // PACK
+                        bases = stage.tile([P, BATCH_COLS, PACK], BF16, align_bytes=64)
+                        nc.vector.tensor_tensor(
+                            out=bases[:],
+                            in0=rise[a][:].rearrange("p r n -> p n r"),
+                            in1=fall[a][:].rearrange("p r n -> p n r"),
+                            op=ALU.max,
+                        )
+                        b_codes = operands.tile([P, BATCH_COLS], U32, align_bytes=64)
+                        b_scales = operands.tile([P, BATCH_COLS], U8, align_bytes=64)
+                        nc.vector.quantize_mx(
+                            out=b_codes[:].bitcast(FP8X4),
+                            scales=b_scales[:],
+                            in_=bases[:].rearrange("p n r -> p (n r)"),
+                        )
+                        for f in range(TILES_PER_BATCH):
+                            last = b == BATCHES - 1 and a == BASIS_GROUPS - 1 and f == TILES_PER_BATCH - 1
+                            for tt in range(TOKEN_TILES):
+                                token_cols = slice(f * TOKENS + tt * P, f * TOKENS + (tt + 1) * P)
+                                nc.tensor.matmul_mx(
+                                    out=acc[tt][:],
+                                    lhsT=b_codes[:, token_cols].bitcast(FP8X4),
+                                    lhsT_scale=b_scales[:, token_cols],
+                                    rhs=w_codes[f, a][:].bitcast(FP8X4),
+                                    rhs_scale=w_scales[f, a][:],
+                                    start=False,
+                                    stop=last,
+                                )
+
+        for tt in range(TOKEN_TILES):
+            result = stage.tile([P, OUTPUTS], F32)
+            nc.scalar.copy(out=result[:], in_=acc[tt][:])
+            nc.sync.dma_start(out=out_rows[tt * P : (tt + 1) * P, :], in_=result[:])

@@ -13,6 +13,7 @@ ACT = mybir.ActivationFunctionType
 
 P = 128
 PACK = 4
+K_PASS = P * PACK
 TOKENS = 512
 FEATURES = 2048
 OUTPUTS = 512
@@ -20,15 +21,11 @@ BASES = 8
 KNOTS = 12
 TOKEN_TILES = TOKENS // P
 OUTPUT_TILES = OUTPUTS // P
-FEATURE_TILES = FEATURES // P
-BASE_PASSES = FEATURES // (P * PACK)
-BASIS_GROUPS = BASES // PACK
-TILES_PER_BATCH = 2
-BATCHES = FEATURE_TILES // TILES_PER_BATCH
-BATCH_COLS = TILES_PER_BATCH * TOKENS
-LAST_UP = 8
-FIRST_DOWN = 3
-WORDS_PER_FEATURE = BASES // 2
+CHUNKS = FEATURES // K_PASS
+PAIRS = BASES // 2
+CHUNKS_PER_BATCH = 2
+BATCHES = CHUNKS // CHUNKS_PER_BATCH
+BATCH_COLS = CHUNKS_PER_BATCH * K_PASS
 
 FLOPS = 2 * TOKENS * OUTPUTS * (FEATURES + FEATURES * BASES)
 
@@ -45,60 +42,68 @@ def knot_constants(nc, consts, grid):
     for k in range(1, 5):
         span[k] = consts.tile([P, KNOTS - k], F32, name="span%d" % k)
         nc.vector.tensor_sub(out=span[k][:], in0=knots[:, k:KNOTS], in1=knots[:, 0 : KNOTS - k])
-
-    n_up = LAST_UP + 1
-    up_two = consts.tile([P, n_up], F32)
-    nc.vector.tensor_mul(out=up_two[:], in0=span[1][:, 0:n_up], in1=span[2][:, 0:n_up])
-    up_three = consts.tile([P, n_up], F32)
-    nc.vector.tensor_mul(out=up_three[:], in0=up_two[:], in1=span[3][:, 0:n_up])
-    up_scale = consts.tile([P, n_up], F32)
-    nc.vector.reciprocal(out=up_scale[:], in_=up_three[:])
-
-    n_down = KNOTS - FIRST_DOWN
-    down_two = consts.tile([P, n_down], F32)
-    nc.vector.tensor_mul(out=down_two[:], in0=span[1][:, 2 : 2 + n_down], in1=span[2][:, 1 : 1 + n_down])
-    down_three = consts.tile([P, n_down], F32)
-    nc.vector.tensor_mul(out=down_three[:], in0=down_two[:], in1=span[3][:, 0:n_down])
-    down_scale = consts.tile([P, n_down], F32)
-    nc.vector.reciprocal(out=down_scale[:], in_=down_three[:])
-    neg_down_scale = consts.tile([P, n_down], F32)
-    nc.vector.tensor_scalar_mul(out=neg_down_scale[:], in0=down_scale[:], scalar1=-1.0)
-
     inv_span1 = consts.tile([P, KNOTS - 1], F32)
     nc.vector.reciprocal(out=inv_span1[:], in_=span[1][:])
-    neg_rise_ratio = consts.tile([P, BASES], F32)
+
+    n = BASES + 1
+    up_two = consts.tile([P, n], F32)
+    nc.vector.tensor_mul(out=up_two[:], in0=span[1][:, 0:n], in1=span[2][:, 0:n])
+    inv_up = consts.tile([P, n], F32)
+    nc.vector.tensor_mul(out=inv_up[:], in0=up_two[:], in1=span[3][:, 0:n])
+    up = consts.tile([P, n], F32)
+    nc.vector.reciprocal(out=up[:], in_=inv_up[:])
+    down_two = consts.tile([P, n], F32)
+    nc.vector.tensor_mul(out=down_two[:], in0=span[1][:, 2 : 2 + n], in1=span[2][:, 1 : 1 + n])
+    inv_down = consts.tile([P, n], F32)
+    nc.vector.tensor_mul(out=inv_down[:], in0=down_two[:], in1=span[3][:, 0:n])
+    down = consts.tile([P, n], F32)
+    nc.vector.reciprocal(out=down[:], in_=inv_down[:])
+
+    rise_ratio = consts.tile([P, BASES], F32)
     nc.vector.scalar_tensor_tensor(
-        out=neg_rise_ratio[:], in0=span[4][:], scalar=-1.0, in1=inv_span1[:, 0:BASES],
-        op0=ALU.mult, op1=ALU.mult,
+        out=rise_ratio[:], in0=span[4][:], scalar=-1.0, in1=inv_span1[:, 0:BASES], op0=ALU.mult, op1=ALU.mult
     )
-    neg_fall_ratio = consts.tile([P, BASES], F32)
+    rise_part = consts.tile([P, BASES], F32)
+    nc.vector.tensor_mul(out=rise_part[:], in0=rise_ratio[:], in1=inv_up[:, 0:BASES])
+    rise_tail = consts.tile([P, BASES], F32)
+    nc.vector.tensor_mul(out=rise_tail[:], in0=rise_part[:], in1=up[:, 1 : 1 + BASES])
+    fall_ratio = consts.tile([P, BASES], F32)
     nc.vector.scalar_tensor_tensor(
-        out=neg_fall_ratio[:], in0=span[4][:], scalar=-1.0, in1=inv_span1[:, 3 : 3 + BASES],
-        op0=ALU.mult, op1=ALU.mult,
+        out=fall_ratio[:], in0=span[4][:], scalar=-1.0, in1=inv_span1[:, 3 : 3 + BASES], op0=ALU.mult, op1=ALU.mult
     )
+    fall_part = consts.tile([P, BASES], F32)
+    nc.vector.tensor_mul(out=fall_part[:], in0=fall_ratio[:], in1=inv_down[:, 1 : 1 + BASES])
+    fall_tail = consts.tile([P, BASES], F32)
+    nc.vector.tensor_mul(out=fall_tail[:], in0=fall_part[:], in1=down[:, 0:BASES])
+    fall_scale = consts.tile([P, BASES], F32)
+    nc.vector.tensor_scalar_mul(out=fall_scale[:], in0=down[:, 1 : 1 + BASES], scalar1=-1.0)
     return {
         "knots": knots,
         "neg_knots": neg_knots,
-        "up_scale": up_scale,
-        "neg_down_scale": neg_down_scale,
-        "neg_rise_ratio": neg_rise_ratio,
-        "neg_fall_ratio": neg_fall_ratio,
+        "rise_scale": up,
+        "rise_tail": rise_tail,
+        "fall_scale": fall_scale,
+        "fall_tail": fall_tail,
     }
 
 
-def quantise_128_rows(nc, turn, stage, ident_bf, rows_sb, codes, scales, first_col):
-    cols = slice(first_col, first_col + P)
-    for c in range(BASE_PASSES):
-        turned = turn.tile([P, PACK, P], BF16, tag="turn")
+def features_to_partitions(nc, banks, ident_bf, rows_sb, grouped):
+    for c in range(CHUNKS):
+        turned = banks.tile([P, PACK, P], BF16, tag="for_vector")
         for t in range(PACK):
             first = (c * PACK + t) * P
             nc.tensor.transpose(turned[:, t, :], rows_sb[:, first : first + P], ident_bf[:])
-        grouped = stage.tile([P, P, PACK], BF16, align_bytes=64, tag="rows_grouped")
-        nc.vector.tensor_copy(out=grouped[:], in_=turned[:].rearrange("p t r -> p r t"))
-        nc.vector.quantize_mx(
-            out=codes[:, c, cols].bitcast(FP8X4),
-            scales=scales[:, c, cols],
-            in_=grouped[:].rearrange("p r t -> p (r t)"),
+        nc.vector.tensor_copy(out=grouped[:, c, :, :], in_=turned[:].rearrange("p t r -> p r t"))
+
+
+def sum_to_partitions(nc, bank, ident_f32, lead, tail, first_col):
+    for t in range(PACK):
+        cols = slice(first_col + t * P, first_col + (t + 1) * P)
+        nc.tensor.matmul(
+            out=bank[:, t, :], lhsT=lead[:, cols], rhs=ident_f32[:], is_transpose=True, start=True, stop=False
+        )
+        nc.tensor.matmul(
+            out=bank[:, t, :], lhsT=tail[:, cols], rhs=ident_f32[:], is_transpose=True, start=False, stop=True
         )
 
 
@@ -110,13 +115,8 @@ def tile_kanblock_pb_kernel(tc, h, grid, w2_base, w2_spline, out):
     with ExitStack() as ctx:
         consts = ctx.enter_context(tc.tile_pool(name="consts", bufs=1))
         keep = ctx.enter_context(tc.tile_pool(name="keep", bufs=1))
-        rows = ctx.enter_context(tc.tile_pool(name="rows", bufs=2))
-        stage = ctx.enter_context(tc.tile_pool(name="stage", bufs=2))
-        work = ctx.enter_context(tc.tile_pool(name="work", bufs=2))
-        cubes = ctx.enter_context(tc.tile_pool(name="cubes", bufs=3))
-        operands = ctx.enter_context(tc.tile_pool(name="operands", bufs=2))
-        sums = ctx.enter_context(tc.psum_pool(name="sums", bufs=1))
-        turn = ctx.enter_context(tc.psum_pool(name="turn", bufs=4))
+        sums = ctx.enter_context(tc.psum_pool(name="sums", bufs=2))
+        banks = ctx.enter_context(tc.psum_pool(name="banks", bufs=3))
 
         ident_bf = consts.tile([P, P], BF16)
         masks.make_identity(nc, ident_bf[:])
@@ -124,163 +124,157 @@ def tile_kanblock_pb_kernel(tc, h, grid, w2_base, w2_spline, out):
         masks.make_identity(nc, ident_f32[:])
         k = knot_constants(nc, consts, grid)
 
-        acc = [sums.tile([P, OUTPUTS], F32, name="acc%d" % tt) for tt in range(TOKEN_TILES)]
+        base_codes = keep.tile([P, CHUNKS, OUTPUTS], U32, align_bytes=64)
+        base_scales = keep.tile([P, CHUNKS, OUTPUTS], U8, align_bytes=64)
+        w_codes = keep.tile([P, CHUNKS, BASES, OUTPUTS], U32, align_bytes=64)
+        w_scales = keep.tile([P, CHUNKS, BASES, OUTPUTS], U8, align_bytes=64)
+        h_all = keep.tile([P, TOKEN_TILES, FEATURES], BF16)
+        nc.gpsimd.dma_start(out=h_all[:], in_=h.rearrange("(tt p) i -> p tt i", p=P))
 
-        x_all = keep.tile([P, FEATURE_TILES, TOKENS], BF16)
-        silu_codes = keep.tile([P, BASE_PASSES, TOKENS], U32, align_bytes=64)
-        silu_scales = keep.tile([P, BASE_PASSES, TOKENS], U8, align_bytes=64)
-        base_codes = keep.tile([P, BASE_PASSES, OUTPUTS], U32, align_bytes=64)
-        base_scales = keep.tile([P, BASE_PASSES, OUTPUTS], U8, align_bytes=64)
+        with ExitStack() as weights:
+            w_rows = weights.enter_context(tc.tile_pool(name="w_rows", bufs=2))
+            w_stage = weights.enter_context(tc.tile_pool(name="w_stage", bufs=2))
+
+            base_grouped = w_stage.tile([P, CHUNKS, OUTPUTS, PACK], BF16, align_bytes=64, bufs=1)
+            for dt in range(OUTPUT_TILES):
+                base_sb = w_rows.tile([P, FEATURES], BF16)
+                nc.sync.dma_start(out=base_sb[:], in_=w2_base[dt * P : (dt + 1) * P, :])
+                features_to_partitions(nc, banks, ident_bf, base_sb, base_grouped[:, :, dt * P : (dt + 1) * P, :])
+            for c in range(CHUNKS):
+                nc.vector.quantize_mx(
+                    out=base_codes[:, c, :].bitcast(FP8X4),
+                    scales=base_scales[:, c, :],
+                    in_=base_grouped[:, c, :, :].rearrange("p d t -> p (d t)"),
+                )
+
+            emptied = 0
+            for c in range(CHUNKS):
+                row_len = K_PASS * BASES
+                w_sb = w_rows.tile([P, OUTPUT_TILES, row_len], BF16)
+                for dt in range(OUTPUT_TILES):
+                    nc.sync.dma_start(out=w_sb[:, dt, :], in_=spline_rows[:, dt, c * row_len : (c + 1) * row_len])
+                w_words = w_sb[:].bitcast(F32).rearrange("p dt (t i q) -> p dt t i q", t=PACK, q=PAIRS)
+                for q in range(PAIRS):
+                    w_grouped = w_stage.tile([P, 2, OUTPUTS, PACK], BF16, align_bytes=64)
+                    for dt in range(OUTPUT_TILES):
+                        by_scalar = emptied % 8 < 5
+                        emptied += 1
+                        turned = banks.tile([P, PACK, P], F32, tag="for_scalar" if by_scalar else "for_vector")
+                        for t in range(PACK):
+                            nc.tensor.transpose(turned[:, t, :], w_words[:, dt, t, :, q], ident_f32[:])
+                        halves = turned[:].bitcast(BF16).rearrange("p t (d e) -> p e d t", e=2)
+                        if by_scalar:
+                            nc.scalar.copy(out=w_grouped[:, :, dt * P : (dt + 1) * P, :], in_=halves)
+                        else:
+                            nc.vector.tensor_copy(out=w_grouped[:, :, dt * P : (dt + 1) * P, :], in_=halves)
+                    for e in range(2):
+                        nc.vector.quantize_mx(
+                            out=w_codes[:, c, 2 * q + e, :].bitcast(FP8X4),
+                            scales=w_scales[:, c, 2 * q + e, :],
+                            in_=w_grouped[:, e, :, :].rearrange("p d t -> p (d t)"),
+                        )
+
+        rows = ctx.enter_context(tc.tile_pool(name="rows", bufs=2))
+        work = ctx.enter_context(tc.tile_pool(name="work", bufs=3))
+        operands = ctx.enter_context(tc.tile_pool(name="operands", bufs=3))
 
         for tt in range(TOKEN_TILES):
-            h_sb = rows.tile([P, FEATURES], BF16)
-            nc.sync.dma_start(out=h_sb[:], in_=h[tt * P : (tt + 1) * P, :])
-            for q in range(FEATURE_TILES // PACK):
-                turned = turn.tile([P, PACK, P], BF16, tag="turn")
-                for t in range(PACK):
-                    first = (q * PACK + t) * P
-                    nc.tensor.transpose(turned[:, t, :], h_sb[:, first : first + P], ident_bf[:])
-                nc.vector.tensor_scalar(
-                    out=x_all[:, q * PACK : (q + 1) * PACK, tt * P : (tt + 1) * P],
-                    in0=turned[:],
-                    scalar1=k["knots"][:, 0:1],
-                    scalar2=k["knots"][:, KNOTS - 1 : KNOTS],
-                    op0=ALU.max,
-                    op1=ALU.min,
-                )
+            h_sb = h_all[:, tt, :]
+            x = rows.tile([P, FEATURES], BF16)
+            nc.vector.tensor_scalar(
+                out=x[:], in0=h_sb, scalar1=k["knots"][:, 0:1], scalar2=k["knots"][:, KNOTS - 1 : KNOTS],
+                op0=ALU.max, op1=ALU.min,
+            )
             silu_sb = rows.tile([P, FEATURES], BF16)
-            nc.scalar.activation(out=silu_sb[:], in_=h_sb[:], func=ACT.Silu)
-            quantise_128_rows(nc, turn, stage, ident_bf, silu_sb, silu_codes, silu_scales, tt * P)
-
-        for dt in range(OUTPUT_TILES):
-            base_sb = rows.tile([P, FEATURES], BF16)
-            nc.sync.dma_start(out=base_sb[:], in_=w2_base[dt * P : (dt + 1) * P, :])
-            quantise_128_rows(nc, turn, stage, ident_bf, base_sb, base_codes, base_scales, dt * P)
-
-        for c in range(BASE_PASSES):
-            for tt in range(TOKEN_TILES):
-                token_cols = slice(tt * P, (tt + 1) * P)
+            nc.scalar.activation(out=silu_sb[:], in_=h_sb, func=ACT.Silu)
+            silu_grouped = rows.tile([P, CHUNKS, P, PACK], BF16, align_bytes=64)
+            features_to_partitions(nc, banks, ident_bf, silu_sb, silu_grouped[:])
+            silu_codes = operands.tile([P, CHUNKS, P], U32, align_bytes=64)
+            silu_scales = operands.tile([P, CHUNKS, P], U8, align_bytes=64)
+            nc.vector.quantize_mx(
+                out=silu_codes[:].rearrange("p c n -> p (c n)").bitcast(FP8X4),
+                scales=silu_scales[:].rearrange("p c n -> p (c n)"),
+                in_=silu_grouped[:].rearrange("p c n t -> p (c n t)"),
+            )
+            acc = sums.tile([P, OUTPUTS], F32)
+            for c in range(CHUNKS):
                 nc.tensor.matmul_mx(
-                    out=acc[tt][:],
-                    lhsT=silu_codes[:, c, token_cols].bitcast(FP8X4),
-                    lhsT_scale=silu_scales[:, c, token_cols],
+                    out=acc[:],
+                    lhsT=silu_codes[:, c, :].bitcast(FP8X4),
+                    lhsT_scale=silu_scales[:, c, :],
                     rhs=base_codes[:, c, :].bitcast(FP8X4),
                     rhs_scale=base_scales[:, c, :],
                     start=(c == 0),
                     stop=False,
                 )
 
-        for b in range(BATCHES):
-            row_len = TILES_PER_BATCH * P * BASES
-            w_sb = rows.tile([P, OUTPUT_TILES, row_len], BF16)
-            nc.sync.dma_start(out=w_sb[:], in_=spline_rows[:, :, b * row_len : (b + 1) * row_len])
-            w_words = w_sb[:].bitcast(F32).rearrange(
-                "p dt (f i q) -> p dt f i q", f=TILES_PER_BATCH, q=WORDS_PER_FEATURE
-            )
-            w_codes = {}
-            w_scales = {}
-            for f in range(TILES_PER_BATCH):
-                for a in range(BASIS_GROUPS):
-                    w_grouped = stage.tile([P, OUTPUTS, 2], F32, align_bytes=64)
-                    for half in range(2):
-                        turned = turn.tile([P, 2, 2 * P], F32, tag="turn")
-                        for u in range(2):
-                            for s in range(2):
-                                nc.tensor.transpose(
-                                    turned[:, u, s * P : (s + 1) * P],
-                                    w_words[:, 2 * half + s, f, :, 2 * a + u],
-                                    ident_f32[:],
-                                )
-                        nc.scalar.copy(
-                            out=w_grouped[:, half * 2 * P : (half + 1) * 2 * P, :],
-                            in_=turned[:].rearrange("p u d -> p d u"),
-                        )
-                    w_codes[f, a] = operands.tile(
-                        [P, OUTPUTS], U32, align_bytes=64, name="w_codes", tag="w_codes", bufs=6
-                    )
-                    w_scales[f, a] = operands.tile(
-                        [P, OUTPUTS], U8, align_bytes=64, name="w_scales", tag="w_scales", bufs=6
-                    )
-                    nc.vector.quantize_mx(
-                        out=w_codes[f, a][:].bitcast(FP8X4),
-                        scales=w_scales[f, a][:],
-                        in_=w_grouped[:].rearrange("p d u -> p (d u)").bitcast(BF16),
-                    )
-
-            x = x_all[:, b * TILES_PER_BATCH : (b + 1) * TILES_PER_BATCH, :].rearrange("p f n -> p (f n)")
-            up = {}
-            down = {}
-            rise = {}
-            fall = {}
-            for a in range(BASIS_GROUPS):
-                rise[a] = work.tile([P, PACK, BATCH_COLS], BF16, name="rise", tag="rise")
-                fall[a] = work.tile([P, PACK, BATCH_COLS], BF16, name="fall", tag="fall")
-            for j in range(KNOTS):
-                square = work.tile([P, BATCH_COLS], F32)
-                nc.scalar.activation(
-                    out=square[:], in_=x, func=ACT.Square, bias=k["neg_knots"][:, j : j + 1], scale=1.0
-                )
-                cube = work.tile([P, BATCH_COLS], F32)
-                nc.vector.scalar_tensor_tensor(
-                    out=cube[:], in0=x, scalar=k["knots"][:, j : j + 1], in1=square[:],
-                    op0=ALU.subtract, op1=ALU.mult,
-                )
-                if j <= LAST_UP:
-                    up[j] = cubes.tile([P, BATCH_COLS], F32, name="up", tag="up")
+            for b in range(BATCHES):
+                xb = x[:, b * BATCH_COLS : (b + 1) * BATCH_COLS]
+                cube = {}
+                rise_tails = {}
+                fall_tails = {}
+                risen = {}
+                for j in range(KNOTS):
+                    square = work.tile([P, BATCH_COLS], F32)
                     nc.scalar.activation(
-                        out=up[j][:], in_=cube[:], func=ACT.Relu, scale=k["up_scale"][:, j : j + 1]
+                        out=square[:], in_=xb, func=ACT.Square, bias=k["neg_knots"][:, j : j + 1], scale=1.0
                     )
-                if j >= FIRST_DOWN:
-                    down[j] = cubes.tile([P, BATCH_COLS], F32, name="down", tag="down")
-                    nc.scalar.activation(
-                        out=down[j][:], in_=cube[:], func=ACT.Relu,
-                        scale=k["neg_down_scale"][:, j - FIRST_DOWN : j - FIRST_DOWN + 1],
-                    )
-                if 1 <= j <= LAST_UP:
-                    g = j - 1
+                    cube[j] = work.tile([P, BATCH_COLS], F32, name="cube", tag="cube", bufs=4)
                     nc.vector.scalar_tensor_tensor(
-                        out=rise[g // PACK][:, g % PACK, :], in0=up[g + 1][:],
-                        scalar=k["neg_rise_ratio"][:, g : g + 1], in1=up[g][:],
-                        op0=ALU.mult, op1=ALU.add,
+                        out=cube[j][:], in0=xb, scalar=k["knots"][:, j : j + 1], in1=square[:],
+                        op0=ALU.subtract, op1=ALU.mult,
                     )
-                if j >= FIRST_DOWN + 1:
-                    g = j - 4
-                    nc.vector.scalar_tensor_tensor(
-                        out=fall[g // PACK][:, g % PACK, :], in0=down[g + 3][:],
-                        scalar=k["neg_fall_ratio"][:, g : g + 1], in1=down[g + 4][:],
-                        op0=ALU.mult, op1=ALU.add,
-                    )
-                    if g % PACK == PACK - 1:
-                        a = g // PACK
-                        bases = stage.tile([P, BATCH_COLS, PACK], BF16, align_bytes=64)
-                        nc.vector.tensor_tensor(
-                            out=bases[:],
-                            in0=rise[a][:].rearrange("p r n -> p n r"),
-                            in1=fall[a][:].rearrange("p r n -> p n r"),
-                            op=ALU.max,
+                    if 1 <= j <= BASES:
+                        g = j - 1
+                        rise_tails[g] = work.tile([P, BATCH_COLS], F32, name="rise_tail", tag="rise_tail")
+                        nc.vector.tensor_scalar(
+                            out=rise_tails[g][:], in0=cube[j][:], scalar1=k["rise_tail"][:, g : g + 1], scalar2=0.0,
+                            op0=ALU.mult, op1=ALU.min,
                         )
-                        b_codes = operands.tile([P, BATCH_COLS], U32, align_bytes=64)
-                        b_scales = operands.tile([P, BATCH_COLS], U8, align_bytes=64)
+                        risen[g] = work.tile([P, CHUNKS_PER_BATCH, P, PACK], BF16, name="risen", tag="risen", bufs=6)
+                        for cc in range(CHUNKS_PER_BATCH):
+                            bank = banks.tile([P, PACK, P], F32, tag="for_scalar")
+                            sum_to_partitions(nc, bank, ident_f32, cube[g], rise_tails[g], cc * K_PASS)
+                            nc.scalar.activation(
+                                out=risen[g][:, cc, :, :], in_=bank[:].rearrange("p t n -> p n t"), func=ACT.Relu,
+                                scale=k["rise_scale"][:, g : g + 1],
+                            )
+                    if 3 <= j <= BASES + 2:
+                        g = j - 3
+                        fall_tails[g] = work.tile([P, BATCH_COLS], F32, name="fall_tail", tag="fall_tail")
+                        nc.scalar.activation(
+                            out=fall_tails[g][:], in_=cube[j][:], func=ACT.Relu, scale=k["fall_tail"][:, g : g + 1]
+                        )
+                    if j >= 4:
+                        g = j - 4
+                        bases = operands.tile([P, CHUNKS_PER_BATCH, P, PACK], BF16, align_bytes=64)
+                        for cc in range(CHUNKS_PER_BATCH):
+                            bank = banks.tile([P, PACK, P], F32, tag="for_vector")
+                            sum_to_partitions(nc, bank, ident_f32, cube[j], fall_tails[g], cc * K_PASS)
+                            nc.vector.scalar_tensor_tensor(
+                                out=bases[:, cc, :, :], in0=bank[:].rearrange("p t n -> p n t"),
+                                scalar=k["fall_scale"][:, g : g + 1], in1=risen[g][:, cc, :, :],
+                                op0=ALU.mult, op1=ALU.max,
+                            )
+                        b_codes = operands.tile([P, CHUNKS_PER_BATCH, P], U32, align_bytes=64)
+                        b_scales = operands.tile([P, CHUNKS_PER_BATCH, P], U8, align_bytes=64)
                         nc.vector.quantize_mx(
-                            out=b_codes[:].bitcast(FP8X4),
-                            scales=b_scales[:],
-                            in_=bases[:].rearrange("p n r -> p (n r)"),
+                            out=b_codes[:].rearrange("p c n -> p (c n)").bitcast(FP8X4),
+                            scales=b_scales[:].rearrange("p c n -> p (c n)"),
+                            in_=bases[:].rearrange("p c n t -> p (c n t)"),
                         )
-                        for f in range(TILES_PER_BATCH):
-                            last = b == BATCHES - 1 and a == BASIS_GROUPS - 1 and f == TILES_PER_BATCH - 1
-                            for tt in range(TOKEN_TILES):
-                                token_cols = slice(f * TOKENS + tt * P, f * TOKENS + (tt + 1) * P)
-                                nc.tensor.matmul_mx(
-                                    out=acc[tt][:],
-                                    lhsT=b_codes[:, token_cols].bitcast(FP8X4),
-                                    lhsT_scale=b_scales[:, token_cols],
-                                    rhs=w_codes[f, a][:].bitcast(FP8X4),
-                                    rhs_scale=w_scales[f, a][:],
-                                    start=False,
-                                    stop=last,
-                                )
+                        for cc in range(CHUNKS_PER_BATCH):
+                            c = b * CHUNKS_PER_BATCH + cc
+                            nc.tensor.matmul_mx(
+                                out=acc[:],
+                                lhsT=b_codes[:, cc, :].bitcast(FP8X4),
+                                lhsT_scale=b_scales[:, cc, :],
+                                rhs=w_codes[:, c, g, :].bitcast(FP8X4),
+                                rhs_scale=w_scales[:, c, g, :],
+                                start=False,
+                                stop=(c == CHUNKS - 1 and g == BASES - 1),
+                            )
 
-        for tt in range(TOKEN_TILES):
-            result = stage.tile([P, OUTPUTS], F32)
-            nc.scalar.copy(out=result[:], in_=acc[tt][:])
+            result = rows.tile([P, OUTPUTS], F32)
+            nc.scalar.copy(out=result[:], in_=acc[:])
             nc.sync.dma_start(out=out_rows[tt * P : (tt + 1) * P, :], in_=result[:])

@@ -26,6 +26,11 @@ PAIRS = BASES // 2
 CHUNKS_PER_BATCH = 2
 BATCHES = CHUNKS // CHUNKS_PER_BATCH
 BATCH_COLS = CHUNKS_PER_BATCH * K_PASS
+BATCH_COUNT = TOKEN_TILES * BATCHES
+STRIDE = BASES
+FIRST_SLOT = -4
+TILE_SLOTS = STRIDE * (BATCHES - 1) + KNOTS + 2
+LAST_SLOT = STRIDE * BATCHES * (TOKEN_TILES - 1) + TILE_SLOTS
 
 FLOPS = 2 * TOKENS * OUTPUTS * (FEATURES + FEATURES * BASES)
 
@@ -96,14 +101,17 @@ def features_to_partitions(nc, banks, ident_bf, rows_sb, grouped):
         nc.vector.tensor_copy(out=grouped[:, c, :, :], in_=turned[:].rearrange("p t r -> p r t"))
 
 
-def sum_to_partitions(nc, bank, ident_f32, lead, tail, first_col):
+def sum_to_partitions(nc, bank, ident_f32, lead, tail, first_col, plain_quarters):
     for t in range(PACK):
         cols = slice(first_col + t * P, first_col + (t + 1) * P)
+        passes_through = t >= plain_quarters
         nc.tensor.matmul(
-            out=bank[:, t, :], lhsT=lead[:, cols], rhs=ident_f32[:], is_transpose=True, start=True, stop=False
+            out=bank[:, t, :], lhsT=lead[:, cols], rhs=ident_f32[:], is_transpose=passes_through,
+            start=True, stop=False,
         )
         nc.tensor.matmul(
-            out=bank[:, t, :], lhsT=tail[:, cols], rhs=ident_f32[:], is_transpose=True, start=False, stop=True
+            out=bank[:, t, :], lhsT=tail[:, cols], rhs=ident_f32[:], is_transpose=passes_through,
+            start=False, stop=True,
         )
 
 
@@ -174,107 +182,198 @@ def tile_kanblock_pb_kernel(tc, h, grid, w2_base, w2_spline, out):
                             in_=w_grouped[:, e, :, :].rearrange("p d t -> p (d t)"),
                         )
 
-        rows = ctx.enter_context(tc.tile_pool(name="rows", bufs=2))
+        rows = ctx.enter_context(tc.tile_pool(name="rows", bufs=1))
         work = ctx.enter_context(tc.tile_pool(name="work", bufs=3))
         operands = ctx.enter_context(tc.tile_pool(name="operands", bufs=3))
 
-        for tt in range(TOKEN_TILES):
-            h_sb = h_all[:, tt, :]
-            x = rows.tile([P, FEATURES], BF16)
+        x = {}
+        silu_sb = {}
+        silu_grouped = {}
+        silu_codes = {}
+        silu_scales = {}
+        acc = {}
+        square = {}
+        cube = {}
+        rise_tail = {}
+        fall_tail = {}
+        rise_bank = {}
+        fall_bank = {}
+        risen = {}
+        bases = {}
+        b_codes = {}
+        b_scales = {}
+
+        def activate(tt):
+            x[tt] = rows.tile([P, FEATURES], BF16, name="x", tag="x", bufs=2)
             nc.vector.tensor_scalar(
-                out=x[:], in0=h_sb, scalar1=k["knots"][:, 0:1], scalar2=k["knots"][:, KNOTS - 1 : KNOTS],
-                op0=ALU.max, op1=ALU.min,
+                out=x[tt][:], in0=h_all[:, tt, :], scalar1=k["knots"][:, 0:1],
+                scalar2=k["knots"][:, KNOTS - 1 : KNOTS], op0=ALU.max, op1=ALU.min,
             )
-            silu_sb = rows.tile([P, FEATURES], BF16)
-            nc.scalar.activation(out=silu_sb[:], in_=h_sb, func=ACT.Silu)
-            silu_grouped = rows.tile([P, CHUNKS, P, PACK], BF16, align_bytes=64)
-            features_to_partitions(nc, banks, ident_bf, silu_sb, silu_grouped[:])
-            silu_codes = operands.tile([P, CHUNKS, P], U32, align_bytes=64)
-            silu_scales = operands.tile([P, CHUNKS, P], U8, align_bytes=64)
+            silu_sb[tt] = rows.tile([P, FEATURES], BF16, name="silu_sb", tag="silu_sb")
+            nc.scalar.activation(out=silu_sb[tt][:], in_=h_all[:, tt, :], func=ACT.Silu)
+
+        def quantise_silu(tt):
+            silu_grouped[tt] = rows.tile([P, CHUNKS, P, PACK], BF16, align_bytes=64, name="silu_grouped", tag="silu_grouped")
+            features_to_partitions(nc, banks, ident_bf, silu_sb[tt], silu_grouped[tt][:])
+            silu_codes[tt] = operands.tile([P, CHUNKS, P], U32, align_bytes=64, name="silu_codes", tag="silu_codes", bufs=2)
+            silu_scales[tt] = operands.tile([P, CHUNKS, P], U8, align_bytes=64, name="silu_scales", tag="silu_scales", bufs=2)
             nc.vector.quantize_mx(
-                out=silu_codes[:].rearrange("p c n -> p (c n)").bitcast(FP8X4),
-                scales=silu_scales[:].rearrange("p c n -> p (c n)"),
-                in_=silu_grouped[:].rearrange("p c n t -> p (c n t)"),
+                out=silu_codes[tt][:].rearrange("p c n -> p (c n)").bitcast(FP8X4),
+                scales=silu_scales[tt][:].rearrange("p c n -> p (c n)"),
+                in_=silu_grouped[tt][:].rearrange("p c n t -> p (c n t)"),
             )
-            acc = sums.tile([P, OUTPUTS], F32)
+
+        def base_product(tt):
+            acc[tt] = sums.tile([P, OUTPUTS], F32, name="acc", tag="acc")
             for c in range(CHUNKS):
                 nc.tensor.matmul_mx(
-                    out=acc[:],
-                    lhsT=silu_codes[:, c, :].bitcast(FP8X4),
-                    lhsT_scale=silu_scales[:, c, :],
+                    out=acc[tt][:],
+                    lhsT=silu_codes[tt][:, c, :].bitcast(FP8X4),
+                    lhsT_scale=silu_scales[tt][:, c, :],
                     rhs=base_codes[:, c, :].bitcast(FP8X4),
                     rhs_scale=base_scales[:, c, :],
                     start=(c == 0),
                     stop=False,
                 )
 
-            for b in range(BATCHES):
-                xb = x[:, b * BATCH_COLS : (b + 1) * BATCH_COLS]
-                cube = {}
-                rise_tails = {}
-                fall_tails = {}
-                risen = {}
-                for j in range(KNOTS):
-                    square = work.tile([P, BATCH_COLS], F32)
-                    nc.scalar.activation(
-                        out=square[:], in_=xb, func=ACT.Square, bias=k["neg_knots"][:, j : j + 1], scale=1.0
-                    )
-                    cube[j] = work.tile([P, BATCH_COLS], F32, name="cube", tag="cube", bufs=4)
-                    nc.vector.scalar_tensor_tensor(
-                        out=cube[j][:], in0=xb, scalar=k["knots"][:, j : j + 1], in1=square[:],
-                        op0=ALU.subtract, op1=ALU.mult,
-                    )
-                    if 1 <= j <= BASES:
-                        g = j - 1
-                        rise_tails[g] = work.tile([P, BATCH_COLS], F32, name="rise_tail", tag="rise_tail")
-                        nc.vector.tensor_scalar(
-                            out=rise_tails[g][:], in0=cube[j][:], scalar1=k["rise_tail"][:, g : g + 1], scalar2=0.0,
-                            op0=ALU.mult, op1=ALU.min,
-                        )
-                        risen[g] = work.tile([P, CHUNKS_PER_BATCH, P, PACK], BF16, name="risen", tag="risen", bufs=6)
-                        for cc in range(CHUNKS_PER_BATCH):
-                            bank = banks.tile([P, PACK, P], F32, tag="for_scalar")
-                            sum_to_partitions(nc, bank, ident_f32, cube[g], rise_tails[g], cc * K_PASS)
-                            nc.scalar.activation(
-                                out=risen[g][:, cc, :, :], in_=bank[:].rearrange("p t n -> p n t"), func=ACT.Relu,
-                                scale=k["rise_scale"][:, g : g + 1],
-                            )
-                    if 3 <= j <= BASES + 2:
-                        g = j - 3
-                        fall_tails[g] = work.tile([P, BATCH_COLS], F32, name="fall_tail", tag="fall_tail")
-                        nc.scalar.activation(
-                            out=fall_tails[g][:], in_=cube[j][:], func=ACT.Relu, scale=k["fall_tail"][:, g : g + 1]
-                        )
-                    if j >= 4:
-                        g = j - 4
-                        bases = operands.tile([P, CHUNKS_PER_BATCH, P, PACK], BF16, align_bytes=64)
-                        for cc in range(CHUNKS_PER_BATCH):
-                            bank = banks.tile([P, PACK, P], F32, tag="for_vector")
-                            sum_to_partitions(nc, bank, ident_f32, cube[j], fall_tails[g], cc * K_PASS)
-                            nc.vector.scalar_tensor_tensor(
-                                out=bases[:, cc, :, :], in0=bank[:].rearrange("p t n -> p n t"),
-                                scalar=k["fall_scale"][:, g : g + 1], in1=risen[g][:, cc, :, :],
-                                op0=ALU.mult, op1=ALU.max,
-                            )
-                        b_codes = operands.tile([P, CHUNKS_PER_BATCH, P], U32, align_bytes=64)
-                        b_scales = operands.tile([P, CHUNKS_PER_BATCH, P], U8, align_bytes=64)
-                        nc.vector.quantize_mx(
-                            out=b_codes[:].rearrange("p c n -> p (c n)").bitcast(FP8X4),
-                            scales=b_scales[:].rearrange("p c n -> p (c n)"),
-                            in_=bases[:].rearrange("p c n t -> p (c n t)"),
-                        )
-                        for cc in range(CHUNKS_PER_BATCH):
-                            c = b * CHUNKS_PER_BATCH + cc
-                            nc.tensor.matmul_mx(
-                                out=acc[:],
-                                lhsT=b_codes[:, cc, :].bitcast(FP8X4),
-                                lhsT_scale=b_scales[:, cc, :],
-                                rhs=w_codes[:, c, g, :].bitcast(FP8X4),
-                                rhs_scale=w_scales[:, c, g, :],
-                                start=False,
-                                stop=(c == CHUNKS - 1 and g == BASES - 1),
-                            )
-
-            result = rows.tile([P, OUTPUTS], F32)
-            nc.scalar.copy(out=result[:], in_=acc[:])
+        def store(tt):
+            result = rows.tile([P, OUTPUTS], F32, name="result", tag="result", bufs=2)
+            nc.scalar.copy(out=result[:], in_=acc[tt][:])
             nc.sync.dma_start(out=out_rows[tt * P : (tt + 1) * P, :], in_=result[:])
+
+        def batch_x(n):
+            first = (n % BATCHES) * BATCH_COLS
+            return x[n // BATCHES][:, first : first + BATCH_COLS]
+
+        def make_square(n, j):
+            if 0 <= j < KNOTS:
+                square[n, j] = work.tile([P, BATCH_COLS], F32, name="square", tag="square", bufs=4)
+                nc.scalar.activation(
+                    out=square[n, j][:], in_=batch_x(n), func=ACT.Square, bias=k["neg_knots"][:, j : j + 1], scale=1.0
+                )
+
+        def make_cube(n, j):
+            if 0 <= j < KNOTS:
+                cube[n, j] = work.tile([P, BATCH_COLS], F32, name="cube", tag="cube", bufs=6)
+                nc.vector.scalar_tensor_tensor(
+                    out=cube[n, j][:], in0=batch_x(n), scalar=k["knots"][:, j : j + 1], in1=square[n, j][:],
+                    op0=ALU.subtract, op1=ALU.mult,
+                )
+
+        def make_rise_tail(n, j):
+            g = j - 1
+            if 0 <= g < BASES:
+                rise_tail[n, g] = work.tile([P, BATCH_COLS], F32, name="rise_tail", tag="rise_tail")
+                nc.vector.tensor_scalar(
+                    out=rise_tail[n, g][:], in0=cube[n, j][:], scalar1=k["rise_tail"][:, g : g + 1], scalar2=0.0,
+                    op0=ALU.mult, op1=ALU.min,
+                )
+
+        def make_fall_tail(n, j):
+            g = j - 3
+            if 0 <= g < BASES:
+                fall_tail[n, g] = work.tile([P, BATCH_COLS], F32, name="fall_tail", tag="fall_tail")
+                nc.scalar.activation(
+                    out=fall_tail[n, g][:], in_=cube[n, j][:], func=ACT.Relu, scale=k["fall_tail"][:, g : g + 1]
+                )
+
+        def sum_rise(n, j):
+            g = j - 1
+            if 0 <= g < BASES:
+                for cc in range(CHUNKS_PER_BATCH):
+                    rise_bank[n, g, cc] = banks.tile([P, PACK, P], F32, name="rise_bank", tag="for_scalar")
+                    sum_to_partitions(nc, rise_bank[n, g, cc], ident_f32, cube[n, g], rise_tail[n, g], cc * K_PASS, 0)
+
+        def round_rise(n, j):
+            g = j - 1
+            if 0 <= g < BASES:
+                risen[n, g] = work.tile([P, CHUNKS_PER_BATCH, P, PACK], BF16, name="risen", tag="risen", bufs=6)
+                for cc in range(CHUNKS_PER_BATCH):
+                    nc.scalar.activation(
+                        out=risen[n, g][:, cc, :, :], in_=rise_bank[n, g, cc][:].rearrange("p t n -> p n t"),
+                        func=ACT.Relu, scale=k["rise_scale"][:, g : g + 1],
+                    )
+
+        def sum_fall(n, j):
+            g = j - 4
+            if 0 <= g < BASES:
+                for cc in range(CHUNKS_PER_BATCH):
+                    fall_bank[n, g, cc] = banks.tile([P, PACK, P], F32, name="fall_bank", tag="for_vector")
+                    sum_to_partitions(
+                        nc, fall_bank[n, g, cc], ident_f32, cube[n, j], fall_tail[n, g], cc * K_PASS, 1 if cc == 0 else 0
+                    )
+
+        def finish_bases(n, j):
+            g = j - 4
+            if 0 <= g < BASES:
+                bases[n, g] = operands.tile([P, CHUNKS_PER_BATCH, P, PACK], BF16, align_bytes=64, name="bases", tag="bases", bufs=2)
+                for cc in range(CHUNKS_PER_BATCH):
+                    nc.vector.scalar_tensor_tensor(
+                        out=bases[n, g][:, cc, :, :], in0=fall_bank[n, g, cc][:].rearrange("p t n -> p n t"),
+                        scalar=k["fall_scale"][:, g : g + 1], in1=risen[n, g][:, cc, :, :],
+                        op0=ALU.mult, op1=ALU.max,
+                    )
+
+        def quantise_bases(n, j):
+            g = j - 4
+            if 0 <= g < BASES:
+                b_codes[n, g] = operands.tile([P, CHUNKS_PER_BATCH, P], U32, align_bytes=64, name="b_codes", tag="b_codes")
+                b_scales[n, g] = operands.tile([P, CHUNKS_PER_BATCH, P], U8, align_bytes=64, name="b_scales", tag="b_scales")
+                nc.vector.quantize_mx(
+                    out=b_codes[n, g][:].rearrange("p c n -> p (c n)").bitcast(FP8X4),
+                    scales=b_scales[n, g][:].rearrange("p c n -> p (c n)"),
+                    in_=bases[n, g][:].rearrange("p c n t -> p (c n t)"),
+                )
+
+        def multiply(n, j, cc):
+            g = j - 4
+            if 0 <= g < BASES:
+                c = (n % BATCHES) * CHUNKS_PER_BATCH + cc
+                nc.tensor.matmul_mx(
+                    out=acc[n // BATCHES][:],
+                    lhsT=b_codes[n, g][:, cc, :].bitcast(FP8X4),
+                    lhsT_scale=b_scales[n, g][:, cc, :],
+                    rhs=w_codes[:, c, g, :].bitcast(FP8X4),
+                    rhs_scale=w_scales[:, c, g, :],
+                    start=False,
+                    stop=(c == CHUNKS - 1 and g == BASES - 1),
+                )
+
+        with tc.manual_schedule():
+            for slot in range(FIRST_SLOT, LAST_SLOT + 1):
+                every_batch = range(BATCH_COUNT)
+                knot = [slot - STRIDE * n for n in every_batch]
+                for tt in range(TOKEN_TILES):
+                    since_start = slot - STRIDE * BATCHES * tt
+                    if since_start == -4:
+                        activate(tt)
+                    if since_start == -2:
+                        base_product(tt)
+                for n in every_batch:
+                    make_square(n, knot[n] + 1)
+                for n in every_batch:
+                    make_cube(n, knot[n])
+                for n in every_batch:
+                    sum_rise(n, knot[n] - 1)
+                for n in every_batch:
+                    multiply(n, knot[n] - 2, 0)
+                for n in every_batch:
+                    round_rise(n, knot[n] - 1)
+                for n in every_batch:
+                    finish_bases(n, knot[n] - 1)
+                for tt in range(TOKEN_TILES):
+                    if slot - STRIDE * BATCHES * tt == -3:
+                        quantise_silu(tt)
+                for n in every_batch:
+                    make_rise_tail(n, knot[n])
+                for n in every_batch:
+                    make_fall_tail(n, knot[n])
+                for n in every_batch:
+                    quantise_bases(n, knot[n] - 1)
+                for n in every_batch:
+                    sum_fall(n, knot[n])
+                for n in every_batch:
+                    multiply(n, knot[n] - 2, 1)
+                for tt in range(TOKEN_TILES):
+                    if slot - STRIDE * BATCHES * tt == TILE_SLOTS:
+                        store(tt)

@@ -165,7 +165,7 @@ def tile_kanblock_pb_kernel(tc, h, grid, w2_base, w2_spline, out):
                 for q in range(PAIRS):
                     w_grouped = w_stage.tile([P, 2, OUTPUTS, PACK], BF16, align_bytes=64)
                     for dt in range(OUTPUT_TILES):
-                        by_scalar = emptied % 8 < 5
+                        by_scalar = emptied % 4 < 3
                         emptied += 1
                         turned = banks.tile([P, PACK, P], F32, tag="for_scalar" if by_scalar else "for_vector")
                         for t in range(PACK):
@@ -264,7 +264,7 @@ def tile_kanblock_pb_kernel(tc, h, grid, w2_base, w2_spline, out):
             g = j - 1
             if 0 <= g < BASES:
                 rise_tail[n, g] = work.tile([P, BATCH_COLS], F32, name="rise_tail", tag="rise_tail")
-                nc.vector.tensor_scalar(
+                nc.gpsimd.tensor_scalar(
                     out=rise_tail[n, g][:], in0=cube[n, j][:], scalar1=k["rise_tail"][:, g : g + 1], scalar2=0.0,
                     op0=ALU.mult, op1=ALU.min,
                 )
@@ -273,9 +273,15 @@ def tile_kanblock_pb_kernel(tc, h, grid, w2_base, w2_spline, out):
             g = j - 3
             if 0 <= g < BASES:
                 fall_tail[n, g] = work.tile([P, BATCH_COLS], F32, name="fall_tail", tag="fall_tail")
-                nc.scalar.activation(
-                    out=fall_tail[n, g][:], in_=cube[n, j][:], func=ACT.Relu, scale=k["fall_tail"][:, g : g + 1]
-                )
+                if g % 2 == 0:
+                    nc.scalar.activation(
+                        out=fall_tail[n, g][:], in_=cube[n, j][:], func=ACT.Relu, scale=k["fall_tail"][:, g : g + 1]
+                    )
+                else:
+                    nc.vector.tensor_scalar(
+                        out=fall_tail[n, g][:], in0=cube[n, j][:], scalar1=k["fall_tail"][:, g : g + 1], scalar2=0.0,
+                        op0=ALU.mult, op1=ALU.max,
+                    )
 
         def sum_rise(n, j):
             g = j - 1

@@ -165,7 +165,7 @@ def tile_kanblock_pb_kernel(tc, h, grid, w2_base, w2_spline, out):
                 for q in range(PAIRS):
                     w_grouped = w_stage.tile([P, 2, OUTPUTS, PACK], BF16, align_bytes=64)
                     for dt in range(OUTPUT_TILES):
-                        by_scalar = emptied % 4 < 3
+                        by_scalar = emptied % 8 < 5
                         emptied += 1
                         turned = banks.tile([P, PACK, P], F32, tag="for_scalar" if by_scalar else "for_vector")
                         for t in range(PACK):
@@ -264,7 +264,7 @@ def tile_kanblock_pb_kernel(tc, h, grid, w2_base, w2_spline, out):
             g = j - 1
             if 0 <= g < BASES:
                 rise_tail[n, g] = work.tile([P, BATCH_COLS], F32, name="rise_tail", tag="rise_tail")
-                nc.gpsimd.tensor_scalar(
+                nc.vector.tensor_scalar(
                     out=rise_tail[n, g][:], in0=cube[n, j][:], scalar1=k["rise_tail"][:, g : g + 1], scalar2=0.0,
                     op0=ALU.mult, op1=ALU.min,
                 )
@@ -273,15 +273,9 @@ def tile_kanblock_pb_kernel(tc, h, grid, w2_base, w2_spline, out):
             g = j - 3
             if 0 <= g < BASES:
                 fall_tail[n, g] = work.tile([P, BATCH_COLS], F32, name="fall_tail", tag="fall_tail")
-                if g % 2 == 0:
-                    nc.scalar.activation(
-                        out=fall_tail[n, g][:], in_=cube[n, j][:], func=ACT.Relu, scale=k["fall_tail"][:, g : g + 1]
-                    )
-                else:
-                    nc.vector.tensor_scalar(
-                        out=fall_tail[n, g][:], in0=cube[n, j][:], scalar1=k["fall_tail"][:, g : g + 1], scalar2=0.0,
-                        op0=ALU.mult, op1=ALU.max,
-                    )
+                nc.scalar.activation(
+                    out=fall_tail[n, g][:], in_=cube[n, j][:], func=ACT.Relu, scale=k["fall_tail"][:, g : g + 1]
+                )
 
         def sum_rise(n, j):
             g = j - 1
@@ -306,7 +300,7 @@ def tile_kanblock_pb_kernel(tc, h, grid, w2_base, w2_spline, out):
                 for cc in range(CHUNKS_PER_BATCH):
                     fall_bank[n, g, cc] = banks.tile([P, PACK, P], F32, name="fall_bank", tag="for_vector")
                     sum_to_partitions(
-                        nc, fall_bank[n, g, cc], ident_f32, cube[n, j], fall_tail[n, g], cc * K_PASS, 1 if cc == 0 else 0
+                        nc, fall_bank[n, g, cc], ident_f32, cube[n, j], fall_tail[n, g], cc * K_PASS, 0
                     )
 
         def finish_bases(n, j):

@@ -22,15 +22,19 @@ KNOTS = 12
 TOKEN_TILES = TOKENS // P
 OUTPUT_TILES = OUTPUTS // P
 CHUNKS = FEATURES // K_PASS
-PAIRS = BASES // 2
+PAIR = 2
+PAIRS = BASES // PAIR
 CHUNKS_PER_BATCH = 2
 BATCHES = CHUNKS // CHUNKS_PER_BATCH
 BATCH_COLS = CHUNKS_PER_BATCH * K_PASS
 BATCH_COUNT = TOKEN_TILES * BATCHES
 STRIDE = BASES
-FIRST_SLOT = -4
-TILE_SLOTS = STRIDE * (BATCHES - 1) + KNOTS + 2
-LAST_SLOT = STRIDE * BATCHES * (TOKEN_TILES - 1) + TILE_SLOTS
+ACTIVATE_AT = -4
+QUANTISE_SILU_AT = -3
+BASE_PRODUCT_AT = -2
+STORE_AT = STRIDE * (BATCHES - 1) + KNOTS + 2
+FIRST_SLOT = ACTIVATE_AT
+LAST_SLOT = STRIDE * BATCHES * (TOKEN_TILES - 1) + STORE_AT
 
 FLOPS = 2 * TOKENS * OUTPUTS * (FEATURES + FEATURES * BASES)
 
@@ -44,24 +48,24 @@ def knot_constants(nc, consts, grid):
     nc.vector.tensor_scalar_mul(out=neg_knots[:], in0=knots[:], scalar1=-1.0)
 
     span = {}
-    for k in range(1, 5):
-        span[k] = consts.tile([P, KNOTS - k], F32, name="span%d" % k)
-        nc.vector.tensor_sub(out=span[k][:], in0=knots[:, k:KNOTS], in1=knots[:, 0 : KNOTS - k])
+    for width in range(1, 5):
+        span[width] = consts.tile([P, KNOTS - width], F32, name="span%d" % width)
+        nc.vector.tensor_sub(out=span[width][:], in0=knots[:, width:KNOTS], in1=knots[:, 0 : KNOTS - width])
     inv_span1 = consts.tile([P, KNOTS - 1], F32)
     nc.vector.reciprocal(out=inv_span1[:], in_=span[1][:])
 
-    n = BASES + 1
-    up_two = consts.tile([P, n], F32)
-    nc.vector.tensor_mul(out=up_two[:], in0=span[1][:, 0:n], in1=span[2][:, 0:n])
-    inv_up = consts.tile([P, n], F32)
-    nc.vector.tensor_mul(out=inv_up[:], in0=up_two[:], in1=span[3][:, 0:n])
-    up = consts.tile([P, n], F32)
+    count = BASES + 1
+    up_two = consts.tile([P, count], F32)
+    nc.vector.tensor_mul(out=up_two[:], in0=span[1][:, 0:count], in1=span[2][:, 0:count])
+    inv_up = consts.tile([P, count], F32)
+    nc.vector.tensor_mul(out=inv_up[:], in0=up_two[:], in1=span[3][:, 0:count])
+    up = consts.tile([P, count], F32)
     nc.vector.reciprocal(out=up[:], in_=inv_up[:])
-    down_two = consts.tile([P, n], F32)
-    nc.vector.tensor_mul(out=down_two[:], in0=span[1][:, 2 : 2 + n], in1=span[2][:, 1 : 1 + n])
-    inv_down = consts.tile([P, n], F32)
-    nc.vector.tensor_mul(out=inv_down[:], in0=down_two[:], in1=span[3][:, 0:n])
-    down = consts.tile([P, n], F32)
+    down_two = consts.tile([P, count], F32)
+    nc.vector.tensor_mul(out=down_two[:], in0=span[1][:, 2 : 2 + count], in1=span[2][:, 1 : 1 + count])
+    inv_down = consts.tile([P, count], F32)
+    nc.vector.tensor_mul(out=inv_down[:], in0=down_two[:], in1=span[3][:, 0:count])
+    down = consts.tile([P, count], F32)
     nc.vector.reciprocal(out=down[:], in_=inv_down[:])
 
     rise_ratio = consts.tile([P, BASES], F32)
@@ -70,48 +74,45 @@ def knot_constants(nc, consts, grid):
     )
     rise_part = consts.tile([P, BASES], F32)
     nc.vector.tensor_mul(out=rise_part[:], in0=rise_ratio[:], in1=inv_up[:, 0:BASES])
-    rise_tail = consts.tile([P, BASES], F32)
-    nc.vector.tensor_mul(out=rise_tail[:], in0=rise_part[:], in1=up[:, 1 : 1 + BASES])
+    rise_tail_factor = consts.tile([P, BASES], F32, name="rise_tail")
+    nc.vector.tensor_mul(out=rise_tail_factor[:], in0=rise_part[:], in1=up[:, 1 : 1 + BASES])
     fall_ratio = consts.tile([P, BASES], F32)
     nc.vector.scalar_tensor_tensor(
         out=fall_ratio[:], in0=span[4][:], scalar=-1.0, in1=inv_span1[:, 3 : 3 + BASES], op0=ALU.mult, op1=ALU.mult
     )
     fall_part = consts.tile([P, BASES], F32)
     nc.vector.tensor_mul(out=fall_part[:], in0=fall_ratio[:], in1=inv_down[:, 1 : 1 + BASES])
-    fall_tail = consts.tile([P, BASES], F32)
-    nc.vector.tensor_mul(out=fall_tail[:], in0=fall_part[:], in1=down[:, 0:BASES])
+    fall_tail_factor = consts.tile([P, BASES], F32, name="fall_tail")
+    nc.vector.tensor_mul(out=fall_tail_factor[:], in0=fall_part[:], in1=down[:, 0:BASES])
     fall_scale = consts.tile([P, BASES], F32)
     nc.vector.tensor_scalar_mul(out=fall_scale[:], in0=down[:, 1 : 1 + BASES], scalar1=-1.0)
     return {
         "knots": knots,
         "neg_knots": neg_knots,
         "rise_scale": up,
-        "rise_tail": rise_tail,
+        "rise_tail_factor": rise_tail_factor,
         "fall_scale": fall_scale,
-        "fall_tail": fall_tail,
+        "fall_tail_factor": fall_tail_factor,
     }
 
 
 def features_to_partitions(nc, banks, ident_bf, rows_sb, grouped):
     for c in range(CHUNKS):
         turned = banks.tile([P, PACK, P], BF16, tag="for_vector")
-        for t in range(PACK):
-            first = (c * PACK + t) * P
-            nc.tensor.transpose(turned[:, t, :], rows_sb[:, first : first + P], ident_bf[:])
-        nc.vector.tensor_copy(out=grouped[:, c, :, :], in_=turned[:].rearrange("p t r -> p r t"))
+        for v in range(PACK):
+            first = (c * PACK + v) * P
+            nc.tensor.transpose(turned[:, v, :], rows_sb[:, first : first + P], ident_bf[:])
+        nc.vector.tensor_copy(out=grouped[:, c, :, :], in_=turned[:].rearrange("p v r -> p r v"))
 
 
-def sum_to_partitions(nc, bank, ident_f32, lead, tail, first_col, plain_quarters):
-    for t in range(PACK):
-        cols = slice(first_col + t * P, first_col + (t + 1) * P)
-        passes_through = t >= plain_quarters
+def sum_to_partitions(nc, bank, ident_f32, lead, tail, first_col):
+    for v in range(PACK):
+        cols = slice(first_col + v * P, first_col + (v + 1) * P)
         nc.tensor.matmul(
-            out=bank[:, t, :], lhsT=lead[:, cols], rhs=ident_f32[:], is_transpose=passes_through,
-            start=True, stop=False,
+            out=bank[:, v, :], lhsT=lead[:, cols], rhs=ident_f32[:], is_transpose=True, start=True, stop=False
         )
         nc.tensor.matmul(
-            out=bank[:, t, :], lhsT=tail[:, cols], rhs=ident_f32[:], is_transpose=passes_through,
-            start=False, stop=True,
+            out=bank[:, v, :], lhsT=tail[:, cols], rhs=ident_f32[:], is_transpose=True, start=False, stop=True
         )
 
 
@@ -130,7 +131,7 @@ def tile_kanblock_pb_kernel(tc, h, grid, w2_base, w2_spline, out):
         masks.make_identity(nc, ident_bf[:])
         ident_f32 = consts.tile([P, P], F32)
         masks.make_identity(nc, ident_f32[:])
-        k = knot_constants(nc, consts, grid)
+        consts_of = knot_constants(nc, consts, grid)
 
         base_codes = keep.tile([P, CHUNKS, OUTPUTS], U32, align_bytes=64)
         base_scales = keep.tile([P, CHUNKS, OUTPUTS], U8, align_bytes=64)
@@ -145,14 +146,14 @@ def tile_kanblock_pb_kernel(tc, h, grid, w2_base, w2_spline, out):
 
             base_grouped = w_stage.tile([P, CHUNKS, OUTPUTS, PACK], BF16, align_bytes=64, bufs=1)
             for dt in range(OUTPUT_TILES):
-                base_sb = w_rows.tile([P, FEATURES], BF16)
+                base_sb = w_rows.tile([P, FEATURES], BF16, bufs=OUTPUT_TILES)
                 nc.sync.dma_start(out=base_sb[:], in_=w2_base[dt * P : (dt + 1) * P, :])
                 features_to_partitions(nc, banks, ident_bf, base_sb, base_grouped[:, :, dt * P : (dt + 1) * P, :])
             for c in range(CHUNKS):
                 nc.vector.quantize_mx(
                     out=base_codes[:, c, :].bitcast(FP8X4),
                     scales=base_scales[:, c, :],
-                    in_=base_grouped[:, c, :, :].rearrange("p d t -> p (d t)"),
+                    in_=base_grouped[:, c, :, :].rearrange("p d v -> p (d v)"),
                 )
 
             emptied = 0
@@ -161,25 +162,25 @@ def tile_kanblock_pb_kernel(tc, h, grid, w2_base, w2_spline, out):
                 w_sb = w_rows.tile([P, OUTPUT_TILES, row_len], BF16)
                 for dt in range(OUTPUT_TILES):
                     nc.sync.dma_start(out=w_sb[:, dt, :], in_=spline_rows[:, dt, c * row_len : (c + 1) * row_len])
-                w_words = w_sb[:].bitcast(F32).rearrange("p dt (t i q) -> p dt t i q", t=PACK, q=PAIRS)
+                w_words = w_sb[:].bitcast(F32).rearrange("p dt (v i q) -> p dt v i q", v=PACK, q=PAIRS)
                 for q in range(PAIRS):
-                    w_grouped = w_stage.tile([P, 2, OUTPUTS, PACK], BF16, align_bytes=64)
+                    w_grouped = w_stage.tile([P, PAIR, OUTPUTS, PACK], BF16, align_bytes=64)
                     for dt in range(OUTPUT_TILES):
                         by_scalar = emptied % 8 < 5
                         emptied += 1
                         turned = banks.tile([P, PACK, P], F32, tag="for_scalar" if by_scalar else "for_vector")
-                        for t in range(PACK):
-                            nc.tensor.transpose(turned[:, t, :], w_words[:, dt, t, :, q], ident_f32[:])
-                        halves = turned[:].bitcast(BF16).rearrange("p t (d e) -> p e d t", e=2)
+                        for v in range(PACK):
+                            nc.tensor.transpose(turned[:, v, :], w_words[:, dt, v, :, q], ident_f32[:])
+                        halves = turned[:].bitcast(BF16).rearrange("p v (d e) -> p e d v", e=PAIR)
                         if by_scalar:
                             nc.scalar.copy(out=w_grouped[:, :, dt * P : (dt + 1) * P, :], in_=halves)
                         else:
                             nc.vector.tensor_copy(out=w_grouped[:, :, dt * P : (dt + 1) * P, :], in_=halves)
-                    for e in range(2):
+                    for e in range(PAIR):
                         nc.vector.quantize_mx(
-                            out=w_codes[:, c, 2 * q + e, :].bitcast(FP8X4),
-                            scales=w_scales[:, c, 2 * q + e, :],
-                            in_=w_grouped[:, e, :, :].rearrange("p d t -> p (d t)"),
+                            out=w_codes[:, c, PAIR * q + e, :].bitcast(FP8X4),
+                            scales=w_scales[:, c, PAIR * q + e, :],
+                            in_=w_grouped[:, e, :, :].rearrange("p d v -> p (d v)"),
                         )
 
         rows = ctx.enter_context(tc.tile_pool(name="rows", bufs=1))
@@ -206,8 +207,8 @@ def tile_kanblock_pb_kernel(tc, h, grid, w2_base, w2_spline, out):
         def activate(tt):
             x[tt] = rows.tile([P, FEATURES], BF16, name="x", tag="x", bufs=2)
             nc.vector.tensor_scalar(
-                out=x[tt][:], in0=h_all[:, tt, :], scalar1=k["knots"][:, 0:1],
-                scalar2=k["knots"][:, KNOTS - 1 : KNOTS], op0=ALU.max, op1=ALU.min,
+                out=x[tt][:], in0=h_all[:, tt, :], scalar1=consts_of["knots"][:, 0:1],
+                scalar2=consts_of["knots"][:, KNOTS - 1 : KNOTS], op0=ALU.max, op1=ALU.min,
             )
             silu_sb[tt] = rows.tile([P, FEATURES], BF16, name="silu_sb", tag="silu_sb")
             nc.scalar.activation(out=silu_sb[tt][:], in_=h_all[:, tt, :], func=ACT.Silu)
@@ -220,7 +221,7 @@ def tile_kanblock_pb_kernel(tc, h, grid, w2_base, w2_spline, out):
             nc.vector.quantize_mx(
                 out=silu_codes[tt][:].rearrange("p c n -> p (c n)").bitcast(FP8X4),
                 scales=silu_scales[tt][:].rearrange("p c n -> p (c n)"),
-                in_=silu_grouped[tt][:].rearrange("p c n t -> p (c n t)"),
+                in_=silu_grouped[tt][:].rearrange("p c n v -> p (c n v)"),
             )
 
         def base_product(tt):
@@ -241,98 +242,102 @@ def tile_kanblock_pb_kernel(tc, h, grid, w2_base, w2_spline, out):
             nc.scalar.copy(out=result[:], in_=acc[tt][:])
             nc.sync.dma_start(out=out_rows[tt * P : (tt + 1) * P, :], in_=result[:])
 
-        def batch_x(n):
-            first = (n % BATCHES) * BATCH_COLS
-            return x[n // BATCHES][:, first : first + BATCH_COLS]
+        def batch_x(batch):
+            first = (batch % BATCHES) * BATCH_COLS
+            return x[batch // BATCHES][:, first : first + BATCH_COLS]
 
-        def make_square(n, j):
+        def make_square(batch, j):
             if 0 <= j < KNOTS:
-                square[n, j] = work.tile([P, BATCH_COLS], F32, name="square", tag="square", bufs=4)
+                square[batch, j] = work.tile([P, BATCH_COLS], F32, name="square", tag="square", bufs=4)
                 nc.scalar.activation(
-                    out=square[n, j][:], in_=batch_x(n), func=ACT.Square, bias=k["neg_knots"][:, j : j + 1], scale=1.0
+                    out=square[batch, j][:], in_=batch_x(batch), func=ACT.Square, bias=consts_of["neg_knots"][:, j : j + 1], scale=1.0
                 )
 
-        def make_cube(n, j):
+        def make_cube(batch, j):
             if 0 <= j < KNOTS:
-                cube[n, j] = work.tile([P, BATCH_COLS], F32, name="cube", tag="cube", bufs=6)
+                cube[batch, j] = work.tile([P, BATCH_COLS], F32, name="cube", tag="cube", bufs=6)
                 nc.vector.scalar_tensor_tensor(
-                    out=cube[n, j][:], in0=batch_x(n), scalar=k["knots"][:, j : j + 1], in1=square[n, j][:],
+                    out=cube[batch, j][:], in0=batch_x(batch), scalar=consts_of["knots"][:, j : j + 1], in1=square[batch, j][:],
                     op0=ALU.subtract, op1=ALU.mult,
                 )
 
-        def make_rise_tail(n, j):
+        def make_rise_tail(batch, j):
             g = j - 1
             if 0 <= g < BASES:
-                rise_tail[n, g] = work.tile([P, BATCH_COLS], F32, name="rise_tail", tag="rise_tail")
+                rise_tail[batch, g] = work.tile([P, BATCH_COLS], F32, name="rise_tail", tag="rise_tail")
                 nc.vector.tensor_scalar(
-                    out=rise_tail[n, g][:], in0=cube[n, j][:], scalar1=k["rise_tail"][:, g : g + 1], scalar2=0.0,
+                    out=rise_tail[batch, g][:], in0=cube[batch, j][:], scalar1=consts_of["rise_tail_factor"][:, g : g + 1], scalar2=0.0,
                     op0=ALU.mult, op1=ALU.min,
                 )
 
-        def make_fall_tail(n, j):
+        def make_fall_tail(batch, j):
             g = j - 3
             if 0 <= g < BASES:
-                fall_tail[n, g] = work.tile([P, BATCH_COLS], F32, name="fall_tail", tag="fall_tail")
-                nc.scalar.activation(
-                    out=fall_tail[n, g][:], in_=cube[n, j][:], func=ACT.Relu, scale=k["fall_tail"][:, g : g + 1]
-                )
+                fall_tail[batch, g] = work.tile([P, BATCH_COLS], F32, name="fall_tail", tag="fall_tail")
+                if g == BASES - 1:
+                    nc.vector.tensor_scalar(
+                        out=fall_tail[batch, g][:], in0=cube[batch, j][:], scalar1=consts_of["fall_tail_factor"][:, g : g + 1],
+                        scalar2=0.0, op0=ALU.mult, op1=ALU.max,
+                    )
+                else:
+                    nc.scalar.activation(
+                        out=fall_tail[batch, g][:], in_=cube[batch, j][:], func=ACT.Relu, scale=consts_of["fall_tail_factor"][:, g : g + 1]
+                    )
 
-        def sum_rise(n, j):
+        def sum_rise(batch, j):
             g = j - 1
             if 0 <= g < BASES:
                 for cc in range(CHUNKS_PER_BATCH):
-                    rise_bank[n, g, cc] = banks.tile([P, PACK, P], F32, name="rise_bank", tag="for_scalar")
-                    sum_to_partitions(nc, rise_bank[n, g, cc], ident_f32, cube[n, g], rise_tail[n, g], cc * K_PASS, 0)
+                    rise_bank[batch, g, cc] = banks.tile([P, PACK, P], F32, name="rise_bank", tag="for_scalar")
+                    sum_to_partitions(nc, rise_bank[batch, g, cc], ident_f32, cube[batch, g], rise_tail[batch, g], cc * K_PASS)
 
-        def round_rise(n, j):
+        def round_rise(batch, j):
             g = j - 1
             if 0 <= g < BASES:
-                risen[n, g] = work.tile([P, CHUNKS_PER_BATCH, P, PACK], BF16, name="risen", tag="risen", bufs=6)
+                risen[batch, g] = work.tile([P, CHUNKS_PER_BATCH, P, PACK], BF16, name="risen", tag="risen", bufs=6)
                 for cc in range(CHUNKS_PER_BATCH):
                     nc.scalar.activation(
-                        out=risen[n, g][:, cc, :, :], in_=rise_bank[n, g, cc][:].rearrange("p t n -> p n t"),
-                        func=ACT.Relu, scale=k["rise_scale"][:, g : g + 1],
+                        out=risen[batch, g][:, cc, :, :], in_=rise_bank[batch, g, cc][:].rearrange("p v n -> p n v"),
+                        func=ACT.Relu, scale=consts_of["rise_scale"][:, g : g + 1],
                     )
 
-        def sum_fall(n, j):
+        def sum_fall(batch, j):
             g = j - 4
             if 0 <= g < BASES:
                 for cc in range(CHUNKS_PER_BATCH):
-                    fall_bank[n, g, cc] = banks.tile([P, PACK, P], F32, name="fall_bank", tag="for_vector")
-                    sum_to_partitions(
-                        nc, fall_bank[n, g, cc], ident_f32, cube[n, j], fall_tail[n, g], cc * K_PASS, 0
-                    )
+                    fall_bank[batch, g, cc] = banks.tile([P, PACK, P], F32, name="fall_bank", tag="for_vector")
+                    sum_to_partitions(nc, fall_bank[batch, g, cc], ident_f32, cube[batch, j], fall_tail[batch, g], cc * K_PASS)
 
-        def finish_bases(n, j):
+        def finish_bases(batch, j):
             g = j - 4
             if 0 <= g < BASES:
-                bases[n, g] = operands.tile([P, CHUNKS_PER_BATCH, P, PACK], BF16, align_bytes=64, name="bases", tag="bases", bufs=2)
+                bases[batch, g] = operands.tile([P, CHUNKS_PER_BATCH, P, PACK], BF16, align_bytes=64, name="bases", tag="bases", bufs=2)
                 for cc in range(CHUNKS_PER_BATCH):
                     nc.vector.scalar_tensor_tensor(
-                        out=bases[n, g][:, cc, :, :], in0=fall_bank[n, g, cc][:].rearrange("p t n -> p n t"),
-                        scalar=k["fall_scale"][:, g : g + 1], in1=risen[n, g][:, cc, :, :],
+                        out=bases[batch, g][:, cc, :, :], in0=fall_bank[batch, g, cc][:].rearrange("p v n -> p n v"),
+                        scalar=consts_of["fall_scale"][:, g : g + 1], in1=risen[batch, g][:, cc, :, :],
                         op0=ALU.mult, op1=ALU.max,
                     )
 
-        def quantise_bases(n, j):
+        def quantise_bases(batch, j):
             g = j - 4
             if 0 <= g < BASES:
-                b_codes[n, g] = operands.tile([P, CHUNKS_PER_BATCH, P], U32, align_bytes=64, name="b_codes", tag="b_codes")
-                b_scales[n, g] = operands.tile([P, CHUNKS_PER_BATCH, P], U8, align_bytes=64, name="b_scales", tag="b_scales")
+                b_codes[batch, g] = operands.tile([P, CHUNKS_PER_BATCH, P], U32, align_bytes=64, name="b_codes", tag="b_codes")
+                b_scales[batch, g] = operands.tile([P, CHUNKS_PER_BATCH, P], U8, align_bytes=64, name="b_scales", tag="b_scales")
                 nc.vector.quantize_mx(
-                    out=b_codes[n, g][:].rearrange("p c n -> p (c n)").bitcast(FP8X4),
-                    scales=b_scales[n, g][:].rearrange("p c n -> p (c n)"),
-                    in_=bases[n, g][:].rearrange("p c n t -> p (c n t)"),
+                    out=b_codes[batch, g][:].rearrange("p cc n -> p (cc n)").bitcast(FP8X4),
+                    scales=b_scales[batch, g][:].rearrange("p cc n -> p (cc n)"),
+                    in_=bases[batch, g][:].rearrange("p cc n v -> p (cc n v)"),
                 )
 
-        def multiply(n, j, cc):
+        def multiply(batch, j, cc):
             g = j - 4
             if 0 <= g < BASES:
-                c = (n % BATCHES) * CHUNKS_PER_BATCH + cc
+                c = (batch % BATCHES) * CHUNKS_PER_BATCH + cc
                 nc.tensor.matmul_mx(
-                    out=acc[n // BATCHES][:],
-                    lhsT=b_codes[n, g][:, cc, :].bitcast(FP8X4),
-                    lhsT_scale=b_scales[n, g][:, cc, :],
+                    out=acc[batch // BATCHES][:],
+                    lhsT=b_codes[batch, g][:, cc, :].bitcast(FP8X4),
+                    lhsT_scale=b_scales[batch, g][:, cc, :],
                     rhs=w_codes[:, c, g, :].bitcast(FP8X4),
                     rhs_scale=w_scales[:, c, g, :],
                     start=False,
@@ -342,38 +347,38 @@ def tile_kanblock_pb_kernel(tc, h, grid, w2_base, w2_spline, out):
         with tc.manual_schedule():
             for slot in range(FIRST_SLOT, LAST_SLOT + 1):
                 every_batch = range(BATCH_COUNT)
-                knot = [slot - STRIDE * n for n in every_batch]
+                knot = [slot - STRIDE * batch for batch in every_batch]
                 for tt in range(TOKEN_TILES):
                     since_start = slot - STRIDE * BATCHES * tt
-                    if since_start == -4:
+                    if since_start == ACTIVATE_AT:
                         activate(tt)
-                    if since_start == -2:
+                    if since_start == BASE_PRODUCT_AT:
                         base_product(tt)
-                for n in every_batch:
-                    make_square(n, knot[n] + 1)
-                for n in every_batch:
-                    make_cube(n, knot[n])
-                for n in every_batch:
-                    sum_rise(n, knot[n] - 1)
-                for n in every_batch:
-                    multiply(n, knot[n] - 2, 0)
-                for n in every_batch:
-                    round_rise(n, knot[n] - 1)
-                for n in every_batch:
-                    finish_bases(n, knot[n] - 1)
+                for batch in every_batch:
+                    make_square(batch, knot[batch] + 1)
+                for batch in every_batch:
+                    make_cube(batch, knot[batch])
+                for batch in every_batch:
+                    sum_rise(batch, knot[batch] - 1)
+                for batch in every_batch:
+                    multiply(batch, knot[batch] - 2, 0)
+                for batch in every_batch:
+                    round_rise(batch, knot[batch] - 1)
+                for batch in every_batch:
+                    finish_bases(batch, knot[batch] - 1)
                 for tt in range(TOKEN_TILES):
-                    if slot - STRIDE * BATCHES * tt == -3:
+                    if slot - STRIDE * BATCHES * tt == QUANTISE_SILU_AT:
                         quantise_silu(tt)
-                for n in every_batch:
-                    make_rise_tail(n, knot[n])
-                for n in every_batch:
-                    make_fall_tail(n, knot[n])
-                for n in every_batch:
-                    quantise_bases(n, knot[n] - 1)
-                for n in every_batch:
-                    sum_fall(n, knot[n])
-                for n in every_batch:
-                    multiply(n, knot[n] - 2, 1)
+                for batch in every_batch:
+                    make_rise_tail(batch, knot[batch])
+                for batch in every_batch:
+                    make_fall_tail(batch, knot[batch])
+                for batch in every_batch:
+                    quantise_bases(batch, knot[batch] - 1)
+                for batch in every_batch:
+                    sum_fall(batch, knot[batch])
+                for batch in every_batch:
+                    multiply(batch, knot[batch] - 2, 1)
                 for tt in range(TOKEN_TILES):
-                    if slot - STRIDE * BATCHES * tt == TILE_SLOTS:
+                    if slot - STRIDE * BATCHES * tt == STORE_AT:
                         store(tt)

@@ -361,8 +361,6 @@ def tile_kanblock_pb_kernel(tc, h, grid, w2_base, w2_spline, out):
                 for batch in every_batch:
                     sum_rise(batch, knot[batch] - 1)
                 for batch in every_batch:
-                    multiply(batch, knot[batch] - 2, 0)
-                for batch in every_batch:
                     round_rise(batch, knot[batch] - 1)
                 for batch in every_batch:
                     finish_bases(batch, knot[batch] - 1)
@@ -378,7 +376,8 @@ def tile_kanblock_pb_kernel(tc, h, grid, w2_base, w2_spline, out):
                 for batch in every_batch:
                     sum_fall(batch, knot[batch])
                 for batch in every_batch:
-                    multiply(batch, knot[batch] - 2, 1)
+                    for cc in range(CHUNKS_PER_BATCH):
+                        multiply(batch, knot[batch] - 2, cc)
                 for tt in range(TOKEN_TILES):
                     if slot - STRIDE * BATCHES * tt == STORE_AT:
                         store(tt)

@@ -166,7 +166,7 @@ def tile_kanblock_pb_kernel(tc, h, grid, w2_base, w2_spline, out):
                 for q in range(PAIRS):
                     w_grouped = w_stage.tile([P, PAIR, OUTPUTS, PACK], BF16, align_bytes=64)
                     for dt in range(OUTPUT_TILES):
-                        by_scalar = emptied % 8 < 5
+                        by_scalar = emptied % 8 < 7
                         emptied += 1
                         turned = banks.tile([P, PACK, P], F32, tag="for_scalar" if by_scalar else "for_vector")
                         for v in range(PACK):

@@ -19,24 +19,46 @@ FEATURES = 2048
 OUTPUTS = 512
 BASES = 8
 KNOTS = 12
+TILES = 8
+TENTS = 4
 TOKEN_TILES = TOKENS // P
 OUTPUT_TILES = OUTPUTS // P
 CHUNKS = FEATURES // K_PASS
 PAIR = 2
 PAIRS = BASES // PAIR
-CHUNKS_PER_BATCH = 2
-BATCHES = CHUNKS // CHUNKS_PER_BATCH
-BATCH_COLS = CHUNKS_PER_BATCH * K_PASS
-BATCH_COUNT = TOKEN_TILES * BATCHES
-STRIDE = BASES
-ACTIVATE_AT = -4
-QUANTISE_SILU_AT = -3
-BASE_PRODUCT_AT = -2
-STORE_AT = STRIDE * (BATCHES - 1) + KNOTS + 2
-FIRST_SLOT = ACTIVATE_AT
-LAST_SLOT = STRIDE * BATCHES * (TOKEN_TILES - 1) + STORE_AT
+BATCH_COUNT = TOKEN_TILES * CHUNKS
+TILE_SLOTS = 4 * CHUNKS
+STRIDE = 4
 
 FLOPS = 2 * TOKENS * OUTPUTS * (FEATURES + FEATURES * BASES)
+
+SCALAR_SUMS = {2: (("rise", 0), ("fall", 5)), 3: (("rise", 1), ("fall", 6)), 4: (("rise", 2), ("fall", 7)), 5: (("fall", 4), ("rise", 3))}
+VECTOR_SUMS = {4: (("rise", 5), ("fall", 1)), 5: (("rise", 7), ("fall", 0)), 6: (("rise", 4), ("fall", 2)), 7: (("rise", 6), ("fall", 3))}
+LAST = 8
+JOINED = (("fall", 1), ("fall", 0), ("fall", 2), ("rise", 6))
+SCALAR_TAILS = (("fall", 4), ("fall", 5), ("rise", 1), ("rise", 2))
+
+
+def lead_tile(kind, g):
+    return g if kind == "rise" else (g + 4) % TILES
+
+
+def tail_tile(kind, g):
+    return (g + 1) % TILES if kind == "rise" else (g + 3) % TILES
+
+
+def lead_is_positive(kind, g):
+    return kind == "rise" and g >= TENTS
+
+
+def tail_is_positive(kind, g):
+    return g >= 3 if kind == "rise" else g == 0
+
+
+def drain_is_positive(kind, g):
+    if (kind, g) in JOINED:
+        return not tail_is_positive(kind, g)
+    return lead_is_positive(kind, g)
 
 
 def knot_constants(nc, consts, grid):
@@ -44,11 +66,9 @@ def knot_constants(nc, consts, grid):
     nc.sync.dma_start(out=knots_bf[:], in_=grid.partition_broadcast(P))
     knots = consts.tile([P, KNOTS], F32)
     nc.vector.tensor_copy(out=knots[:], in_=knots_bf[:])
-    neg_knots = consts.tile([P, KNOTS], F32)
-    nc.vector.tensor_scalar_mul(out=neg_knots[:], in0=knots[:], scalar1=-1.0)
 
     span = {}
-    for width in range(1, 5):
+    for width in (1, 2, 3, 4, 8):
         span[width] = consts.tile([P, KNOTS - width], F32, name="span%d" % width)
         nc.vector.tensor_sub(out=span[width][:], in0=knots[:, width:KNOTS], in1=knots[:, 0 : KNOTS - width])
     inv_span1 = consts.tile([P, KNOTS - 1], F32)
@@ -68,52 +88,96 @@ def knot_constants(nc, consts, grid):
     down = consts.tile([P, count], F32)
     nc.vector.reciprocal(out=down[:], in_=inv_down[:])
 
-    rise_ratio = consts.tile([P, BASES], F32)
-    nc.vector.scalar_tensor_tensor(
-        out=rise_ratio[:], in0=span[4][:], scalar=-1.0, in1=inv_span1[:, 0:BASES], op0=ALU.mult, op1=ALU.mult
-    )
-    rise_part = consts.tile([P, BASES], F32)
-    nc.vector.tensor_mul(out=rise_part[:], in0=rise_ratio[:], in1=inv_up[:, 0:BASES])
-    rise_tail_factor = consts.tile([P, BASES], F32, name="rise_tail")
-    nc.vector.tensor_mul(out=rise_tail_factor[:], in0=rise_part[:], in1=up[:, 1 : 1 + BASES])
-    fall_ratio = consts.tile([P, BASES], F32)
-    nc.vector.scalar_tensor_tensor(
-        out=fall_ratio[:], in0=span[4][:], scalar=-1.0, in1=inv_span1[:, 3 : 3 + BASES], op0=ALU.mult, op1=ALU.mult
-    )
-    fall_part = consts.tile([P, BASES], F32)
-    nc.vector.tensor_mul(out=fall_part[:], in0=fall_ratio[:], in1=inv_down[:, 1 : 1 + BASES])
-    fall_tail_factor = consts.tile([P, BASES], F32, name="fall_tail")
-    nc.vector.tensor_mul(out=fall_tail_factor[:], in0=fall_part[:], in1=down[:, 0:BASES])
-    fall_scale = consts.tile([P, BASES], F32)
-    nc.vector.tensor_scalar_mul(out=fall_scale[:], in0=down[:, 1 : 1 + BASES], scalar1=-1.0)
+    def product(name, first, *others):
+        value = first
+        for i in range(len(others)):
+            out = consts.tile([P, BASES], F32, name="%s_%d" % (name, i))
+            nc.vector.tensor_mul(out=out[:], in0=value, in1=others[i])
+            value = out[:]
+        return value
+
+    rise_ratio = product("rise_ratio", span[4][:], inv_span1[:, 0:BASES], inv_up[:, 0:BASES], up[:, 1 : 1 + BASES])
+    fall_ratio = product("fall_ratio", span[4][:], inv_span1[:, 3 : 3 + BASES], inv_down[:, 1 : 1 + BASES], down[:, 0:BASES])
+    inv_fall_ratio = consts.tile([P, BASES], F32)
+    nc.vector.reciprocal(out=inv_fall_ratio[:], in_=fall_ratio)
+
+    weight = consts.tile([P, 2 * TILES], F32)
+
+    def column(tile, j):
+        return tile[:, j : j + 1]
+
+    def times(k, value, factor):
+        nc.vector.tensor_mul(out=column(weight, k), in0=value, in1=factor)
+
+    nc.vector.memset(weight[:, 0:1], 1.0)
+    times(1, column(weight, 0), column(rise_ratio, 0))
+    times(2, column(weight, 1), column(inv_fall_ratio, 6))
+    through = consts.tile([P, 1], F32)
+    nc.vector.tensor_mul(out=through[:], in0=column(weight, 1), in1=column(rise_ratio, 1))
+    times(3, through[:], column(inv_fall_ratio, 7))
+    times(4, column(weight, 3), column(inv_fall_ratio, 0))
+    times(5, column(weight, 4), column(inv_fall_ratio, 1))
+    times(6, column(weight, 5), column(inv_fall_ratio, 2))
+    times(7, column(weight, 6), column(rise_ratio, 6))
+    nc.vector.tensor_copy(out=weight[:, TILES : 2 * TILES], in_=weight[:, 0:TILES])
+    inv_weight = consts.tile([P, 2 * TILES], F32)
+    nc.vector.reciprocal(out=inv_weight[:], in_=weight[:])
+
+    root_raw = consts.tile([P, TILES], F32)
+    nc.scalar.sqrt(out=root_raw[:], in_=weight[:, 0:TILES])
+    inv_root = consts.tile([P, TILES], F32)
+    nc.vector.reciprocal(out=inv_root[:], in_=root_raw[:])
+    root_other = consts.tile([P, TILES], F32)
+    nc.vector.tensor_mul(out=root_other[:], in0=inv_root[:], in1=weight[:, 0:TILES])
+    root_sum = consts.tile([P, TILES], F32)
+    nc.vector.tensor_add(out=root_sum[:], in0=root_raw[:], in1=root_other[:])
+    root = consts.tile([P, TILES], F32)
+    nc.vector.tensor_scalar_mul(out=root[:], in0=root_sum[:], scalar1=0.5)
+
+    ends = consts.tile([P, TENTS], F32)
+    nc.vector.tensor_add(out=ends[:], in0=knots[:, 0:TENTS], in1=knots[:, 8 : 8 + TENTS])
+    neg_centre = consts.tile([P, TENTS], F32)
+    nc.vector.tensor_scalar_mul(out=neg_centre[:], in0=ends[:], scalar1=-0.5)
+    offset = consts.tile([P, TILES], F32)
+    nc.vector.tensor_scalar_mul(out=offset[:, 0:TENTS], in0=span[8][:], scalar1=0.5)
+    nc.vector.tensor_copy(out=offset[:, TENTS:TILES], in_=knots[:, TENTS:TILES])
+    root_offset = consts.tile([P, TILES], F32)
+    nc.vector.tensor_mul(out=root_offset[:], in0=offset[:], in1=root[:])
+    bias = consts.tile([P, TILES], F32)
+    nc.vector.tensor_scalar_mul(out=bias[:], in0=root_offset[:], scalar1=-1.0)
+
+    drain = {
+        "rise": product("rise_drain", up[:, 0:BASES], inv_weight[:, 0:BASES]),
+        "fall": product("fall_drain", down[:, 1 : 1 + BASES], inv_weight[:, 4 : 4 + BASES]),
+    }
+    factor = {
+        "rise": product("rise_factor", rise_ratio, weight[:, 0:BASES], inv_weight[:, 1 : 1 + BASES]),
+        "fall": product("fall_factor", fall_ratio, weight[:, 4 : 4 + BASES], inv_weight[:, 3 : 3 + BASES]),
+    }
+    neg_drain = {}
+    neg_factor = {}
+    for kind in ("rise", "fall"):
+        neg_drain[kind] = consts.tile([P, BASES], F32, name="neg_drain_" + kind)
+        nc.vector.tensor_scalar_mul(out=neg_drain[kind][:], in0=drain[kind], scalar1=-1.0)
+        neg_factor[kind] = consts.tile([P, BASES], F32, name="neg_factor_" + kind)
+        nc.vector.tensor_scalar_mul(out=neg_factor[kind][:], in0=factor[kind], scalar1=-1.0)
+
+    def drain_of(kind, g):
+        return column(drain[kind] if drain_is_positive(kind, g) else neg_drain[kind], g)
+
+    def factor_of(kind, g):
+        positive = tail_is_positive(kind, g) != lead_is_positive(kind, g)
+        return column(factor[kind] if positive else neg_factor[kind], g)
+
     return {
         "knots": knots,
-        "neg_knots": neg_knots,
-        "rise_scale": up,
-        "rise_tail_factor": rise_tail_factor,
-        "fall_scale": fall_scale,
-        "fall_tail_factor": fall_tail_factor,
+        "neg_centre": neg_centre,
+        "offset": offset,
+        "bias": bias,
+        "root": root,
+        "drain_of": drain_of,
+        "factor_of": factor_of,
     }
-
-
-def features_to_partitions(nc, banks, ident_bf, rows_sb, grouped):
-    for c in range(CHUNKS):
-        turned = banks.tile([P, PACK, P], BF16, tag="for_vector")
-        for v in range(PACK):
-            first = (c * PACK + v) * P
-            nc.tensor.transpose(turned[:, v, :], rows_sb[:, first : first + P], ident_bf[:])
-        nc.vector.tensor_copy(out=grouped[:, c, :, :], in_=turned[:].rearrange("p v r -> p r v"))
-
-
-def sum_to_partitions(nc, bank, ident_f32, lead, tail, first_col):
-    for v in range(PACK):
-        cols = slice(first_col + v * P, first_col + (v + 1) * P)
-        nc.tensor.matmul(
-            out=bank[:, v, :], lhsT=lead[:, cols], rhs=ident_f32[:], is_transpose=True, start=True, stop=False
-        )
-        nc.tensor.matmul(
-            out=bank[:, v, :], lhsT=tail[:, cols], rhs=ident_f32[:], is_transpose=True, start=False, stop=True
-        )
 
 
 def tile_kanblock_pb_kernel(tc, h, grid, w2_base, w2_spline, out):
@@ -124,11 +188,10 @@ def tile_kanblock_pb_kernel(tc, h, grid, w2_base, w2_spline, out):
     with ExitStack() as ctx:
         consts = ctx.enter_context(tc.tile_pool(name="consts", bufs=1))
         keep = ctx.enter_context(tc.tile_pool(name="keep", bufs=1))
-        sums = ctx.enter_context(tc.psum_pool(name="sums", bufs=2))
-        banks = ctx.enter_context(tc.psum_pool(name="banks", bufs=3))
+        sums = ctx.enter_context(tc.psum_pool(name="sums", bufs=1))
+        banks = ctx.enter_context(tc.psum_pool(name="banks", bufs=1))
+        BANKS = {"for_scalar": 3, "for_vector": 2, "for_weights": 2}
 
-        ident_bf = consts.tile([P, P], BF16)
-        masks.make_identity(nc, ident_bf[:])
         ident_f32 = consts.tile([P, P], F32)
         masks.make_identity(nc, ident_f32[:])
         consts_of = knot_constants(nc, consts, grid)
@@ -137,87 +200,133 @@ def tile_kanblock_pb_kernel(tc, h, grid, w2_base, w2_spline, out):
         base_scales = keep.tile([P, CHUNKS, OUTPUTS], U8, align_bytes=64)
         w_codes = keep.tile([P, CHUNKS, BASES, OUTPUTS], U32, align_bytes=64)
         w_scales = keep.tile([P, CHUNKS, BASES, OUTPUTS], U8, align_bytes=64)
-        h_all = keep.tile([P, TOKEN_TILES, FEATURES], BF16)
-        nc.gpsimd.dma_start(out=h_all[:], in_=h.rearrange("(tt p) i -> p tt i", p=P))
+        h_rows = ctx.enter_context(tc.tile_pool(name="h_rows", bufs=1))
+        w_rows = ctx.enter_context(tc.tile_pool(name="w_rows", bufs=4))
+        w_stage = ctx.enter_context(tc.tile_pool(name="w_stage", bufs=2))
+        rows = ctx.enter_context(tc.tile_pool(name="rows", bufs=1))
+        work = ctx.enter_context(tc.tile_pool(name="work", bufs=1))
+        operands = ctx.enter_context(tc.tile_pool(name="operands", bufs=4))
 
-        with ExitStack() as weights:
-            w_rows = weights.enter_context(tc.tile_pool(name="w_rows", bufs=2))
-            w_stage = weights.enter_context(tc.tile_pool(name="w_stage", bufs=2))
+        def new_bank(tag, shape, dtype=F32):
+            return banks.tile(shape, dtype, name="bank", tag=tag, bufs=BANKS[tag])
 
-            base_grouped = w_stage.tile([P, CHUNKS, OUTPUTS, PACK], BF16, align_bytes=64, bufs=1)
-            for dt in range(OUTPUT_TILES):
-                base_sb = w_rows.tile([P, FEATURES], BF16, bufs=OUTPUT_TILES)
-                nc.sync.dma_start(out=base_sb[:], in_=w2_base[dt * P : (dt + 1) * P, :])
-                features_to_partitions(nc, banks, ident_bf, base_sb, base_grouped[:, :, dt * P : (dt + 1) * P, :])
+        def empty(tag, out, in_):
+            if tag == "for_scalar":
+                nc.scalar.copy(out=out, in_=in_)
+            else:
+                nc.vector.tensor_copy(out=out, in_=in_)
+
+        def pairs_to_partitions(rows_sb, first_chunk, grouped, tag):
+            words = rows_sb[:].bitcast(F32)
+            turned = new_bank("for_weights", [P, 2, PAIR, P])
+            for cc in range(2):
+                for u in range(PAIR):
+                    first = ((first_chunk + cc) * PAIR + u) * P
+                    nc.tensor.transpose(turned[:, cc, u, :], words[:, first : first + P], ident_f32[:])
+            empty(tag, grouped[:, first_chunk : first_chunk + 2, :, :], turned[:].rearrange("p c u r -> p c r u"))
+
+        base_sb = {}
+        base_grouped = {}
+
+        def load_base(dt):
+            base_sb[dt] = rows.tile([P, FEATURES], BF16, name="unquantised", tag="unquantised")
+            nc.sync.dma_start(out=base_sb[dt][:], in_=w2_base[dt * P : (dt + 1) * P, :])
+
+        def turn_base(dt):
+            base_grouped[dt] = rows.tile([P, CHUNKS, P, PACK], BF16, align_bytes=64, name="grouped", tag="grouped")
+            words = base_grouped[dt][:].bitcast(F32)
+            for c in range(0, CHUNKS, 2):
+                pairs_to_partitions(base_sb[dt], c, words, "for_vector" if c else "for_scalar")
+
+        def quantise_base(dt):
+            cols = slice(dt * P, (dt + 1) * P)
             for c in range(CHUNKS):
                 nc.vector.quantize_mx(
-                    out=base_codes[:, c, :].bitcast(FP8X4),
-                    scales=base_scales[:, c, :],
-                    in_=base_grouped[:, c, :, :].rearrange("p d v -> p (d v)"),
+                    out=base_codes[:, c, cols].bitcast(FP8X4),
+                    scales=base_scales[:, c, cols],
+                    in_=base_grouped[dt][:, c, :, :].rearrange("p d v -> p (d v)"),
                 )
 
-            emptied = 0
-            for c in range(CHUNKS):
-                row_len = K_PASS * BASES
-                w_sb = w_rows.tile([P, OUTPUT_TILES, row_len], BF16)
-                for dt in range(OUTPUT_TILES):
-                    nc.sync.dma_start(out=w_sb[:, dt, :], in_=spline_rows[:, dt, c * row_len : (c + 1) * row_len])
-                w_words = w_sb[:].bitcast(F32).rearrange("p dt (v i q) -> p dt v i q", v=PACK, q=PAIRS)
-                for q in range(PAIRS):
-                    w_grouped = w_stage.tile([P, PAIR, OUTPUTS, PACK], BF16, align_bytes=64)
-                    for dt in range(OUTPUT_TILES):
-                        by_scalar = emptied % 8 < 7
-                        emptied += 1
-                        turned = banks.tile([P, PACK, P], F32, tag="for_scalar" if by_scalar else "for_vector")
-                        for v in range(PACK):
-                            nc.tensor.transpose(turned[:, v, :], w_words[:, dt, v, :, q], ident_f32[:])
-                        halves = turned[:].bitcast(BF16).rearrange("p v (d e) -> p e d v", e=PAIR)
-                        if by_scalar:
-                            nc.scalar.copy(out=w_grouped[:, :, dt * P : (dt + 1) * P, :], in_=halves)
-                        else:
-                            nc.vector.tensor_copy(out=w_grouped[:, :, dt * P : (dt + 1) * P, :], in_=halves)
-                    for e in range(PAIR):
-                        nc.vector.quantize_mx(
-                            out=w_codes[:, c, PAIR * q + e, :].bitcast(FP8X4),
-                            scales=w_scales[:, c, PAIR * q + e, :],
-                            in_=w_grouped[:, e, :, :].rearrange("p d v -> p (d v)"),
-                        )
+        w_sb = {}
+        w_grouped = {}
 
-        rows = ctx.enter_context(tc.tile_pool(name="rows", bufs=1))
-        work = ctx.enter_context(tc.tile_pool(name="work", bufs=3))
-        operands = ctx.enter_context(tc.tile_pool(name="operands", bufs=3))
+        def load_spline(unit):
+            c, half = unit
+            row_len = K_PASS * BASES
+            for dt in (2 * half, 2 * half + 1):
+                w_sb[c, dt] = w_rows.tile([P, row_len], BF16, name="w_sb", tag="w_sb")
+                nc.sync.dma_start(out=w_sb[c, dt][:], in_=spline_rows[:, dt, c * row_len : (c + 1) * row_len])
 
+        turned = {}
+
+        def turn_spline(unit, q):
+            c, half = unit
+            for i in range(2):
+                words = w_sb[c, 2 * half + i][:].bitcast(F32).rearrange("p (v i q) -> p v i q", v=PACK, q=PAIRS)
+                turned[i] = new_bank("for_weights", [P, PACK, P])
+                for v in range(PACK):
+                    nc.tensor.transpose(turned[i][:, v, :], words[:, v, :, q], ident_f32[:])
+
+        def copy_spline(unit, q):
+            w_grouped[unit, q] = w_stage.tile([P, PAIR, 2 * P, PACK], BF16, align_bytes=64, name="w_grouped", tag="w_grouped")
+            for i in range(2):
+                empty(
+                    "for_vector" if (unit, q, i) in W_VECTOR else "for_scalar", w_grouped[unit, q][:, :, i * P : (i + 1) * P, :],
+                    turned[i][:].bitcast(BF16).rearrange("p v (d e) -> p e d v", e=PAIR),
+                )
+
+        def quantise_spline(unit, q):
+            c, half = unit
+            cols = slice(2 * half * P, 2 * (half + 1) * P)
+            for e in range(PAIR):
+                nc.vector.quantize_mx(
+                    out=w_codes[:, c, PAIR * q + e, cols].bitcast(FP8X4),
+                    scales=w_scales[:, c, PAIR * q + e, cols],
+                    in_=w_grouped[unit, q][:, e, :, :].rearrange("p d v -> p (d v)"),
+                )
+
+        h_sb = {}
         x = {}
         silu_sb = {}
         silu_grouped = {}
         silu_codes = {}
         silu_scales = {}
         acc = {}
+        folded = {}
         square = {}
-        cube = {}
-        rise_tail = {}
-        fall_tail = {}
-        rise_bank = {}
-        fall_bank = {}
-        risen = {}
+        tile = {}
+        tail = {}
+        bank = {}
+        drained = {}
         bases = {}
         b_codes = {}
         b_scales = {}
 
-        def activate(tt):
+        def load(tt):
+            h_sb[tt] = h_rows.tile([P, FEATURES], BF16, name="h_sb", tag="h_sb")
+            nc.sync.dma_start(out=h_sb[tt][:], in_=h[tt * P : (tt + 1) * P, :])
+
+        def clamp(tt):
             x[tt] = rows.tile([P, FEATURES], BF16, name="x", tag="x", bufs=2)
             nc.vector.tensor_scalar(
-                out=x[tt][:], in0=h_all[:, tt, :], scalar1=consts_of["knots"][:, 0:1],
+                out=x[tt][:], in0=h_sb[tt][:], scalar1=consts_of["knots"][:, 0:1],
                 scalar2=consts_of["knots"][:, KNOTS - 1 : KNOTS], op0=ALU.max, op1=ALU.min,
             )
-            silu_sb[tt] = rows.tile([P, FEATURES], BF16, name="silu_sb", tag="silu_sb")
-            nc.scalar.activation(out=silu_sb[tt][:], in_=h_all[:, tt, :], func=ACT.Silu)
+
+        def activate(tt, c):
+            if c == 0:
+                silu_sb[tt] = rows.tile([P, FEATURES], BF16, name="unquantised", tag="unquantised")
+            cols = slice(c * K_PASS, (c + 1) * K_PASS)
+            nc.scalar.activation(out=silu_sb[tt][:, cols], in_=h_sb[tt][:, cols], func=ACT.Silu)
+
+        def turn_silu(tt, c):
+            if c == 0:
+                silu_grouped[tt] = rows.tile([P, CHUNKS, P, PACK], BF16, align_bytes=64, name="grouped", tag="grouped")
+            pairs_to_partitions(silu_sb[tt], c, silu_grouped[tt][:].bitcast(F32), "for_vector" if c else "for_scalar")
 
         def quantise_silu(tt):
-            silu_grouped[tt] = rows.tile([P, CHUNKS, P, PACK], BF16, align_bytes=64, name="silu_grouped", tag="silu_grouped")
-            features_to_partitions(nc, banks, ident_bf, silu_sb[tt], silu_grouped[tt][:])
-            silu_codes[tt] = operands.tile([P, CHUNKS, P], U32, align_bytes=64, name="silu_codes", tag="silu_codes", bufs=2)
-            silu_scales[tt] = operands.tile([P, CHUNKS, P], U8, align_bytes=64, name="silu_scales", tag="silu_scales", bufs=2)
+            silu_codes[tt] = rows.tile([P, CHUNKS, P], U32, align_bytes=64, name="silu_codes", tag="silu_codes")
+            silu_scales[tt] = rows.tile([P, CHUNKS, P], U8, align_bytes=64, name="silu_scales", tag="silu_scales")
             nc.vector.quantize_mx(
                 out=silu_codes[tt][:].rearrange("p c n -> p (c n)").bitcast(FP8X4),
                 scales=silu_scales[tt][:].rearrange("p c n -> p (c n)"),
@@ -225,7 +334,6 @@ def tile_kanblock_pb_kernel(tc, h, grid, w2_base, w2_spline, out):
             )
 
         def base_product(tt):
-            acc[tt] = sums.tile([P, OUTPUTS], F32, name="acc", tag="acc")
             for c in range(CHUNKS):
                 nc.tensor.matmul_mx(
                     out=acc[tt][:],
@@ -233,151 +341,225 @@ def tile_kanblock_pb_kernel(tc, h, grid, w2_base, w2_spline, out):
                     lhsT_scale=silu_scales[tt][:, c, :],
                     rhs=base_codes[:, c, :].bitcast(FP8X4),
                     rhs_scale=base_scales[:, c, :],
-                    start=(c == 0),
+                    start=False,
                     stop=False,
                 )
 
         def store(tt):
-            result = rows.tile([P, OUTPUTS], F32, name="result", tag="result", bufs=2)
+            result = rows.tile([P, OUTPUTS], F32, name="result", tag="result")
             nc.scalar.copy(out=result[:], in_=acc[tt][:])
             nc.sync.dma_start(out=out_rows[tt * P : (tt + 1) * P, :], in_=result[:])
 
-        def batch_x(batch):
-            first = (batch % BATCHES) * BATCH_COLS
-            return x[batch // BATCHES][:, first : first + BATCH_COLS]
+        def batch_x(b):
+            first = (b % CHUNKS) * K_PASS
+            return x[b // CHUNKS][:, first : first + K_PASS]
 
-        def make_square(batch, j):
-            if 0 <= j < KNOTS:
-                square[batch, j] = work.tile([P, BATCH_COLS], F32, name="square", tag="square", bufs=4)
-                nc.scalar.activation(
-                    out=square[batch, j][:], in_=batch_x(batch), func=ACT.Square, bias=consts_of["neg_knots"][:, j : j + 1], scale=1.0
-                )
+        def column(name, k):
+            return consts_of[name][:, k : k + 1]
 
-        def make_cube(batch, j):
-            if 0 <= j < KNOTS:
-                cube[batch, j] = work.tile([P, BATCH_COLS], F32, name="cube", tag="cube", bufs=6)
+        def fold(b, k):
+            folded[b, k] = work.tile([P, K_PASS], F32, name="folded", tag="folded", bufs=2)
+            nc.scalar.activation(out=folded[b, k][:], in_=batch_x(b), func=ACT.Abs, bias=column("neg_centre", k), scale=1.0)
+
+        def argument(b, k):
+            return folded[b, k][:] if k < TENTS else batch_x(b)
+
+        def make_square(b, k):
+            tag = "tent" if k < TENTS else "cube"
+            square[b, k] = work.tile([P, K_PASS], F32, name=tag, tag=tag, bufs=TENT_BUFS if k < TENTS else CUBE_BUFS)
+            nc.scalar.activation(out=square[b, k][:], in_=argument(b, k), func=ACT.Square, bias=column("bias", k), scale=column("root", k))
+
+        def make_tile(b, k):
+            tile[b, k] = square[b, k]
+            nc.vector.scalar_tensor_tensor(
+                out=tile[b, k][:], in0=argument(b, k), scalar=column("offset", k), in1=square[b, k][:],
+                op0=ALU.subtract, op1=ALU.mult,
+            )
+
+        def tail_key(kind, g):
+            return SHARED.get((kind, g), (kind, g))
+
+        def make_tail(b, kind, g):
+            if (kind, g) in SHARED:
+                return
+            source = tile[b, tail_tile(kind, g)][:]
+            tail[b, kind, g] = work.tile([P, K_PASS], F32, name="tail", tag="tail", bufs=TAIL_BUFS)
+            into = tail[b, kind, g][:]
+            factor = consts_of["factor_of"](kind, g)
+            if (kind, g) in JOINED:
                 nc.vector.scalar_tensor_tensor(
-                    out=cube[batch, j][:], in0=batch_x(batch), scalar=consts_of["knots"][:, j : j + 1], in1=square[batch, j][:],
-                    op0=ALU.subtract, op1=ALU.mult,
+                    out=into, in0=source, scalar=0.0, in1=tile[b, lead_tile(kind, g)][:],
+                    op0=ALU.max if tail_is_positive(kind, g) else ALU.min,
+                    op1=ALU.add if tail_is_positive(kind, g) != lead_is_positive(kind, g) else ALU.subtract,
                 )
-
-        def make_rise_tail(batch, j):
-            g = j - 1
-            if 0 <= g < BASES:
-                rise_tail[batch, g] = work.tile([P, BATCH_COLS], F32, name="rise_tail", tag="rise_tail")
+            elif (kind, g) in SCALAR_TAILS:
+                nc.scalar.activation(out=into, in_=source, func=ACT.Relu, scale=factor)
+            else:
                 nc.vector.tensor_scalar(
-                    out=rise_tail[batch, g][:], in0=cube[batch, j][:], scalar1=consts_of["rise_tail_factor"][:, g : g + 1], scalar2=0.0,
-                    op0=ALU.mult, op1=ALU.min,
+                    out=into, in0=source, scalar1=factor, scalar2=0.0,
+                    op0=ALU.mult, op1=ALU.min if lead_is_positive(kind, g) else ALU.max,
                 )
 
-        def make_fall_tail(batch, j):
-            g = j - 3
-            if 0 <= g < BASES:
-                fall_tail[batch, g] = work.tile([P, BATCH_COLS], F32, name="fall_tail", tag="fall_tail")
-                if g == BASES - 1:
-                    nc.vector.tensor_scalar(
-                        out=fall_tail[batch, g][:], in0=cube[batch, j][:], scalar1=consts_of["fall_tail_factor"][:, g : g + 1],
-                        scalar2=0.0, op0=ALU.mult, op1=ALU.max,
-                    )
+        def sum_up(members):
+            for b, q, i, kind, g, tag in members:
+                bank[b, kind, g] = new_bank(tag, [P, PACK, P])
+            for v in range(PACK):
+                cols = slice(v * P, (v + 1) * P)
+                for part in range(2):
+                    for b, q, i, kind, g, tag in members:
+                        into = bank[b, kind, g][:, v, :]
+                        tail_sb = tail[(b,) + tail_key(kind, g)]
+                        lead_sb = tile[b, lead_tile(kind, g)]
+                        if (kind, g) in JOINED:
+                            if part == 0:
+                                nc.tensor.transpose(into, tail_sb[:, cols], ident_f32[:])
+                        else:
+                            nc.tensor.matmul(
+                                out=into, lhsT=(tail_sb if part else lead_sb)[:, cols], rhs=ident_f32[:], is_transpose=True,
+                                start=(part == 0), stop=(part == 1),
+                            )
+
+        def round_sum(b, kind, g):
+            drained[b, g] = work.tile([P, P, PACK], BF16, name="drained", tag="drained", bufs=DRAINED_BUFS)
+            nc.scalar.activation(
+                out=drained[b, g][:], in_=bank[b, kind, g][:].rearrange("p v n -> p n v"),
+                func=ACT.Relu, scale=consts_of["drain_of"](kind, g),
+            )
+
+        def finish(b, q, i, kind, g):
+            if i == 0:
+                bases[b, q] = operands.tile([P, 2, P, PACK], BF16, align_bytes=64, name="bases", tag="bases", bufs=3)
+            nc.vector.scalar_tensor_tensor(
+                out=bases[b, q][:, i, :, :], in0=bank[b, kind, g][:].rearrange("p v n -> p n v"),
+                scalar=consts_of["drain_of"](kind, g), in1=drained[b, g][:], op0=ALU.mult, op1=ALU.max,
+            )
+
+        def take_out(members):
+            for b, q, i, kind, g, tag in members:
+                if tag == "for_scalar":
+                    round_sum(b, kind, g)
                 else:
-                    nc.scalar.activation(
-                        out=fall_tail[batch, g][:], in_=cube[batch, j][:], func=ACT.Relu, scale=consts_of["fall_tail_factor"][:, g : g + 1]
-                    )
+                    finish(b, q, i, kind, g)
 
-        def sum_rise(batch, j):
-            g = j - 1
-            if 0 <= g < BASES:
-                for cc in range(CHUNKS_PER_BATCH):
-                    rise_bank[batch, g, cc] = banks.tile([P, PACK, P], F32, name="rise_bank", tag="for_scalar")
-                    sum_to_partitions(nc, rise_bank[batch, g, cc], ident_f32, cube[batch, g], rise_tail[batch, g], cc * K_PASS)
+        def quantise_bases(b, q):
+            b_codes[b, q] = operands.tile([P, 2, P], U32, align_bytes=64, name="b_codes", tag="b_codes")
+            b_scales[b, q] = operands.tile([P, 2, P], U8, align_bytes=64, name="b_scales", tag="b_scales")
+            nc.vector.quantize_mx(
+                out=b_codes[b, q][:].rearrange("p i n -> p (i n)").bitcast(FP8X4),
+                scales=b_scales[b, q][:].rearrange("p i n -> p (i n)"),
+                in_=bases[b, q][:].rearrange("p i n v -> p (i n v)"),
+            )
 
-        def round_rise(batch, j):
-            g = j - 1
-            if 0 <= g < BASES:
-                risen[batch, g] = work.tile([P, CHUNKS_PER_BATCH, P, PACK], BF16, name="risen", tag="risen", bufs=6)
-                for cc in range(CHUNKS_PER_BATCH):
-                    nc.scalar.activation(
-                        out=risen[batch, g][:, cc, :, :], in_=rise_bank[batch, g, cc][:].rearrange("p v n -> p n v"),
-                        func=ACT.Relu, scale=consts_of["rise_scale"][:, g : g + 1],
-                    )
-
-        def sum_fall(batch, j):
-            g = j - 4
-            if 0 <= g < BASES:
-                for cc in range(CHUNKS_PER_BATCH):
-                    fall_bank[batch, g, cc] = banks.tile([P, PACK, P], F32, name="fall_bank", tag="for_vector")
-                    sum_to_partitions(nc, fall_bank[batch, g, cc], ident_f32, cube[batch, j], fall_tail[batch, g], cc * K_PASS)
-
-        def finish_bases(batch, j):
-            g = j - 4
-            if 0 <= g < BASES:
-                bases[batch, g] = operands.tile([P, CHUNKS_PER_BATCH, P, PACK], BF16, align_bytes=64, name="bases", tag="bases", bufs=2)
-                for cc in range(CHUNKS_PER_BATCH):
-                    nc.vector.scalar_tensor_tensor(
-                        out=bases[batch, g][:, cc, :, :], in0=fall_bank[batch, g, cc][:].rearrange("p v n -> p n v"),
-                        scalar=consts_of["fall_scale"][:, g : g + 1], in1=risen[batch, g][:, cc, :, :],
-                        op0=ALU.mult, op1=ALU.max,
-                    )
-
-        def quantise_bases(batch, j):
-            g = j - 4
-            if 0 <= g < BASES:
-                b_codes[batch, g] = operands.tile([P, CHUNKS_PER_BATCH, P], U32, align_bytes=64, name="b_codes", tag="b_codes")
-                b_scales[batch, g] = operands.tile([P, CHUNKS_PER_BATCH, P], U8, align_bytes=64, name="b_scales", tag="b_scales")
-                nc.vector.quantize_mx(
-                    out=b_codes[batch, g][:].rearrange("p cc n -> p (cc n)").bitcast(FP8X4),
-                    scales=b_scales[batch, g][:].rearrange("p cc n -> p (cc n)"),
-                    in_=bases[batch, g][:].rearrange("p cc n v -> p (cc n v)"),
-                )
-
-        def multiply(batch, j, cc):
-            g = j - 4
-            if 0 <= g < BASES:
-                c = (batch % BATCHES) * CHUNKS_PER_BATCH + cc
+        def multiply(b, q):
+            tt, c = b // CHUNKS, b % CHUNKS
+            for i in range(2):
+                g = VECTOR_SUMS[q][i][1]
+                first = c == 0 and q == FIRST_VECTOR and i == 0
+                if first:
+                    acc[tt] = sums.tile([P, OUTPUTS], F32, name="acc", tag="acc")
                 nc.tensor.matmul_mx(
-                    out=acc[batch // BATCHES][:],
-                    lhsT=b_codes[batch, g][:, cc, :].bitcast(FP8X4),
-                    lhsT_scale=b_scales[batch, g][:, cc, :],
+                    out=acc[tt][:],
+                    lhsT=b_codes[b, q][:, i, :].bitcast(FP8X4),
+                    lhsT_scale=b_scales[b, q][:, i, :],
                     rhs=w_codes[:, c, g, :].bitcast(FP8X4),
                     rhs_scale=w_scales[:, c, g, :],
-                    start=False,
-                    stop=(c == CHUNKS - 1 and g == BASES - 1),
+                    start=first,
+                    stop=(c == CHUNKS - 1 and q == LAST - 1 and i == 1),
                 )
 
+        TENT_BUFS = 7
+        CUBE_BUFS = 7
+        TAIL_BUFS = 9
+        DRAINED_BUFS = 10
+        FIRST_VECTOR = 4
+        W_VECTOR = [((c, half), q, 1) for c in range(CHUNKS) for half in range(2) for q in range(PAIRS) if q < 3]
+        SHARED = {("fall", 6): ("rise", 0), ("fall", 7): ("rise", 1)}
+
+        units = [(c, half) for c in range(CHUNKS) for half in range(2)]
+        load(0)
+        steps = [(unit, q) for unit in units for q in range(PAIRS)]
+        load_spline(units[0])
+        load_spline(units[1])
+
         with tc.manual_schedule():
-            for slot in range(FIRST_SLOT, LAST_SLOT + 1):
-                every_batch = range(BATCH_COUNT)
-                knot = [slot - STRIDE * batch for batch in every_batch]
-                for tt in range(TOKEN_TILES):
-                    since_start = slot - STRIDE * BATCHES * tt
-                    if since_start == ACTIVATE_AT:
-                        activate(tt)
-                    if since_start == BASE_PRODUCT_AT:
-                        base_product(tt)
-                for batch in every_batch:
-                    make_square(batch, knot[batch] + 1)
-                for batch in every_batch:
-                    make_cube(batch, knot[batch])
-                for batch in every_batch:
-                    sum_rise(batch, knot[batch] - 1)
-                for batch in every_batch:
-                    round_rise(batch, knot[batch] - 1)
-                for batch in every_batch:
-                    finish_bases(batch, knot[batch] - 1)
-                for tt in range(TOKEN_TILES):
-                    if slot - STRIDE * BATCHES * tt == QUANTISE_SILU_AT:
-                        quantise_silu(tt)
-                for batch in every_batch:
-                    make_rise_tail(batch, knot[batch])
-                for batch in every_batch:
-                    make_fall_tail(batch, knot[batch])
-                for batch in every_batch:
-                    quantise_bases(batch, knot[batch] - 1)
-                for batch in every_batch:
-                    sum_fall(batch, knot[batch])
-                for batch in every_batch:
-                    for cc in range(CHUNKS_PER_BATCH):
-                        multiply(batch, knot[batch] - 2, cc)
-                for tt in range(TOKEN_TILES):
-                    if slot - STRIDE * BATCHES * tt == STORE_AT:
+            late = []
+            open_step = None
+            for slot in range(-1, STRIDE * (BATCH_COUNT - 1) + LAST + 5):
+                live = [(b, slot - STRIDE * b) for b in range(BATCH_COUNT)]
+                ages = [(tt, slot - TILE_SLOTS * tt) for tt in range(TOKEN_TILES)]
+                first_step, second_step = [steps[s] if 0 <= s < len(steps) else None for s in (2 * slot, 2 * slot + 1)]
+                for tt, age in ages:
+                    if age == -1:
+                        clamp(tt)
+                    if age == TILE_SLOTS + 6:
                         store(tt)
+                sums_of = [[], []]
+                for b, q in live:
+                    for i in range(2):
+                        if q in SCALAR_SUMS:
+                            sums_of[i].append((b, q, i) + SCALAR_SUMS[q][i] + ("for_scalar",))
+                for b, q in live:
+                    for i in range(2):
+                        if q in VECTOR_SUMS:
+                            sums_of[i].append((b, q, i) + VECTOR_SUMS[q][i] + ("for_vector",))
+                squares = [(b, q + 1) for b, q in live if 0 <= q + 1 < STRIDE]
+                take_out(late)
+                if open_step:
+                    copy_spline(*open_step)
+                if slot in (12, 13, 14, 15):
+                    turn_base(slot - 12)
+                for tt, age in ages:
+                    if age in (9, 10):
+                        turn_silu(tt, 2 * (age - 9))
+                for b, q in live:
+                    if 0 <= q < STRIDE:
+                        make_tile(b, q)
+                        make_tile(b, q + TENTS)
+                for b, k in squares:
+                    fold(b, k)
+                    make_square(b, k)
+                sum_up(sums_of[0])
+                if first_step:
+                    turn_spline(*first_step)
+                take_out(sums_of[0])
+                if open_step:
+                    quantise_spline(*open_step)
+                for b, q in live:
+                    for kind, g in SCALAR_SUMS.get(q + 1, ()) + VECTOR_SUMS.get(q + 1, ()):
+                        make_tail(b, kind, g)
+                if first_step:
+                    copy_spline(*first_step)
+                for b, k in squares:
+                    make_square(b, k + TENTS)
+                sum_up(sums_of[1])
+                late = sums_of[1]
+                if second_step:
+                    turn_spline(*second_step)
+                    unit, q = second_step
+                    if q == PAIRS - 1 and units.index(unit) + 2 < len(units):
+                        load_spline(units[units.index(unit) + 2])
+                open_step = second_step
+                if slot in (12, 13, 14, 15):
+                    quantise_base(slot - 12)
+                if slot in (11, 12, 13, 14):
+                    load_base(slot - 11)
+                for tt, age in ages:
+                    if 4 <= age < 8:
+                        activate(tt, age - 4)
+                    if age == 8 and tt + 1 < TOKEN_TILES:
+                        load(tt + 1)
+                    if age == 11:
+                        quantise_silu(tt)
+                for b, q in live:
+                    if q - 1 in VECTOR_SUMS:
+                        quantise_bases(b, q - 1)
+                if first_step:
+                    quantise_spline(*first_step)
+                if slot % 2 == 1:
+                    for b, q in live:
+                        for made in (q - 3, q - 2):
+                            if made in VECTOR_SUMS:
+                                multiply(b, made)
+                    for tt, age in ages:
+                        if age == 19:
+                            base_product(tt)

@@ -33,9 +33,9 @@ STRIDE = 4
 FLOPS = 2 * TOKENS * OUTPUTS * (FEATURES + FEATURES * BASES)
 
 SCALAR_SUMS = {2: (("rise", 0), ("fall", 5)), 3: (("rise", 1), ("fall", 6)), 4: (("rise", 2), ("fall", 7)), 5: (("fall", 4), ("rise", 3))}
-VECTOR_SUMS = {4: (("rise", 5), ("fall", 1)), 5: (("rise", 7), ("fall", 0)), 6: (("rise", 4), ("fall", 2)), 7: (("rise", 6), ("fall", 3))}
+VECTOR_SUMS = {4: (("rise", 5), ("fall", 1)), 5: (("rise", 7), ("fall", 0)), 6: (("rise", 4), ("fall", 2)), 7: (("fall", 3), ("rise", 6))}
 LAST = 8
-JOINED = (("fall", 1), ("fall", 0), ("fall", 2), ("rise", 6))
+JOINED = (("fall", 1), ("fall", 2))
 SCALAR_TAILS = (("fall", 4), ("fall", 5), ("rise", 1), ("rise", 2))
 
 
@@ -190,7 +190,7 @@ def tile_kanblock_pb_kernel(tc, h, grid, w2_base, w2_spline, out):
         keep = ctx.enter_context(tc.tile_pool(name="keep", bufs=1))
         sums = ctx.enter_context(tc.psum_pool(name="sums", bufs=1))
         banks = ctx.enter_context(tc.psum_pool(name="banks", bufs=1))
-        BANKS = {"for_scalar": 3, "for_vector": 2, "for_weights": 2}
+        BANKS = {"for_scalar": 3, "for_vector": 2, "weights_by_scalar": 1, "weights_by_vector": 1}
 
         ident_f32 = consts.tile([P, P], F32)
         masks.make_identity(nc, ident_f32[:])
@@ -202,7 +202,7 @@ def tile_kanblock_pb_kernel(tc, h, grid, w2_base, w2_spline, out):
         w_scales = keep.tile([P, CHUNKS, BASES, OUTPUTS], U8, align_bytes=64)
         h_rows = ctx.enter_context(tc.tile_pool(name="h_rows", bufs=1))
         w_rows = ctx.enter_context(tc.tile_pool(name="w_rows", bufs=4))
-        w_stage = ctx.enter_context(tc.tile_pool(name="w_stage", bufs=2))
+        w_stage = ctx.enter_context(tc.tile_pool(name="w_stage", bufs=3))
         rows = ctx.enter_context(tc.tile_pool(name="rows", bufs=1))
         work = ctx.enter_context(tc.tile_pool(name="work", bufs=1))
         operands = ctx.enter_context(tc.tile_pool(name="operands", bufs=4))
@@ -211,14 +211,14 @@ def tile_kanblock_pb_kernel(tc, h, grid, w2_base, w2_spline, out):
             return banks.tile(shape, dtype, name="bank", tag=tag, bufs=BANKS[tag])
 
         def empty(tag, out, in_):
-            if tag == "for_scalar":
+            if tag == "weights_by_scalar":
                 nc.scalar.copy(out=out, in_=in_)
             else:
                 nc.vector.tensor_copy(out=out, in_=in_)
 
         def pairs_to_partitions(rows_sb, first_chunk, grouped, tag):
             words = rows_sb[:].bitcast(F32)
-            turned = new_bank("for_weights", [P, 2, PAIR, P])
+            turned = new_bank(tag, [P, 2, PAIR, P])
             for cc in range(2):
                 for u in range(PAIR):
                     first = ((first_chunk + cc) * PAIR + u) * P
@@ -228,15 +228,17 @@ def tile_kanblock_pb_kernel(tc, h, grid, w2_base, w2_spline, out):
         base_sb = {}
         base_grouped = {}
 
-        def load_base(dt):
-            base_sb[dt] = rows.tile([P, FEATURES], BF16, name="unquantised", tag="unquantised")
-            nc.sync.dma_start(out=base_sb[dt][:], in_=w2_base[dt * P : (dt + 1) * P, :])
+        def load_base(half):
+            for i in range(2):
+                dt = 2 * half + i
+                base_sb[dt] = w_rows.tile([P, FEATURES], BF16, name="w_sb", tag="w_sb")
+                nc.sync.dma_start(out=base_sb[dt][:], in_=w2_base[dt * P : (dt + 1) * P, :])
 
         def turn_base(dt):
             base_grouped[dt] = rows.tile([P, CHUNKS, P, PACK], BF16, align_bytes=64, name="grouped", tag="grouped")
             words = base_grouped[dt][:].bitcast(F32)
             for c in range(0, CHUNKS, 2):
-                pairs_to_partitions(base_sb[dt], c, words, "for_vector" if c else "for_scalar")
+                pairs_to_partitions(base_sb[dt], c, words, W_TAGS[c // 2])
 
         def quantise_base(dt):
             cols = slice(dt * P, (dt + 1) * P)
@@ -258,32 +260,33 @@ def tile_kanblock_pb_kernel(tc, h, grid, w2_base, w2_spline, out):
                 nc.sync.dma_start(out=w_sb[c, dt][:], in_=spline_rows[:, dt, c * row_len : (c + 1) * row_len])
 
         turned = {}
+        W_TAGS = ("weights_by_scalar", "weights_by_vector")
 
-        def turn_spline(unit, q):
-            c, half = unit
-            for i in range(2):
-                words = w_sb[c, 2 * half + i][:].bitcast(F32).rearrange("p (v i q) -> p v i q", v=PACK, q=PAIRS)
-                turned[i] = new_bank("for_weights", [P, PACK, P])
+        def turn_spline(step, i):
+            (c, half), q = step
+            words = w_sb[c, 2 * half + i][:].bitcast(F32).rearrange("p (v i q) -> p v i q", v=PACK, q=PAIRS)
+            for k in range(2):
+                turned[k] = new_bank(W_TAGS[k], [P, PACK, P])
                 for v in range(PACK):
-                    nc.tensor.transpose(turned[i][:, v, :], words[:, v, :, q], ident_f32[:])
+                    nc.tensor.transpose(turned[k][:, v, :], words[:, v, :, q + k], ident_f32[:])
 
-        def copy_spline(unit, q):
-            w_grouped[unit, q] = w_stage.tile([P, PAIR, 2 * P, PACK], BF16, align_bytes=64, name="w_grouped", tag="w_grouped")
-            for i in range(2):
-                empty(
-                    "for_vector" if (unit, q, i) in W_VECTOR else "for_scalar", w_grouped[unit, q][:, :, i * P : (i + 1) * P, :],
-                    turned[i][:].bitcast(BF16).rearrange("p v (d e) -> p e d v", e=PAIR),
-                )
+        def copy_spline(step, i):
+            for k in range(2):
+                if i == 0:
+                    w_grouped[step, k] = w_stage.tile([P, PAIR, 2 * P, PACK], BF16, align_bytes=64, name="w_grouped", tag="w_grouped")
+                empty(W_TAGS[k], w_grouped[step, k][:, :, i * P : (i + 1) * P, :], turned[k][:].bitcast(BF16).rearrange("p v (d e) -> p e d v", e=PAIR))
 
-        def quantise_spline(unit, q):
-            c, half = unit
+        def quantise_spline(step):
+            (c, half), q = step
             cols = slice(2 * half * P, 2 * (half + 1) * P)
-            for e in range(PAIR):
-                nc.vector.quantize_mx(
-                    out=w_codes[:, c, PAIR * q + e, cols].bitcast(FP8X4),
-                    scales=w_scales[:, c, PAIR * q + e, cols],
-                    in_=w_grouped[unit, q][:, e, :, :].rearrange("p d v -> p (d v)"),
-                )
+            for k in range(2):
+                for e in range(PAIR):
+                    g = PAIR * (q + k) + e
+                    nc.vector.quantize_mx(
+                        out=w_codes[:, c, g, cols].bitcast(FP8X4),
+                        scales=w_scales[:, c, g, cols],
+                        in_=w_grouped[step, k][:, e, :, :].rearrange("p d v -> p (d v)"),
+                    )
 
         h_sb = {}
         x = {}
@@ -322,7 +325,7 @@ def tile_kanblock_pb_kernel(tc, h, grid, w2_base, w2_spline, out):
         def turn_silu(tt, c):
             if c == 0:
                 silu_grouped[tt] = rows.tile([P, CHUNKS, P, PACK], BF16, align_bytes=64, name="grouped", tag="grouped")
-            pairs_to_partitions(silu_sb[tt], c, silu_grouped[tt][:].bitcast(F32), "for_vector" if c else "for_scalar")
+            pairs_to_partitions(silu_sb[tt], c, silu_grouped[tt][:].bitcast(F32), W_TAGS[c // 2])
 
         def quantise_silu(tt):
             silu_codes[tt] = rows.tile([P, CHUNKS, P], U32, align_bytes=64, name="silu_codes", tag="silu_codes")
@@ -400,9 +403,12 @@ def tile_kanblock_pb_kernel(tc, h, grid, w2_base, w2_spline, out):
                     op0=ALU.mult, op1=ALU.min if lead_is_positive(kind, g) else ALU.max,
                 )
 
-        def sum_up(members):
+        def sum_up(members, warm=False):
             for b, q, i, kind, g, tag in members:
                 bank[b, kind, g] = new_bank(tag, [P, PACK, P])
+            if warm and members:
+                b, q, i, kind, g, tag = members[0]
+                nc.tensor.matmul(out=bank[b, kind, g][:, 0, :], lhsT=ident_f32[:], rhs=ident_f32[:], start=True, stop=True)
             for v in range(PACK):
                 cols = slice(v * P, (v + 1) * P)
                 for part in range(2):
@@ -468,26 +474,25 @@ def tile_kanblock_pb_kernel(tc, h, grid, w2_base, w2_spline, out):
                 )
 
         TENT_BUFS = 7
-        CUBE_BUFS = 7
+        CUBE_BUFS = 8
         TAIL_BUFS = 9
         DRAINED_BUFS = 10
         FIRST_VECTOR = 4
-        W_VECTOR = [((c, half), q, 1) for c in range(CHUNKS) for half in range(2) for q in range(PAIRS) if q < 3]
         SHARED = {("fall", 6): ("rise", 0), ("fall", 7): ("rise", 1)}
 
         units = [(c, half) for c in range(CHUNKS) for half in range(2)]
         load(0)
-        steps = [(unit, q) for unit in units for q in range(PAIRS)]
+        steps = [(unit, q) for unit in units for q in range(0, PAIRS, 2)]
         load_spline(units[0])
         load_spline(units[1])
 
         with tc.manual_schedule():
             late = []
-            open_step = None
             for slot in range(-1, STRIDE * (BATCH_COUNT - 1) + LAST + 5):
                 live = [(b, slot - STRIDE * b) for b in range(BATCH_COUNT)]
                 ages = [(tt, slot - TILE_SLOTS * tt) for tt in range(TOKEN_TILES)]
-                first_step, second_step = [steps[s] if 0 <= s < len(steps) else None for s in (2 * slot, 2 * slot + 1)]
+                now = steps[slot] if 0 <= slot < len(steps) else None
+                before = steps[slot - 1] if 0 < slot <= len(steps) else None
                 for tt, age in ages:
                     if age == -1:
                         clamp(tt)
@@ -504,10 +509,10 @@ def tile_kanblock_pb_kernel(tc, h, grid, w2_base, w2_spline, out):
                             sums_of[i].append((b, q, i) + VECTOR_SUMS[q][i] + ("for_vector",))
                 squares = [(b, q + 1) for b, q in live if 0 <= q + 1 < STRIDE]
                 take_out(late)
-                if open_step:
-                    copy_spline(*open_step)
-                if slot in (12, 13, 14, 15):
-                    turn_base(slot - 12)
+                if before:
+                    copy_spline(before, 1)
+                if slot in (16, 17, 18, 19):
+                    turn_base(slot - 16)
                 for tt, age in ages:
                     if age in (9, 10):
                         turn_silu(tt, 2 * (age - 9))
@@ -517,32 +522,31 @@ def tile_kanblock_pb_kernel(tc, h, grid, w2_base, w2_spline, out):
                         make_tile(b, q + TENTS)
                 for b, k in squares:
                     fold(b, k)
+                    make_square(b, k + TENTS)
                     make_square(b, k)
-                sum_up(sums_of[0])
-                if first_step:
-                    turn_spline(*first_step)
-                take_out(sums_of[0])
-                if open_step:
-                    quantise_spline(*open_step)
                 for b, q in live:
                     for kind, g in SCALAR_SUMS.get(q + 1, ()) + VECTOR_SUMS.get(q + 1, ()):
                         make_tail(b, kind, g)
-                if first_step:
-                    copy_spline(*first_step)
-                for b, k in squares:
-                    make_square(b, k + TENTS)
-                sum_up(sums_of[1])
+                sum_up(sums_of[0])
+                if now:
+                    turn_spline(now, 0)
+                take_out(sums_of[0])
+                if before:
+                    quantise_spline(before)
+                if now:
+                    copy_spline(now, 0)
+                sum_up(sums_of[1], warm=True)
                 late = sums_of[1]
-                if second_step:
-                    turn_spline(*second_step)
-                    unit, q = second_step
-                    if q == PAIRS - 1 and units.index(unit) + 2 < len(units):
-                        load_spline(units[units.index(unit) + 2])
-                open_step = second_step
-                if slot in (12, 13, 14, 15):
-                    quantise_base(slot - 12)
-                if slot in (11, 12, 13, 14):
-                    load_base(slot - 11)
+                if now:
+                    turn_spline(now, 1)
+                    if slot % 2 == 1:
+                        u = slot // 2 + 2
+                        if u < len(units):
+                            load_spline(units[u])
+                        else:
+                            load_base(u - len(units))
+                if slot in (16, 17, 18, 19):
+                    quantise_base(slot - 16)
                 for tt, age in ages:
                     if 4 <= age < 8:
                         activate(tt, age - 4)
@@ -553,13 +557,9 @@ def tile_kanblock_pb_kernel(tc, h, grid, w2_base, w2_spline, out):
                 for b, q in live:
                     if q - 1 in VECTOR_SUMS:
                         quantise_bases(b, q - 1)
-                if first_step:
-                    quantise_spline(*first_step)
-                if slot % 2 == 1:
-                    for b, q in live:
-                        for made in (q - 3, q - 2):
-                            if made in VECTOR_SUMS:
-                                multiply(b, made)
-                    for tt, age in ages:
-                        if age == 19:
-                            base_product(tt)
+                for tt, age in ages:
+                    if age == TILE_SLOTS + 5:
+                        base_product(tt)
+                for b, q in live:
+                    if q - 2 in VECTOR_SUMS:
+                        multiply(b, q - 2)

@@ -32,11 +32,11 @@ STRIDE = 4
 
 FLOPS = 2 * TOKENS * OUTPUTS * (FEATURES + FEATURES * BASES)
 
-SCALAR_SUMS = {2: (("rise", 0), ("fall", 5)), 3: (("rise", 1), ("fall", 6)), 4: (("rise", 2), ("fall", 7)), 5: (("fall", 4), ("rise", 3))}
-VECTOR_SUMS = {4: (("rise", 5), ("fall", 1)), 5: (("rise", 7), ("fall", 0)), 6: (("rise", 4), ("fall", 2)), 7: (("fall", 3), ("rise", 6))}
+SCALAR_SUMS = {2: (0, 4), 3: (1, 5), 4: (6, 7), 5: (2, 3)}
+VECTOR_SUMS = {4: 0, 5: 6, 6: 2, 7: 4}
 LAST = 8
-JOINED = (("fall", 1), ("fall", 2))
-SCALAR_TAILS = (("fall", 4), ("fall", 5), ("rise", 1), ("rise", 2))
+JOINED = (("rise", 3), ("rise", 5))
+SCALAR_TAILS = (("rise", 1), ("rise", 2), ("fall", 1), ("fall", 4), ("fall", 2))
 
 
 def lead_tile(kind, g):
@@ -62,31 +62,8 @@ def drain_is_positive(kind, g):
 
 
 def knot_constants(nc, consts, grid):
-    knots_bf = consts.tile([P, KNOTS], BF16)
-    nc.sync.dma_start(out=knots_bf[:], in_=grid.partition_broadcast(P))
-    knots = consts.tile([P, KNOTS], F32)
-    nc.vector.tensor_copy(out=knots[:], in_=knots_bf[:])
-
-    span = {}
-    for width in (1, 2, 3, 4, 8):
-        span[width] = consts.tile([P, KNOTS - width], F32, name="span%d" % width)
-        nc.vector.tensor_sub(out=span[width][:], in0=knots[:, width:KNOTS], in1=knots[:, 0 : KNOTS - width])
-    inv_span1 = consts.tile([P, KNOTS - 1], F32)
-    nc.vector.reciprocal(out=inv_span1[:], in_=span[1][:])
-
-    count = BASES + 1
-    up_two = consts.tile([P, count], F32)
-    nc.vector.tensor_mul(out=up_two[:], in0=span[1][:, 0:count], in1=span[2][:, 0:count])
-    inv_up = consts.tile([P, count], F32)
-    nc.vector.tensor_mul(out=inv_up[:], in0=up_two[:], in1=span[3][:, 0:count])
-    up = consts.tile([P, count], F32)
-    nc.vector.reciprocal(out=up[:], in_=inv_up[:])
-    down_two = consts.tile([P, count], F32)
-    nc.vector.tensor_mul(out=down_two[:], in0=span[1][:, 2 : 2 + count], in1=span[2][:, 1 : 1 + count])
-    inv_down = consts.tile([P, count], F32)
-    nc.vector.tensor_mul(out=inv_down[:], in0=down_two[:], in1=span[3][:, 0:count])
-    down = consts.tile([P, count], F32)
-    nc.vector.reciprocal(out=down[:], in_=inv_down[:])
+    def column(tile, j):
+        return tile[:, j : j + 1]
 
     def product(name, first, *others):
         value = first
@@ -96,35 +73,64 @@ def knot_constants(nc, consts, grid):
             value = out[:]
         return value
 
+    knots_bf = consts.tile([P, KNOTS], BF16)
+    nc.sync.dma_start(out=knots_bf[:], in_=grid.partition_broadcast(P))
+    knots = consts.tile([P, KNOTS], F32)
+    nc.vector.tensor_copy(out=knots[:], in_=knots_bf[:])
+
+    ends = consts.tile([P, TENTS], F32)
+    nc.vector.tensor_add(out=ends[:], in0=knots[:, 0:TENTS], in1=knots[:, 8 : 8 + TENTS])
+    span = {}
+    for width in (1, 2, 3, 4, 8):
+        span[width] = consts.tile([P, KNOTS - width], F32, name="span%d" % width)
+        nc.vector.tensor_sub(out=span[width][:], in0=knots[:, width:KNOTS], in1=knots[:, 0 : KNOTS - width])
+    neg_centre = consts.tile([P, TENTS], F32)
+    nc.vector.tensor_scalar_mul(out=neg_centre[:], in0=ends[:], scalar1=-0.5)
+    offset = consts.tile([P, TILES], F32)
+    nc.vector.tensor_scalar_mul(out=offset[:, 0:TENTS], in0=span[8][:], scalar1=0.5)
+    nc.vector.tensor_copy(out=offset[:, TENTS:TILES], in_=knots[:, TENTS:TILES])
+    inv_span1 = consts.tile([P, KNOTS - 1], F32)
+    nc.vector.reciprocal(out=inv_span1[:], in_=span[1][:])
+
+    count = BASES + 1
+    down_two = consts.tile([P, count], F32)
+    nc.vector.tensor_mul(out=down_two[:], in0=span[1][:, 2 : 2 + count], in1=span[2][:, 1 : 1 + count])
+    up_two = consts.tile([P, count], F32)
+    nc.vector.tensor_mul(out=up_two[:], in0=span[1][:, 0:count], in1=span[2][:, 0:count])
+    inv_down = consts.tile([P, count], F32)
+    nc.vector.tensor_mul(out=inv_down[:], in0=down_two[:], in1=span[3][:, 0:count])
+    inv_up = consts.tile([P, count], F32)
+    nc.vector.tensor_mul(out=inv_up[:], in0=up_two[:], in1=span[3][:, 0:count])
+    down = consts.tile([P, count], F32)
+    nc.vector.reciprocal(out=down[:], in_=inv_down[:])
+    up = consts.tile([P, count], F32)
+    nc.vector.reciprocal(out=up[:], in_=inv_up[:])
+
     rise_ratio = product("rise_ratio", span[4][:], inv_span1[:, 0:BASES], inv_up[:, 0:BASES], up[:, 1 : 1 + BASES])
     fall_ratio = product("fall_ratio", span[4][:], inv_span1[:, 3 : 3 + BASES], inv_down[:, 1 : 1 + BASES], down[:, 0:BASES])
-    inv_fall_ratio = consts.tile([P, BASES], F32)
-    nc.vector.reciprocal(out=inv_fall_ratio[:], in_=fall_ratio)
 
     weight = consts.tile([P, 2 * TILES], F32)
-
-    def column(tile, j):
-        return tile[:, j : j + 1]
+    step = product("step", down[:, 1 : 1 + BASES], inv_down[:, 0:BASES])
+    inv_fall_6 = consts.tile([P, 1], F32)
+    nc.vector.reciprocal(out=inv_fall_6[:], in_=column(fall_ratio, 6))
 
     def times(k, value, factor):
         nc.vector.tensor_mul(out=column(weight, k), in0=value, in1=factor)
 
     nc.vector.memset(weight[:, 0:1], 1.0)
-    times(1, column(weight, 0), column(rise_ratio, 0))
-    times(2, column(weight, 1), column(inv_fall_ratio, 6))
-    through = consts.tile([P, 1], F32)
-    nc.vector.tensor_mul(out=through[:], in0=column(weight, 1), in1=column(rise_ratio, 1))
-    times(3, through[:], column(inv_fall_ratio, 7))
-    times(4, column(weight, 3), column(inv_fall_ratio, 0))
-    times(5, column(weight, 4), column(inv_fall_ratio, 1))
-    times(6, column(weight, 5), column(inv_fall_ratio, 2))
-    times(7, column(weight, 6), column(rise_ratio, 6))
+    times(2, column(rise_ratio, 0), inv_fall_6[:])
+    times(1, column(weight, 0), column(step, 8 - 3))
+    times(3, column(weight, 2), column(step, 10 - 3))
+    times(4, column(weight, 3), column(rise_ratio, 3))
+    times(5, column(weight, 4), column(step, 4 - 3))
+    times(6, column(weight, 5), column(rise_ratio, 5))
+    times(7, column(weight, 6), column(step, 6 - 3))
     nc.vector.tensor_copy(out=weight[:, TILES : 2 * TILES], in_=weight[:, 0:TILES])
-    inv_weight = consts.tile([P, 2 * TILES], F32)
-    nc.vector.reciprocal(out=inv_weight[:], in_=weight[:])
 
     root_raw = consts.tile([P, TILES], F32)
     nc.scalar.sqrt(out=root_raw[:], in_=weight[:, 0:TILES])
+    inv_weight = consts.tile([P, 2 * TILES], F32)
+    nc.vector.reciprocal(out=inv_weight[:], in_=weight[:])
     inv_root = consts.tile([P, TILES], F32)
     nc.vector.reciprocal(out=inv_root[:], in_=root_raw[:])
     root_other = consts.tile([P, TILES], F32)
@@ -133,34 +139,26 @@ def knot_constants(nc, consts, grid):
     nc.vector.tensor_add(out=root_sum[:], in0=root_raw[:], in1=root_other[:])
     root = consts.tile([P, TILES], F32)
     nc.vector.tensor_scalar_mul(out=root[:], in0=root_sum[:], scalar1=0.5)
-
-    ends = consts.tile([P, TENTS], F32)
-    nc.vector.tensor_add(out=ends[:], in0=knots[:, 0:TENTS], in1=knots[:, 8 : 8 + TENTS])
-    neg_centre = consts.tile([P, TENTS], F32)
-    nc.vector.tensor_scalar_mul(out=neg_centre[:], in0=ends[:], scalar1=-0.5)
-    offset = consts.tile([P, TILES], F32)
-    nc.vector.tensor_scalar_mul(out=offset[:, 0:TENTS], in0=span[8][:], scalar1=0.5)
-    nc.vector.tensor_copy(out=offset[:, TENTS:TILES], in_=knots[:, TENTS:TILES])
     root_offset = consts.tile([P, TILES], F32)
     nc.vector.tensor_mul(out=root_offset[:], in0=offset[:], in1=root[:])
     bias = consts.tile([P, TILES], F32)
     nc.vector.tensor_scalar_mul(out=bias[:], in0=root_offset[:], scalar1=-1.0)
 
-    drain = {
-        "rise": product("rise_drain", up[:, 0:BASES], inv_weight[:, 0:BASES]),
-        "fall": product("fall_drain", down[:, 1 : 1 + BASES], inv_weight[:, 4 : 4 + BASES]),
-    }
     factor = {
         "rise": product("rise_factor", rise_ratio, weight[:, 0:BASES], inv_weight[:, 1 : 1 + BASES]),
         "fall": product("fall_factor", fall_ratio, weight[:, 4 : 4 + BASES], inv_weight[:, 3 : 3 + BASES]),
     }
+    drain = {
+        "rise": product("rise_drain", up[:, 0:BASES], inv_weight[:, 0:BASES]),
+        "fall": product("fall_drain", down[:, 1 : 1 + BASES], inv_weight[:, 4 : 4 + BASES]),
+    }
     neg_drain = {}
     neg_factor = {}
     for kind in ("rise", "fall"):
-        neg_drain[kind] = consts.tile([P, BASES], F32, name="neg_drain_" + kind)
-        nc.vector.tensor_scalar_mul(out=neg_drain[kind][:], in0=drain[kind], scalar1=-1.0)
         neg_factor[kind] = consts.tile([P, BASES], F32, name="neg_factor_" + kind)
         nc.vector.tensor_scalar_mul(out=neg_factor[kind][:], in0=factor[kind], scalar1=-1.0)
+        neg_drain[kind] = consts.tile([P, BASES], F32, name="neg_drain_" + kind)
+        nc.vector.tensor_scalar_mul(out=neg_drain[kind][:], in0=drain[kind], scalar1=-1.0)
 
     def drain_of(kind, g):
         return column(drain[kind] if drain_is_positive(kind, g) else neg_drain[kind], g)
@@ -198,8 +196,8 @@ def tile_kanblock_pb_kernel(tc, h, grid, w2_base, w2_spline, out):
 
         base_codes = keep.tile([P, CHUNKS, OUTPUTS], U32, align_bytes=64)
         base_scales = keep.tile([P, CHUNKS, OUTPUTS], U8, align_bytes=64)
-        w_codes = keep.tile([P, CHUNKS, BASES, OUTPUTS], U32, align_bytes=64)
-        w_scales = keep.tile([P, CHUNKS, BASES, OUTPUTS], U8, align_bytes=64)
+        w_codes = keep.tile([P, CHUNKS, 2, PAIRS, OUTPUTS], U32, align_bytes=64)
+        w_scales = keep.tile([P, CHUNKS, 2, PAIRS, OUTPUTS], U8, align_bytes=64)
         h_rows = ctx.enter_context(tc.tile_pool(name="h_rows", bufs=1))
         w_rows = ctx.enter_context(tc.tile_pool(name="w_rows", bufs=4))
         w_stage = ctx.enter_context(tc.tile_pool(name="w_stage", bufs=3))
@@ -273,19 +271,19 @@ def tile_kanblock_pb_kernel(tc, h, grid, w2_base, w2_spline, out):
         def copy_spline(step, i):
             for k in range(2):
                 if i == 0:
-                    w_grouped[step, k] = w_stage.tile([P, PAIR, 2 * P, PACK], BF16, align_bytes=64, name="w_grouped", tag="w_grouped")
-                empty(W_TAGS[k], w_grouped[step, k][:, :, i * P : (i + 1) * P, :], turned[k][:].bitcast(BF16).rearrange("p v (d e) -> p e d v", e=PAIR))
+                    w_grouped[step, k] = w_stage.tile([P, 2, 2 * P, PACK], BF16, align_bytes=64, name="w_grouped", tag="w_grouped")
+                words = w_grouped[step, k][:].bitcast(F32)
+                empty(W_TAGS[k], words[:, :, i * P : (i + 1) * P, :], turned[k][:].rearrange("p (m v) d -> p m d v", m=2))
 
         def quantise_spline(step):
             (c, half), q = step
             cols = slice(2 * half * P, 2 * (half + 1) * P)
             for k in range(2):
-                for e in range(PAIR):
-                    g = PAIR * (q + k) + e
+                for m in range(2):
                     nc.vector.quantize_mx(
-                        out=w_codes[:, c, g, cols].bitcast(FP8X4),
-                        scales=w_scales[:, c, g, cols],
-                        in_=w_grouped[step, k][:, e, :, :].rearrange("p d v -> p (d v)"),
+                        out=w_codes[:, c, m, q + k, cols].bitcast(FP8X4),
+                        scales=w_scales[:, c, m, q + k, cols],
+                        in_=w_grouped[step, k][:, m, :, :].rearrange("p d v -> p (d v)"),
                     )
 
         h_sb = {}
@@ -368,8 +366,8 @@ def tile_kanblock_pb_kernel(tc, h, grid, w2_base, w2_spline, out):
             return folded[b, k][:] if k < TENTS else batch_x(b)
 
         def make_square(b, k):
-            tag = "tent" if k < TENTS else "cube"
-            square[b, k] = work.tile([P, K_PASS], F32, name=tag, tag=tag, bufs=TENT_BUFS if k < TENTS else CUBE_BUFS)
+            tag, bufs = ("early_tent", 5) if k < 2 else ("late_tent", 3) if k < TENTS else ("cube", CUBE_BUFS)
+            square[b, k] = work.tile([P, K_PASS], F32, name=tag, tag=tag, bufs=bufs)
             nc.scalar.activation(out=square[b, k][:], in_=argument(b, k), func=ACT.Square, bias=column("bias", k), scale=column("root", k))
 
         def make_tile(b, k):
@@ -386,7 +384,8 @@ def tile_kanblock_pb_kernel(tc, h, grid, w2_base, w2_spline, out):
             if (kind, g) in SHARED:
                 return
             source = tile[b, tail_tile(kind, g)][:]
-            tail[b, kind, g] = work.tile([P, K_PASS], F32, name="tail", tag="tail", bufs=TAIL_BUFS)
+            tag, bufs = ("shared_tail", 2) if (kind, g) == ("rise", 0) else ("tail", TAIL_BUFS)
+            tail[b, kind, g] = work.tile([P, K_PASS], F32, name=tag, tag=tag, bufs=bufs)
             into = tail[b, kind, g][:]
             factor = consts_of["factor_of"](kind, g)
             if (kind, g) in JOINED:
@@ -404,16 +403,16 @@ def tile_kanblock_pb_kernel(tc, h, grid, w2_base, w2_spline, out):
                 )
 
         def sum_up(members, warm=False):
-            for b, q, i, kind, g, tag in members:
-                bank[b, kind, g] = new_bank(tag, [P, PACK, P])
+            for b, tag, key, quarters in members:
+                bank[key] = new_bank(tag, [P, PACK, P])
             if warm and members:
-                b, q, i, kind, g, tag = members[0]
-                nc.tensor.matmul(out=bank[b, kind, g][:, 0, :], lhsT=ident_f32[:], rhs=ident_f32[:], start=True, stop=True)
-            for v in range(PACK):
-                cols = slice(v * P, (v + 1) * P)
+                nc.tensor.matmul(out=bank[members[0][2]][:, 0, :], lhsT=ident_f32[:], rhs=ident_f32[:], start=True, stop=True)
+            for quarter in range(PACK):
                 for part in range(2):
-                    for b, q, i, kind, g, tag in members:
-                        into = bank[b, kind, g][:, v, :]
+                    for b, tag, key, quarters in members:
+                        kind, g, block = quarters[quarter]
+                        cols = slice(block * P, (block + 1) * P)
+                        into = bank[key][:, quarter, :]
                         tail_sb = tail[(b,) + tail_key(kind, g)]
                         lead_sb = tile[b, lead_tile(kind, g)]
                         if (kind, g) in JOINED:
@@ -425,60 +424,70 @@ def tile_kanblock_pb_kernel(tc, h, grid, w2_base, w2_spline, out):
                                 start=(part == 0), stop=(part == 1),
                             )
 
-        def round_sum(b, kind, g):
-            drained[b, g] = work.tile([P, P, PACK], BF16, name="drained", tag="drained", bufs=DRAINED_BUFS)
+        def scalar_member(b, g):
+            return (b, "for_scalar", (b, "rise", g), [("rise", g, v) for v in range(PACK)])
+
+        def vector_member(b, q, m):
+            g = VECTOR_SUMS[q]
+            return (b, "for_vector", (b, q, m), [("fall", g + e, 2 * m + v) for v in range(2) for e in range(PAIR)])
+
+        def round_sum(b, g):
+            pair = g // PAIR
+            if g % PAIR == 0:
+                drained[b, pair] = work.tile([P, PACK, PAIR, P], BF16, name="drained", tag="drained", bufs=DRAINED_BUFS)
             nc.scalar.activation(
-                out=drained[b, g][:], in_=bank[b, kind, g][:].rearrange("p v n -> p n v"),
-                func=ACT.Relu, scale=consts_of["drain_of"](kind, g),
+                out=drained[b, pair][:, :, g % PAIR, :], in_=bank[b, "rise", g][:], func=ACT.Relu, scale=consts_of["drain_of"]("rise", g),
             )
 
-        def finish(b, q, i, kind, g):
-            if i == 0:
-                bases[b, q] = operands.tile([P, 2, P, PACK], BF16, align_bytes=64, name="bases", tag="bases", bufs=3)
+        def finish(b, q, m):
+            g = VECTOR_SUMS[q]
+            if m == 0:
+                bases[b, q] = operands.tile([P, 2, P, PACK], BF16, align_bytes=64, name="bases", tag="bases", bufs=2)
             nc.vector.scalar_tensor_tensor(
-                out=bases[b, q][:, i, :, :], in0=bank[b, kind, g][:].rearrange("p v n -> p n v"),
-                scalar=consts_of["drain_of"](kind, g), in1=drained[b, g][:], op0=ALU.mult, op1=ALU.max,
+                out=bases[b, q][:, m, :, :],
+                in0=bank[b, q, m][:].rearrange("p w n -> p n w"),
+                scalar=consts_of["drain_of"]("fall", g),
+                in1=drained[b, g // PAIR][:, 2 * m : 2 * m + 2, :, :].rearrange("p v e n -> p n (v e)"),
+                op0=ALU.mult, op1=ALU.max,
             )
 
         def take_out(members):
-            for b, q, i, kind, g, tag in members:
+            for b, tag, key, quarters in members:
                 if tag == "for_scalar":
-                    round_sum(b, kind, g)
+                    round_sum(b, key[2])
                 else:
-                    finish(b, q, i, kind, g)
+                    finish(*key)
 
         def quantise_bases(b, q):
             b_codes[b, q] = operands.tile([P, 2, P], U32, align_bytes=64, name="b_codes", tag="b_codes")
             b_scales[b, q] = operands.tile([P, 2, P], U8, align_bytes=64, name="b_scales", tag="b_scales")
             nc.vector.quantize_mx(
-                out=b_codes[b, q][:].rearrange("p i n -> p (i n)").bitcast(FP8X4),
-                scales=b_scales[b, q][:].rearrange("p i n -> p (i n)"),
-                in_=bases[b, q][:].rearrange("p i n v -> p (i n v)"),
+                out=b_codes[b, q][:].rearrange("p m n -> p (m n)").bitcast(FP8X4),
+                scales=b_scales[b, q][:].rearrange("p m n -> p (m n)"),
+                in_=bases[b, q][:].rearrange("p m n v -> p (m n v)"),
             )
 
         def multiply(b, q):
             tt, c = b // CHUNKS, b % CHUNKS
-            for i in range(2):
-                g = VECTOR_SUMS[q][i][1]
-                first = c == 0 and q == FIRST_VECTOR and i == 0
+            for m in range(2):
+                first = c == 0 and q == FIRST_VECTOR and m == 0
                 if first:
                     acc[tt] = sums.tile([P, OUTPUTS], F32, name="acc", tag="acc")
                 nc.tensor.matmul_mx(
                     out=acc[tt][:],
-                    lhsT=b_codes[b, q][:, i, :].bitcast(FP8X4),
-                    lhsT_scale=b_scales[b, q][:, i, :],
-                    rhs=w_codes[:, c, g, :].bitcast(FP8X4),
-                    rhs_scale=w_scales[:, c, g, :],
+                    lhsT=b_codes[b, q][:, m, :].bitcast(FP8X4),
+                    lhsT_scale=b_scales[b, q][:, m, :],
+                    rhs=w_codes[:, c, m, VECTOR_SUMS[q] // PAIR, :].bitcast(FP8X4),
+                    rhs_scale=w_scales[:, c, m, VECTOR_SUMS[q] // PAIR, :],
                     start=first,
-                    stop=(c == CHUNKS - 1 and q == LAST - 1 and i == 1),
+                    stop=(c == CHUNKS - 1 and q == LAST - 1 and m == 1),
                 )
 
-        TENT_BUFS = 7
-        CUBE_BUFS = 8
-        TAIL_BUFS = 9
-        DRAINED_BUFS = 10
+        CUBE_BUFS = 6
+        TAIL_BUFS = 8
+        DRAINED_BUFS = 5
         FIRST_VECTOR = 4
-        SHARED = {("fall", 6): ("rise", 0), ("fall", 7): ("rise", 1)}
+        SHARED = {("fall", 6): ("rise", 0)}
 
         units = [(c, half) for c in range(CHUNKS) for half in range(2)]
         load(0)
@@ -502,11 +511,11 @@ def tile_kanblock_pb_kernel(tc, h, grid, w2_base, w2_spline, out):
                 for b, q in live:
                     for i in range(2):
                         if q in SCALAR_SUMS:
-                            sums_of[i].append((b, q, i) + SCALAR_SUMS[q][i] + ("for_scalar",))
+                            sums_of[i].append(scalar_member(b, SCALAR_SUMS[q][i]))
                 for b, q in live:
                     for i in range(2):
                         if q in VECTOR_SUMS:
-                            sums_of[i].append((b, q, i) + VECTOR_SUMS[q][i] + ("for_vector",))
+                            sums_of[i].append(vector_member(b, q, i))
                 squares = [(b, q + 1) for b, q in live if 0 <= q + 1 < STRIDE]
                 take_out(late)
                 if before:
@@ -525,8 +534,11 @@ def tile_kanblock_pb_kernel(tc, h, grid, w2_base, w2_spline, out):
                     make_square(b, k + TENTS)
                     make_square(b, k)
                 for b, q in live:
-                    for kind, g in SCALAR_SUMS.get(q + 1, ()) + VECTOR_SUMS.get(q + 1, ()):
-                        make_tail(b, kind, g)
+                    for g in SCALAR_SUMS.get(q + 1, ()):
+                        make_tail(b, "rise", g)
+                    if q + 1 in VECTOR_SUMS:
+                        for e in range(PAIR):
+                            make_tail(b, "fall", VECTOR_SUMS[q + 1] + e)
                 sum_up(sums_of[0])
                 if now:
                     turn_spline(now, 0)

@@ -36,7 +36,7 @@ SCALAR_SUMS = {2: (0, 4), 3: (1, 5), 4: (6, 7), 5: (2, 3)}
 VECTOR_SUMS = {4: 0, 5: 6, 6: 2, 7: 4}
 LAST = 8
 JOINED = (("rise", 3), ("rise", 5))
-SCALAR_TAILS = (("rise", 1), ("rise", 2), ("fall", 1), ("fall", 4), ("fall", 2))
+SCALAR_TAILS = (("rise", 1), ("rise", 2), ("fall", 1), ("fall", 4))
 
 
 def lead_tile(kind, g):
@@ -273,7 +273,7 @@ def tile_kanblock_pb_kernel(tc, h, grid, w2_base, w2_spline, out):
                 if i == 0:
                     w_grouped[step, k] = w_stage.tile([P, 2, 2 * P, PACK], BF16, align_bytes=64, name="w_grouped", tag="w_grouped")
                 words = w_grouped[step, k][:].bitcast(F32)
-                empty(W_TAGS[k], words[:, :, i * P : (i + 1) * P, :], turned[k][:].rearrange("p (m v) d -> p m d v", m=2))
+                empty(W_TAGS[1] if k == 1 and i == 1 else W_TAGS[0], words[:, :, i * P : (i + 1) * P, :], turned[k][:].rearrange("p (m v) d -> p m d v", m=2))
 
         def quantise_spline(step):
             (c, half), q = step
@@ -402,11 +402,9 @@ def tile_kanblock_pb_kernel(tc, h, grid, w2_base, w2_spline, out):
                     op0=ALU.mult, op1=ALU.min if lead_is_positive(kind, g) else ALU.max,
                 )
 
-        def sum_up(members, warm=False):
+        def sum_up(members):
             for b, tag, key, quarters in members:
                 bank[key] = new_bank(tag, [P, PACK, P])
-            if warm and members:
-                nc.tensor.matmul(out=bank[members[0][2]][:, 0, :], lhsT=ident_f32[:], rhs=ident_f32[:], start=True, stop=True)
             for quarter in range(PACK):
                 for part in range(2):
                     for b, tag, key, quarters in members:
@@ -547,7 +545,7 @@ def tile_kanblock_pb_kernel(tc, h, grid, w2_base, w2_spline, out):
                     quantise_spline(before)
                 if now:
                     copy_spline(now, 0)
-                sum_up(sums_of[1], warm=True)
+                sum_up(sums_of[1])
                 late = sums_of[1]
                 if now:
                     turn_spline(now, 1)

@@ -35,8 +35,8 @@ FLOPS = 2 * TOKENS * OUTPUTS * (FEATURES + FEATURES * BASES)
 SCALAR_SUMS = {2: (0, 4), 3: (1, 5), 4: (6, 7), 5: (2, 3)}
 VECTOR_SUMS = {4: 0, 5: 6, 6: 2, 7: 4}
 LAST = 8
-JOINED = (("rise", 3), ("rise", 5))
-SCALAR_TAILS = (("rise", 1), ("rise", 2), ("fall", 1), ("fall", 4))
+JOINED = ()
+SCALAR_TAILS = (("rise", 1), ("rise", 2), ("fall", 1), ("fall", 4), ("fall", 2))
 
 
 def lead_tile(kind, g):
@@ -61,9 +61,32 @@ def drain_is_positive(kind, g):
     return lead_is_positive(kind, g)
 
 
-def knot_constants(nc, consts, grid):
-    def column(tile, j):
-        return tile[:, j : j + 1]
+def column(tile, j):
+    return tile[:, j : j + 1]
+
+
+def first_constants(nc, consts, grid):
+    knots_bf = consts.tile([P, KNOTS], BF16)
+    nc.sync.dma_start(out=knots_bf[:], in_=grid.partition_broadcast(P))
+    knots = consts.tile([P, KNOTS], F32)
+    nc.vector.tensor_copy(out=knots[:], in_=knots_bf[:])
+
+    ends = consts.tile([P, TENTS], F32)
+    nc.vector.tensor_add(out=ends[:], in0=knots[:, 0:TENTS], in1=knots[:, 8 : 8 + TENTS])
+    width8 = consts.tile([P, TENTS], F32)
+    nc.vector.tensor_sub(out=width8[:], in0=knots[:, 8 : 8 + TENTS], in1=knots[:, 0:TENTS])
+    neg_centre = consts.tile([P, TENTS], F32)
+    nc.vector.tensor_scalar_mul(out=neg_centre[:], in0=ends[:], scalar1=-0.5)
+    offset = consts.tile([P, TILES], F32)
+    nc.vector.tensor_scalar_mul(out=offset[:, 0:TENTS], in0=width8[:], scalar1=0.5)
+    nc.vector.tensor_copy(out=offset[:, TENTS:TILES], in_=knots[:, TENTS:TILES])
+    neg_offset = consts.tile([P, TILES], F32)
+    nc.vector.tensor_scalar_mul(out=neg_offset[:], in0=offset[:], scalar1=-1.0)
+    return {"knots": knots, "neg_centre": neg_centre, "offset": offset, "neg_offset": neg_offset}
+
+
+def add_other_constants(nc, consts, consts_of):
+    knots = consts_of["knots"]
 
     def product(name, first, *others):
         value = first
@@ -73,22 +96,10 @@ def knot_constants(nc, consts, grid):
             value = out[:]
         return value
 
-    knots_bf = consts.tile([P, KNOTS], BF16)
-    nc.sync.dma_start(out=knots_bf[:], in_=grid.partition_broadcast(P))
-    knots = consts.tile([P, KNOTS], F32)
-    nc.vector.tensor_copy(out=knots[:], in_=knots_bf[:])
-
-    ends = consts.tile([P, TENTS], F32)
-    nc.vector.tensor_add(out=ends[:], in0=knots[:, 0:TENTS], in1=knots[:, 8 : 8 + TENTS])
     span = {}
-    for width in (1, 2, 3, 4, 8):
+    for width in (1, 2, 3, 4):
         span[width] = consts.tile([P, KNOTS - width], F32, name="span%d" % width)
         nc.vector.tensor_sub(out=span[width][:], in0=knots[:, width:KNOTS], in1=knots[:, 0 : KNOTS - width])
-    neg_centre = consts.tile([P, TENTS], F32)
-    nc.vector.tensor_scalar_mul(out=neg_centre[:], in0=ends[:], scalar1=-0.5)
-    offset = consts.tile([P, TILES], F32)
-    nc.vector.tensor_scalar_mul(out=offset[:, 0:TENTS], in0=span[8][:], scalar1=0.5)
-    nc.vector.tensor_copy(out=offset[:, TENTS:TILES], in_=knots[:, TENTS:TILES])
     inv_span1 = consts.tile([P, KNOTS - 1], F32)
     nc.vector.reciprocal(out=inv_span1[:], in_=span[1][:])
 
@@ -121,9 +132,9 @@ def knot_constants(nc, consts, grid):
     times(2, column(rise_ratio, 0), inv_fall_6[:])
     times(1, column(weight, 0), column(step, 8 - 3))
     times(3, column(weight, 2), column(step, 10 - 3))
-    times(4, column(weight, 3), column(rise_ratio, 3))
+    nc.vector.memset(weight[:, 4:5], 1.0)
+    nc.vector.memset(weight[:, 6:7], 1.0)
     times(5, column(weight, 4), column(step, 4 - 3))
-    times(6, column(weight, 5), column(rise_ratio, 5))
     times(7, column(weight, 6), column(step, 6 - 3))
     nc.vector.tensor_copy(out=weight[:, TILES : 2 * TILES], in_=weight[:, 0:TILES])
 
@@ -139,10 +150,8 @@ def knot_constants(nc, consts, grid):
     nc.vector.tensor_add(out=root_sum[:], in0=root_raw[:], in1=root_other[:])
     root = consts.tile([P, TILES], F32)
     nc.vector.tensor_scalar_mul(out=root[:], in0=root_sum[:], scalar1=0.5)
-    root_offset = consts.tile([P, TILES], F32)
-    nc.vector.tensor_mul(out=root_offset[:], in0=offset[:], in1=root[:])
     bias = consts.tile([P, TILES], F32)
-    nc.vector.tensor_scalar_mul(out=bias[:], in0=root_offset[:], scalar1=-1.0)
+    nc.vector.tensor_mul(out=bias[:], in0=consts_of["neg_offset"][:], in1=root[:])
 
     factor = {
         "rise": product("rise_factor", rise_ratio, weight[:, 0:BASES], inv_weight[:, 1 : 1 + BASES]),
@@ -167,15 +176,10 @@ def knot_constants(nc, consts, grid):
         positive = tail_is_positive(kind, g) != lead_is_positive(kind, g)
         return column(factor[kind] if positive else neg_factor[kind], g)
 
-    return {
-        "knots": knots,
-        "neg_centre": neg_centre,
-        "offset": offset,
-        "bias": bias,
-        "root": root,
-        "drain_of": drain_of,
-        "factor_of": factor_of,
-    }
+    consts_of["bias"] = bias
+    consts_of["root"] = root
+    consts_of["drain_of"] = drain_of
+    consts_of["factor_of"] = factor_of
 
 
 def tile_kanblock_pb_kernel(tc, h, grid, w2_base, w2_spline, out):
@@ -192,7 +196,6 @@ def tile_kanblock_pb_kernel(tc, h, grid, w2_base, w2_spline, out):
 
         ident_f32 = consts.tile([P, P], F32)
         masks.make_identity(nc, ident_f32[:])
-        consts_of = knot_constants(nc, consts, grid)
 
         base_codes = keep.tile([P, CHUNKS, OUTPUTS], U32, align_bytes=64)
         base_scales = keep.tile([P, CHUNKS, OUTPUTS], U8, align_bytes=64)
@@ -355,12 +358,9 @@ def tile_kanblock_pb_kernel(tc, h, grid, w2_base, w2_spline, out):
             first = (b % CHUNKS) * K_PASS
             return x[b // CHUNKS][:, first : first + K_PASS]
 
-        def column(name, k):
-            return consts_of[name][:, k : k + 1]
-
         def fold(b, k):
             folded[b, k] = work.tile([P, K_PASS], F32, name="folded", tag="folded", bufs=2)
-            nc.scalar.activation(out=folded[b, k][:], in_=batch_x(b), func=ACT.Abs, bias=column("neg_centre", k), scale=1.0)
+            nc.scalar.activation(out=folded[b, k][:], in_=batch_x(b), func=ACT.Abs, bias=column(consts_of["neg_centre"], k), scale=1.0)
 
         def argument(b, k):
             return folded[b, k][:] if k < TENTS else batch_x(b)
@@ -368,12 +368,16 @@ def tile_kanblock_pb_kernel(tc, h, grid, w2_base, w2_spline, out):
         def make_square(b, k):
             tag, bufs = ("early_tent", 5) if k < 2 else ("late_tent", 3) if k < TENTS else ("cube", CUBE_BUFS)
             square[b, k] = work.tile([P, K_PASS], F32, name=tag, tag=tag, bufs=bufs)
-            nc.scalar.activation(out=square[b, k][:], in_=argument(b, k), func=ACT.Square, bias=column("bias", k), scale=column("root", k))
+            if k in UNWEIGHTED:
+                bias, scale = column(consts_of["neg_offset"], k), 1.0
+            else:
+                bias, scale = column(consts_of["bias"], k), column(consts_of["root"], k)
+            nc.scalar.activation(out=square[b, k][:], in_=argument(b, k), func=ACT.Square, bias=bias, scale=scale)
 
         def make_tile(b, k):
             tile[b, k] = square[b, k]
             nc.vector.scalar_tensor_tensor(
-                out=tile[b, k][:], in0=argument(b, k), scalar=column("offset", k), in1=square[b, k][:],
+                out=tile[b, k][:], in0=argument(b, k), scalar=column(consts_of["offset"], k), in1=square[b, k][:],
                 op0=ALU.subtract, op1=ALU.mult,
             )
 
@@ -481,6 +485,7 @@ def tile_kanblock_pb_kernel(tc, h, grid, w2_base, w2_spline, out):
                     stop=(c == CHUNKS - 1 and q == LAST - 1 and m == 1),
                 )
 
+        UNWEIGHTED = (0, 4, 6)
         CUBE_BUFS = 6
         TAIL_BUFS = 8
         DRAINED_BUFS = 5
@@ -488,18 +493,19 @@ def tile_kanblock_pb_kernel(tc, h, grid, w2_base, w2_spline, out):
         SHARED = {("fall", 6): ("rise", 0)}
 
         units = [(c, half) for c in range(CHUNKS) for half in range(2)]
-        load(0)
         steps = [(unit, q) for unit in units for q in range(0, PAIRS, 2)]
-        load_spline(units[0])
-        load_spline(units[1])
 
         with tc.manual_schedule():
+            consts_of = first_constants(nc, consts, grid)
+            load(0)
+            load_spline(units[0])
+            load_spline(units[1])
             late = []
             for slot in range(-1, STRIDE * (BATCH_COUNT - 1) + LAST + 5):
                 live = [(b, slot - STRIDE * b) for b in range(BATCH_COUNT)]
                 ages = [(tt, slot - TILE_SLOTS * tt) for tt in range(TOKEN_TILES)]
-                now = steps[slot] if 0 <= slot < len(steps) else None
-                before = steps[slot - 1] if 0 < slot <= len(steps) else None
+                now = steps[slot + 1] if slot + 1 < len(steps) else None
+                before = steps[slot] if 0 <= slot < len(steps) else None
                 for tt, age in ages:
                     if age == -1:
                         clamp(tt)
@@ -545,11 +551,13 @@ def tile_kanblock_pb_kernel(tc, h, grid, w2_base, w2_spline, out):
                     quantise_spline(before)
                 if now:
                     copy_spline(now, 0)
+                if slot == -1:
+                    add_other_constants(nc, consts, consts_of)
                 sum_up(sums_of[1])
                 late = sums_of[1]
                 if now:
                     turn_spline(now, 1)
-                    if slot % 2 == 1:
+                    if slot % 2 == 0:
                         u = slot // 2 + 2
                         if u < len(units):
                             load_spline(units[u])

@@ -13,30 +13,47 @@ ACT = mybir.ActivationFunctionType
 
 P = 128
 PACK = 4
-K_PASS = P * PACK
 TOKENS = 512
 FEATURES = 2048
 OUTPUTS = 512
 BASES = 8
 KNOTS = 12
-TILES = 8
-TENTS = 4
-TOKEN_TILES = TOKENS // P
-OUTPUT_TILES = OUTPUTS // P
-CHUNKS = FEATURES // K_PASS
 PAIR = 2
 PAIRS = BASES // PAIR
-BATCH_COUNT = TOKEN_TILES * CHUNKS
-TILE_SLOTS = 4 * CHUNKS
+TOKEN_TILES = TOKENS // P
+OUTPUT_TILES = OUTPUTS // P
+CHUNK = P * PACK
+CHUNKS = FEATURES // CHUNK
+HALVES = 2
+TILES = 8
+TENTS = 4
+
+TILES_AT_ONCE = 2
+ROUND = TILES_AT_ONCE * CHUNKS
+BATCHES = TOKEN_TILES * CHUNKS
 STRIDE = 4
+ROUND_SLOTS = STRIDE * ROUND
+SUMS_OF_RISES = {2: (0, 4), 3: (1, 5), 4: (2, 6), 5: (3, 7)}
+SUMS_OF_FALLS = {4: 0, 5: 4, 6: 2, 7: 6}
+MULTIPLY_AFTER = 2
+FIRST_PASS = min(SUMS_OF_FALLS) + MULTIPLY_AFTER
+LAST_PASS = max(SUMS_OF_FALLS) + MULTIPLY_AFTER
+PAIR_ORDER = [SUMS_OF_FALLS[q] // PAIR for q in sorted(SUMS_OF_FALLS)]
+
+SHARED_BY_BOTH = ("rise", 0)
+SHARED_TAIL = {("fall", 6): SHARED_BY_BOTH}
+TAILS_BY_SCALAR = (("rise", 0), ("rise", 1), ("rise", 2), ("rise", 3))
 
 FLOPS = 2 * TOKENS * OUTPUTS * (FEATURES + FEATURES * BASES)
 
-SCALAR_SUMS = {2: (0, 4), 3: (1, 5), 4: (6, 7), 5: (2, 3)}
-VECTOR_SUMS = {4: 0, 5: 6, 6: 2, 7: 4}
-LAST = 8
-JOINED = ()
-SCALAR_TAILS = (("rise", 1), ("rise", 2), ("fall", 1), ("fall", 4), ("fall", 2))
+
+def batch_place(b):
+    within = b % ROUND
+    return b // ROUND * TILES_AT_ONCE + within % TILES_AT_ONCE, within // TILES_AT_ONCE
+
+
+def batch_number(tt, c):
+    return tt // TILES_AT_ONCE * ROUND + c * TILES_AT_ONCE + tt % TILES_AT_ONCE
 
 
 def lead_tile(kind, g):
@@ -51,14 +68,8 @@ def lead_is_positive(kind, g):
     return kind == "rise" and g >= TENTS
 
 
-def tail_is_positive(kind, g):
+def tail_keeps_positive(kind, g):
     return g >= 3 if kind == "rise" else g == 0
-
-
-def drain_is_positive(kind, g):
-    if (kind, g) in JOINED:
-        return not tail_is_positive(kind, g)
-    return lead_is_positive(kind, g)
 
 
 def column(tile, j):
@@ -70,34 +81,33 @@ def first_constants(nc, consts, grid):
     nc.sync.dma_start(out=knots_bf[:], in_=grid.partition_broadcast(P))
     knots = consts.tile([P, KNOTS], F32)
     nc.vector.tensor_copy(out=knots[:], in_=knots_bf[:])
-
     ends = consts.tile([P, TENTS], F32)
     nc.vector.tensor_add(out=ends[:], in0=knots[:, 0:TENTS], in1=knots[:, 8 : 8 + TENTS])
-    width8 = consts.tile([P, TENTS], F32)
-    nc.vector.tensor_sub(out=width8[:], in0=knots[:, 8 : 8 + TENTS], in1=knots[:, 0:TENTS])
+    width = consts.tile([P, TENTS], F32)
+    nc.vector.tensor_sub(out=width[:], in0=knots[:, 8 : 8 + TENTS], in1=knots[:, 0:TENTS])
     neg_centre = consts.tile([P, TENTS], F32)
     nc.vector.tensor_scalar_mul(out=neg_centre[:], in0=ends[:], scalar1=-0.5)
     offset = consts.tile([P, TILES], F32)
-    nc.vector.tensor_scalar_mul(out=offset[:, 0:TENTS], in0=width8[:], scalar1=0.5)
+    nc.vector.tensor_scalar_mul(out=offset[:, 0:TENTS], in0=width[:], scalar1=0.5)
     nc.vector.tensor_copy(out=offset[:, TENTS:TILES], in_=knots[:, TENTS:TILES])
     neg_offset = consts.tile([P, TILES], F32)
     nc.vector.tensor_scalar_mul(out=neg_offset[:], in0=offset[:], scalar1=-1.0)
     return {"knots": knots, "neg_centre": neg_centre, "offset": offset, "neg_offset": neg_offset}
 
 
-def add_other_constants(nc, consts, consts_of):
-    knots = consts_of["knots"]
+def other_constants(nc, consts, first):
+    knots = first["knots"]
 
-    def product(name, first, *others):
-        value = first
-        for i in range(len(others)):
+    def product(name, *factors):
+        value = factors[0]
+        for i in range(1, len(factors)):
             out = consts.tile([P, BASES], F32, name="%s_%d" % (name, i))
-            nc.vector.tensor_mul(out=out[:], in0=value, in1=others[i])
+            nc.vector.tensor_mul(out=out[:], in0=value, in1=factors[i])
             value = out[:]
         return value
 
     span = {}
-    for width in (1, 2, 3, 4):
+    for width in range(1, 5):
         span[width] = consts.tile([P, KNOTS - width], F32, name="span%d" % width)
         nc.vector.tensor_sub(out=span[width][:], in0=knots[:, width:KNOTS], in1=knots[:, 0 : KNOTS - width])
     inv_span1 = consts.tile([P, KNOTS - 1], F32)
@@ -125,17 +135,16 @@ def add_other_constants(nc, consts, consts_of):
     inv_fall_6 = consts.tile([P, 1], F32)
     nc.vector.reciprocal(out=inv_fall_6[:], in_=column(fall_ratio, 6))
 
-    def times(k, value, factor):
+    def weigh(k, value, factor):
         nc.vector.tensor_mul(out=column(weight, k), in0=value, in1=factor)
 
-    nc.vector.memset(weight[:, 0:1], 1.0)
-    times(2, column(rise_ratio, 0), inv_fall_6[:])
-    times(1, column(weight, 0), column(step, 8 - 3))
-    times(3, column(weight, 2), column(step, 10 - 3))
-    nc.vector.memset(weight[:, 4:5], 1.0)
-    nc.vector.memset(weight[:, 6:7], 1.0)
-    times(5, column(weight, 4), column(step, 4 - 3))
-    times(7, column(weight, 6), column(step, 6 - 3))
+    for k in (0, 4, 6):
+        nc.vector.memset(column(weight, k), 1.0)
+    weigh(2, column(rise_ratio, 0), inv_fall_6[:])
+    for k in (0, 2):
+        weigh(k + 1, column(weight, k), column(step, k + 8 - 3))
+    for k in (4, 6):
+        weigh(k + 1, column(weight, k), column(step, k - 3))
     nc.vector.tensor_copy(out=weight[:, TILES : 2 * TILES], in_=weight[:, 0:TILES])
 
     root_raw = consts.tile([P, TILES], F32)
@@ -151,35 +160,30 @@ def add_other_constants(nc, consts, consts_of):
     root = consts.tile([P, TILES], F32)
     nc.vector.tensor_scalar_mul(out=root[:], in0=root_sum[:], scalar1=0.5)
     bias = consts.tile([P, TILES], F32)
-    nc.vector.tensor_mul(out=bias[:], in0=consts_of["neg_offset"][:], in1=root[:])
+    nc.vector.tensor_mul(out=bias[:], in0=first["neg_offset"][:], in1=root[:])
 
     factor = {
         "rise": product("rise_factor", rise_ratio, weight[:, 0:BASES], inv_weight[:, 1 : 1 + BASES]),
         "fall": product("fall_factor", fall_ratio, weight[:, 4 : 4 + BASES], inv_weight[:, 3 : 3 + BASES]),
     }
-    drain = {
-        "rise": product("rise_drain", up[:, 0:BASES], inv_weight[:, 0:BASES]),
-        "fall": product("fall_drain", down[:, 1 : 1 + BASES], inv_weight[:, 4 : 4 + BASES]),
+    scale = {
+        "rise": product("rise_scale", up[:, 0:BASES], inv_weight[:, 0:BASES]),
+        "fall": product("fall_scale", down[:, 1 : 1 + BASES], inv_weight[:, 4 : 4 + BASES]),
     }
-    neg_drain = {}
-    neg_factor = {}
+    negative = {}
     for kind in ("rise", "fall"):
-        neg_factor[kind] = consts.tile([P, BASES], F32, name="neg_factor_" + kind)
-        nc.vector.tensor_scalar_mul(out=neg_factor[kind][:], in0=factor[kind], scalar1=-1.0)
-        neg_drain[kind] = consts.tile([P, BASES], F32, name="neg_drain_" + kind)
-        nc.vector.tensor_scalar_mul(out=neg_drain[kind][:], in0=drain[kind], scalar1=-1.0)
-
-    def drain_of(kind, g):
-        return column(drain[kind] if drain_is_positive(kind, g) else neg_drain[kind], g)
+        for name, value in (("factor", factor[kind]), ("scale", scale[kind])):
+            negative[name, kind] = consts.tile([P, BASES], F32, name="neg_%s_%s" % (name, kind))
+            nc.vector.tensor_scalar_mul(out=negative[name, kind][:], in0=value, scalar1=-1.0)
 
     def factor_of(kind, g):
-        positive = tail_is_positive(kind, g) != lead_is_positive(kind, g)
-        return column(factor[kind] if positive else neg_factor[kind], g)
+        positive = tail_keeps_positive(kind, g) != lead_is_positive(kind, g)
+        return column(factor[kind] if positive else negative["factor", kind], g)
 
-    consts_of["bias"] = bias
-    consts_of["root"] = root
-    consts_of["drain_of"] = drain_of
-    consts_of["factor_of"] = factor_of
+    def scale_of(kind, g):
+        return column(scale[kind] if lead_is_positive(kind, g) else negative["scale", kind], g)
+
+    return {"root": root, "bias": bias, "factor_of": factor_of, "scale_of": scale_of}
 
 
 def tile_kanblock_pb_kernel(tc, h, grid, w2_base, w2_spline, out):
@@ -190,56 +194,98 @@ def tile_kanblock_pb_kernel(tc, h, grid, w2_base, w2_spline, out):
     with ExitStack() as ctx:
         consts = ctx.enter_context(tc.tile_pool(name="consts", bufs=1))
         keep = ctx.enter_context(tc.tile_pool(name="keep", bufs=1))
-        sums = ctx.enter_context(tc.psum_pool(name="sums", bufs=1))
-        banks = ctx.enter_context(tc.psum_pool(name="banks", bufs=1))
-        BANKS = {"for_scalar": 3, "for_vector": 2, "weights_by_scalar": 1, "weights_by_vector": 1}
-
-        ident_f32 = consts.tile([P, P], F32)
-        masks.make_identity(nc, ident_f32[:])
-
-        base_codes = keep.tile([P, CHUNKS, OUTPUTS], U32, align_bytes=64)
-        base_scales = keep.tile([P, CHUNKS, OUTPUTS], U8, align_bytes=64)
-        w_codes = keep.tile([P, CHUNKS, 2, PAIRS, OUTPUTS], U32, align_bytes=64)
-        w_scales = keep.tile([P, CHUNKS, 2, PAIRS, OUTPUTS], U8, align_bytes=64)
-        h_rows = ctx.enter_context(tc.tile_pool(name="h_rows", bufs=1))
         w_rows = ctx.enter_context(tc.tile_pool(name="w_rows", bufs=4))
-        w_stage = ctx.enter_context(tc.tile_pool(name="w_stage", bufs=3))
         rows = ctx.enter_context(tc.tile_pool(name="rows", bufs=1))
         work = ctx.enter_context(tc.tile_pool(name="work", bufs=1))
         operands = ctx.enter_context(tc.tile_pool(name="operands", bufs=4))
+        sums = ctx.enter_context(tc.psum_pool(name="sums", bufs=TILES_AT_ONCE))
+        rise_banks = ctx.enter_context(tc.psum_pool(name="rise_banks", bufs=2))
+        fall_banks = ctx.enter_context(tc.psum_pool(name="fall_banks", bufs=2))
+        turn_banks = ctx.enter_context(tc.psum_pool(name="turn_banks", bufs=2))
 
-        def new_bank(tag, shape, dtype=F32):
-            return banks.tile(shape, dtype, name="bank", tag=tag, bufs=BANKS[tag])
+        ident = consts.tile([P, P], F32)
+        masks.make_identity(nc, ident[:])
+        base_codes = keep.tile([P, CHUNKS, OUTPUTS], U32, align_bytes=64)
+        base_scales = keep.tile([P, CHUNKS, OUTPUTS], U8, align_bytes=64)
+        w_codes = keep.tile([P, CHUNKS, HALVES, PAIRS, OUTPUTS], U32, align_bytes=64)
+        w_scales = keep.tile([P, CHUNKS, HALVES, PAIRS, OUTPUTS], U8, align_bytes=64)
 
-        def empty(tag, out, in_):
-            if tag == "weights_by_scalar":
-                nc.scalar.copy(out=out, in_=in_)
-            else:
+        constant = {}
+        w_sb = {}
+        w_grouped = {}
+        base_sb = {}
+        unquantised = {}
+        grouped = {}
+        silu_codes = {}
+        silu_scales = {}
+        h_sb = {}
+        x = {}
+        acc = {}
+        folded = {}
+        square = {}
+        tile = {}
+        tail = {}
+        bank = {}
+        risen = {}
+        bases = {}
+        b_codes = {}
+        b_scales = {}
+
+        def take_out(out, in_, by_vector):
+            if by_vector:
                 nc.vector.tensor_copy(out=out, in_=in_)
+            else:
+                nc.scalar.copy(out=out, in_=in_)
 
-        def pairs_to_partitions(rows_sb, first_chunk, grouped, tag):
+        def load_spline(unit):
+            c, half = unit
+            row_len = CHUNK * BASES
+            for dt in (2 * half, 2 * half + 1):
+                w_sb[c, dt] = w_rows.tile([P, row_len], BF16, name="w_sb", tag="w_sb")
+                nc.sync.dma_start(out=w_sb[c, dt][:], in_=spline_rows[:, dt, c * row_len : (c + 1) * row_len])
+
+        def turn_spline(step, part):
+            (c, half), q = step
+            words = w_sb[c, 2 * half + part][:].bitcast(F32).rearrange("p (v i q) -> p v i q", v=PACK, q=PAIRS)
+            bank["spline"] = turn_banks.tile([P, PACK, P], F32, name="turned", tag="turned")
+            for v in range(PACK):
+                nc.tensor.transpose(bank["spline"][:, v, :], words[:, v, :, q], ident[:])
+
+        def copy_spline(step, part):
+            if part == 0:
+                w_grouped[step] = w_rows.tile([P, HALVES, 2 * P, PACK], BF16, align_bytes=64, name="w_grouped", tag="w_grouped", bufs=2)
+            take_out(
+                w_grouped[step][:].bitcast(F32)[:, :, part * P : (part + 1) * P, :],
+                bank["spline"][:].rearrange("p (m v) d -> p m d v", m=HALVES),
+                by_vector=part == 1 and q % 2 == 0,
+            )
+
+        def quantise_spline(step):
+            (c, half), q = step
+            cols = slice(2 * half * P, 2 * (half + 1) * P)
+            for m in range(HALVES):
+                nc.vector.quantize_mx(
+                    out=w_codes[:, c, m, q, cols].bitcast(FP8X4),
+                    scales=w_scales[:, c, m, q, cols],
+                    in_=w_grouped[step][:, m, :, :].rearrange("p d v -> p (d v)"),
+                )
+
+        def turn_words(key, rows_sb, part):
+            if part == 0:
+                grouped[key] = rows.tile([P, CHUNKS, P, PACK], BF16, align_bytes=64, name="grouped", tag="grouped")
             words = rows_sb[:].bitcast(F32)
-            turned = new_bank(tag, [P, 2, PAIR, P])
+            chunks = slice(2 * part, 2 * part + 2)
+            turned = turn_banks.tile([P, 2, PAIR, P], F32, name="turned", tag="turned")
             for cc in range(2):
                 for u in range(PAIR):
-                    first = ((first_chunk + cc) * PAIR + u) * P
-                    nc.tensor.transpose(turned[:, cc, u, :], words[:, first : first + P], ident_f32[:])
-            empty(tag, grouped[:, first_chunk : first_chunk + 2, :, :], turned[:].rearrange("p c u r -> p c r u"))
-
-        base_sb = {}
-        base_grouped = {}
+                    start = ((2 * part + cc) * PAIR + u) * P
+                    nc.tensor.transpose(turned[:, cc, u, :], words[:, start : start + P], ident[:])
+            take_out(grouped[key][:].bitcast(F32)[:, chunks, :, :], turned[:].rearrange("p c u r -> p c r u"), by_vector=part == 1)
 
         def load_base(half):
-            for i in range(2):
-                dt = 2 * half + i
+            for dt in (2 * half, 2 * half + 1):
                 base_sb[dt] = w_rows.tile([P, FEATURES], BF16, name="w_sb", tag="w_sb")
                 nc.sync.dma_start(out=base_sb[dt][:], in_=w2_base[dt * P : (dt + 1) * P, :])
-
-        def turn_base(dt):
-            base_grouped[dt] = rows.tile([P, CHUNKS, P, PACK], BF16, align_bytes=64, name="grouped", tag="grouped")
-            words = base_grouped[dt][:].bitcast(F32)
-            for c in range(0, CHUNKS, 2):
-                pairs_to_partitions(base_sb[dt], c, words, W_TAGS[c // 2])
 
         def quantise_base(dt):
             cols = slice(dt * P, (dt + 1) * P)
@@ -247,95 +293,27 @@ def tile_kanblock_pb_kernel(tc, h, grid, w2_base, w2_spline, out):
                 nc.vector.quantize_mx(
                     out=base_codes[:, c, cols].bitcast(FP8X4),
                     scales=base_scales[:, c, cols],
-                    in_=base_grouped[dt][:, c, :, :].rearrange("p d v -> p (d v)"),
+                    in_=grouped["base", dt][:, c, :, :].rearrange("p d v -> p (d v)"),
                 )
-
-        w_sb = {}
-        w_grouped = {}
-
-        def load_spline(unit):
-            c, half = unit
-            row_len = K_PASS * BASES
-            for dt in (2 * half, 2 * half + 1):
-                w_sb[c, dt] = w_rows.tile([P, row_len], BF16, name="w_sb", tag="w_sb")
-                nc.sync.dma_start(out=w_sb[c, dt][:], in_=spline_rows[:, dt, c * row_len : (c + 1) * row_len])
-
-        turned = {}
-        W_TAGS = ("weights_by_scalar", "weights_by_vector")
-
-        def turn_spline(step, i):
-            (c, half), q = step
-            words = w_sb[c, 2 * half + i][:].bitcast(F32).rearrange("p (v i q) -> p v i q", v=PACK, q=PAIRS)
-            for k in range(2):
-                turned[k] = new_bank(W_TAGS[k], [P, PACK, P])
-                for v in range(PACK):
-                    nc.tensor.transpose(turned[k][:, v, :], words[:, v, :, q + k], ident_f32[:])
-
-        def copy_spline(step, i):
-            for k in range(2):
-                if i == 0:
-                    w_grouped[step, k] = w_stage.tile([P, 2, 2 * P, PACK], BF16, align_bytes=64, name="w_grouped", tag="w_grouped")
-                words = w_grouped[step, k][:].bitcast(F32)
-                empty(W_TAGS[1] if k == 1 and i == 1 else W_TAGS[0], words[:, :, i * P : (i + 1) * P, :], turned[k][:].rearrange("p (m v) d -> p m d v", m=2))
-
-        def quantise_spline(step):
-            (c, half), q = step
-            cols = slice(2 * half * P, 2 * (half + 1) * P)
-            for k in range(2):
-                for m in range(2):
-                    nc.vector.quantize_mx(
-                        out=w_codes[:, c, m, q + k, cols].bitcast(FP8X4),
-                        scales=w_scales[:, c, m, q + k, cols],
-                        in_=w_grouped[step, k][:, m, :, :].rearrange("p d v -> p (d v)"),
-                    )
-
-        h_sb = {}
-        x = {}
-        silu_sb = {}
-        silu_grouped = {}
-        silu_codes = {}
-        silu_scales = {}
-        acc = {}
-        folded = {}
-        square = {}
-        tile = {}
-        tail = {}
-        bank = {}
-        drained = {}
-        bases = {}
-        b_codes = {}
-        b_scales = {}
-
-        def load(tt):
-            h_sb[tt] = h_rows.tile([P, FEATURES], BF16, name="h_sb", tag="h_sb")
-            nc.sync.dma_start(out=h_sb[tt][:], in_=h[tt * P : (tt + 1) * P, :])
-
-        def clamp(tt):
-            x[tt] = rows.tile([P, FEATURES], BF16, name="x", tag="x", bufs=2)
-            nc.vector.tensor_scalar(
-                out=x[tt][:], in0=h_sb[tt][:], scalar1=consts_of["knots"][:, 0:1],
-                scalar2=consts_of["knots"][:, KNOTS - 1 : KNOTS], op0=ALU.max, op1=ALU.min,
-            )
 
         def activate(tt, c):
             if c == 0:
-                silu_sb[tt] = rows.tile([P, FEATURES], BF16, name="unquantised", tag="unquantised")
-            cols = slice(c * K_PASS, (c + 1) * K_PASS)
-            nc.scalar.activation(out=silu_sb[tt][:, cols], in_=h_sb[tt][:, cols], func=ACT.Silu)
-
-        def turn_silu(tt, c):
-            if c == 0:
-                silu_grouped[tt] = rows.tile([P, CHUNKS, P, PACK], BF16, align_bytes=64, name="grouped", tag="grouped")
-            pairs_to_partitions(silu_sb[tt], c, silu_grouped[tt][:].bitcast(F32), W_TAGS[c // 2])
+                unquantised[tt] = rows.tile([P, FEATURES], BF16, name="unquantised", tag="unquantised")
+            cols = slice(c * CHUNK, (c + 1) * CHUNK)
+            nc.scalar.activation(out=unquantised[tt][:, cols], in_=h_sb[tt][:, cols], func=ACT.Silu)
 
         def quantise_silu(tt):
-            silu_codes[tt] = rows.tile([P, CHUNKS, P], U32, align_bytes=64, name="silu_codes", tag="silu_codes")
-            silu_scales[tt] = rows.tile([P, CHUNKS, P], U8, align_bytes=64, name="silu_scales", tag="silu_scales")
+            silu_codes[tt] = rows.tile([P, CHUNKS, P], U32, align_bytes=64, name="silu_codes", tag="silu_codes", bufs=TILES_AT_ONCE)
+            silu_scales[tt] = rows.tile([P, CHUNKS, P], U8, align_bytes=64, name="silu_scales", tag="silu_scales", bufs=TILES_AT_ONCE)
             nc.vector.quantize_mx(
                 out=silu_codes[tt][:].rearrange("p c n -> p (c n)").bitcast(FP8X4),
                 scales=silu_scales[tt][:].rearrange("p c n -> p (c n)"),
-                in_=silu_grouped[tt][:].rearrange("p c n v -> p (c n v)"),
+                in_=grouped["silu", tt][:].rearrange("p c n v -> p (c n v)"),
             )
+
+        def load_h(tt):
+            h_sb[tt] = rows.tile([P, FEATURES], BF16, name="h_sb", tag="h_sb", bufs=TILES_AT_ONCE)
+            nc.sync.dma_start(out=h_sb[tt][:], in_=h[tt * P : (tt + 1) * P, :])
 
         def base_product(tt):
             for c in range(CHUNKS):
@@ -354,115 +332,100 @@ def tile_kanblock_pb_kernel(tc, h, grid, w2_base, w2_spline, out):
             nc.scalar.copy(out=result[:], in_=acc[tt][:])
             nc.sync.dma_start(out=out_rows[tt * P : (tt + 1) * P, :], in_=result[:])
 
-        def batch_x(b):
-            first = (b % CHUNKS) * K_PASS
-            return x[b // CHUNKS][:, first : first + K_PASS]
+        def clamp(b):
+            tt, c = batch_place(b)
+            x[b] = work.tile([P, CHUNK], BF16, name="x", tag="x", bufs=3)
+            nc.vector.tensor_scalar(
+                out=x[b][:], in0=h_sb[tt][:, c * CHUNK : (c + 1) * CHUNK], scalar1=column(constant["knots"], 0),
+                scalar2=column(constant["knots"], KNOTS - 1), op0=ALU.max, op1=ALU.min,
+            )
 
         def fold(b, k):
-            folded[b, k] = work.tile([P, K_PASS], F32, name="folded", tag="folded", bufs=2)
-            nc.scalar.activation(out=folded[b, k][:], in_=batch_x(b), func=ACT.Abs, bias=column(consts_of["neg_centre"], k), scale=1.0)
+            folded[b, k] = work.tile([P, CHUNK], F32, name="folded", tag="folded", bufs=2)
+            nc.scalar.activation(out=folded[b, k][:], in_=x[b][:], func=ACT.Abs, bias=column(constant["neg_centre"], k), scale=1.0)
 
         def argument(b, k):
-            return folded[b, k][:] if k < TENTS else batch_x(b)
+            return folded[b, k][:] if k < TENTS else x[b][:]
 
         def make_square(b, k):
-            tag, bufs = ("early_tent", 5) if k < 2 else ("late_tent", 3) if k < TENTS else ("cube", CUBE_BUFS)
-            square[b, k] = work.tile([P, K_PASS], F32, name=tag, tag=tag, bufs=bufs)
-            if k in UNWEIGHTED:
-                bias, scale = column(consts_of["neg_offset"], k), 1.0
+            tag, bufs = (("early_tent", 4) if k < 2 else ("late_tent", 4)) if k < TENTS else ("cube", 6)
+            square[b, k] = work.tile([P, CHUNK], F32, name=tag, tag=tag, bufs=bufs)
+            if k in (0, 4):
+                bias, root = column(constant["neg_offset"], k), 1.0
             else:
-                bias, scale = column(consts_of["bias"], k), column(consts_of["root"], k)
-            nc.scalar.activation(out=square[b, k][:], in_=argument(b, k), func=ACT.Square, bias=bias, scale=scale)
+                bias, root = column(constant["bias"], k), column(constant["root"], k)
+            nc.scalar.activation(out=square[b, k][:], in_=argument(b, k), func=ACT.Square, bias=bias, scale=root)
 
         def make_tile(b, k):
             tile[b, k] = square[b, k]
             nc.vector.scalar_tensor_tensor(
-                out=tile[b, k][:], in0=argument(b, k), scalar=column(consts_of["offset"], k), in1=square[b, k][:],
+                out=tile[b, k][:], in0=argument(b, k), scalar=column(constant["offset"], k), in1=square[b, k][:],
                 op0=ALU.subtract, op1=ALU.mult,
             )
 
-        def tail_key(kind, g):
-            return SHARED.get((kind, g), (kind, g))
-
         def make_tail(b, kind, g):
-            if (kind, g) in SHARED:
+            if (kind, g) in SHARED_TAIL:
                 return
-            source = tile[b, tail_tile(kind, g)][:]
-            tag, bufs = ("shared_tail", 2) if (kind, g) == ("rise", 0) else ("tail", TAIL_BUFS)
-            tail[b, kind, g] = work.tile([P, K_PASS], F32, name=tag, tag=tag, bufs=bufs)
-            into = tail[b, kind, g][:]
-            factor = consts_of["factor_of"](kind, g)
-            if (kind, g) in JOINED:
-                nc.vector.scalar_tensor_tensor(
-                    out=into, in0=source, scalar=0.0, in1=tile[b, lead_tile(kind, g)][:],
-                    op0=ALU.max if tail_is_positive(kind, g) else ALU.min,
-                    op1=ALU.add if tail_is_positive(kind, g) != lead_is_positive(kind, g) else ALU.subtract,
-                )
-            elif (kind, g) in SCALAR_TAILS:
+            tag, bufs = ("shared_tail", 3) if (kind, g) == SHARED_BY_BOTH else ("tail", 8)
+            tail[b, kind, g] = work.tile([P, CHUNK], F32, name=tag, tag=tag, bufs=bufs)
+            into, source = tail[b, kind, g][:], tile[b, tail_tile(kind, g)][:]
+            factor = constant["factor_of"](kind, g)
+            if (kind, g) in TAILS_BY_SCALAR:
                 nc.scalar.activation(out=into, in_=source, func=ACT.Relu, scale=factor)
             else:
                 nc.vector.tensor_scalar(
-                    out=into, in0=source, scalar1=factor, scalar2=0.0,
-                    op0=ALU.mult, op1=ALU.min if lead_is_positive(kind, g) else ALU.max,
+                    out=into, in0=source, scalar1=factor, scalar2=0.0, op0=ALU.mult, op1=ALU.min if lead_is_positive(kind, g) else ALU.max
                 )
 
+        def rise_sum(b, g):
+            return (b, rise_banks, ("rise", b, g), [("rise", g, w) for w in range(PACK)])
+
+        def fall_sum(b, q, m):
+            g = SUMS_OF_FALLS[q]
+            return (b, fall_banks, ("fall", b, q, m), [("fall", g + e, 2 * m + v) for v in range(2) for e in range(PAIR)])
+
         def sum_up(members):
-            for b, tag, key, quarters in members:
-                bank[key] = new_bank(tag, [P, PACK, P])
+            for b, pool, key, quarters in members:
+                bank[key] = pool.tile([P, PACK, P], F32, name="bank", tag="bank")
             for quarter in range(PACK):
-                for part in range(2):
-                    for b, tag, key, quarters in members:
+                for start in (True, False):
+                    for b, pool, key, quarters in members:
                         kind, g, block = quarters[quarter]
-                        cols = slice(block * P, (block + 1) * P)
-                        into = bank[key][:, quarter, :]
-                        tail_sb = tail[(b,) + tail_key(kind, g)]
-                        lead_sb = tile[b, lead_tile(kind, g)]
-                        if (kind, g) in JOINED:
-                            if part == 0:
-                                nc.tensor.transpose(into, tail_sb[:, cols], ident_f32[:])
-                        else:
-                            nc.tensor.matmul(
-                                out=into, lhsT=(tail_sb if part else lead_sb)[:, cols], rhs=ident_f32[:], is_transpose=True,
-                                start=(part == 0), stop=(part == 1),
-                            )
+                        operand = tile[b, lead_tile(kind, g)] if start else tail[(b,) + SHARED_TAIL.get((kind, g), (kind, g))]
+                        nc.tensor.matmul(
+                            out=bank[key][:, quarter, :], lhsT=operand[:, block * P : (block + 1) * P], rhs=ident[:],
+                            is_transpose=True, start=start, stop=not start,
+                        )
 
-        def scalar_member(b, g):
-            return (b, "for_scalar", (b, "rise", g), [("rise", g, v) for v in range(PACK)])
+        def finish_sums(members):
+            for b, pool, key, quarters in members:
+                if key[0] == "rise":
+                    round_rise(b, key[2])
+                else:
+                    finish_bases(b, key[2], key[3])
 
-        def vector_member(b, q, m):
-            g = VECTOR_SUMS[q]
-            return (b, "for_vector", (b, q, m), [("fall", g + e, 2 * m + v) for v in range(2) for e in range(PAIR)])
-
-        def round_sum(b, g):
-            pair = g // PAIR
+        def round_rise(b, g):
             if g % PAIR == 0:
-                drained[b, pair] = work.tile([P, PACK, PAIR, P], BF16, name="drained", tag="drained", bufs=DRAINED_BUFS)
+                risen[b, g // PAIR] = work.tile([P, PACK, PAIR, P], BF16, name="risen", tag="risen", bufs=5)
             nc.scalar.activation(
-                out=drained[b, pair][:, :, g % PAIR, :], in_=bank[b, "rise", g][:], func=ACT.Relu, scale=consts_of["drain_of"]("rise", g),
+                out=risen[b, g // PAIR][:, :, g % PAIR, :], in_=bank["rise", b, g][:], func=ACT.Relu, scale=constant["scale_of"]("rise", g)
             )
 
-        def finish(b, q, m):
-            g = VECTOR_SUMS[q]
+        def finish_bases(b, q, m):
+            g = SUMS_OF_FALLS[q]
             if m == 0:
-                bases[b, q] = operands.tile([P, 2, P, PACK], BF16, align_bytes=64, name="bases", tag="bases", bufs=2)
+                bases[b, q] = operands.tile([P, HALVES, P, PACK], BF16, align_bytes=64, name="bases", tag="bases", bufs=2)
             nc.vector.scalar_tensor_tensor(
                 out=bases[b, q][:, m, :, :],
-                in0=bank[b, q, m][:].rearrange("p w n -> p n w"),
-                scalar=consts_of["drain_of"]("fall", g),
-                in1=drained[b, g // PAIR][:, 2 * m : 2 * m + 2, :, :].rearrange("p v e n -> p n (v e)"),
+                in0=bank["fall", b, q, m][:].rearrange("p w n -> p n w"),
+                scalar=constant["scale_of"]("fall", g),
+                in1=risen[b, g // PAIR][:, 2 * m : 2 * m + 2, :, :].rearrange("p v e n -> p n (v e)"),
                 op0=ALU.mult, op1=ALU.max,
             )
 
-        def take_out(members):
-            for b, tag, key, quarters in members:
-                if tag == "for_scalar":
-                    round_sum(b, key[2])
-                else:
-                    finish(*key)
-
         def quantise_bases(b, q):
-            b_codes[b, q] = operands.tile([P, 2, P], U32, align_bytes=64, name="b_codes", tag="b_codes")
-            b_scales[b, q] = operands.tile([P, 2, P], U8, align_bytes=64, name="b_scales", tag="b_scales")
+            b_codes[b, q] = operands.tile([P, HALVES, P], U32, align_bytes=64, name="b_codes", tag="b_codes")
+            b_scales[b, q] = operands.tile([P, HALVES, P], U8, align_bytes=64, name="b_scales", tag="b_scales")
             nc.vector.quantize_mx(
                 out=b_codes[b, q][:].rearrange("p m n -> p (m n)").bitcast(FP8X4),
                 scales=b_scales[b, q][:].rearrange("p m n -> p (m n)"),
@@ -470,114 +433,117 @@ def tile_kanblock_pb_kernel(tc, h, grid, w2_base, w2_spline, out):
             )
 
         def multiply(b, q):
-            tt, c = b // CHUNKS, b % CHUNKS
-            for m in range(2):
-                first = c == 0 and q == FIRST_VECTOR and m == 0
+            tt, c = batch_place(b)
+            for m in range(HALVES):
+                first = c == 0 and q == min(SUMS_OF_FALLS) and m == 0
                 if first:
                     acc[tt] = sums.tile([P, OUTPUTS], F32, name="acc", tag="acc")
                 nc.tensor.matmul_mx(
                     out=acc[tt][:],
                     lhsT=b_codes[b, q][:, m, :].bitcast(FP8X4),
                     lhsT_scale=b_scales[b, q][:, m, :],
-                    rhs=w_codes[:, c, m, VECTOR_SUMS[q] // PAIR, :].bitcast(FP8X4),
-                    rhs_scale=w_scales[:, c, m, VECTOR_SUMS[q] // PAIR, :],
+                    rhs=w_codes[:, c, m, SUMS_OF_FALLS[q] // PAIR, :].bitcast(FP8X4),
+                    rhs_scale=w_scales[:, c, m, SUMS_OF_FALLS[q] // PAIR, :],
                     start=first,
-                    stop=(c == CHUNKS - 1 and q == LAST - 1 and m == 1),
+                    stop=(c == CHUNKS - 1 and q == max(SUMS_OF_FALLS) and m == HALVES - 1),
                 )
 
-        UNWEIGHTED = (0, 4, 6)
-        CUBE_BUFS = 6
-        TAIL_BUFS = 8
-        DRAINED_BUFS = 5
-        FIRST_VECTOR = 4
-        SHARED = {("fall", 6): ("rise", 0)}
-
         units = [(c, half) for c in range(CHUNKS) for half in range(2)]
-        steps = [(unit, q) for unit in units for q in range(0, PAIRS, 2)]
+        steps = [(unit, q) for unit in units for q in PAIR_ORDER]
+        base_from = len(steps) - 3
 
         with tc.manual_schedule():
-            consts_of = first_constants(nc, consts, grid)
-            load(0)
+            constant = first_constants(nc, consts, grid)
+            load_h(0)
             load_spline(units[0])
             load_spline(units[1])
+            load_h(1)
             late = []
-            for slot in range(-1, STRIDE * (BATCH_COUNT - 1) + LAST + 5):
-                live = [(b, slot - STRIDE * b) for b in range(BATCH_COUNT)]
-                ages = [(tt, slot - TILE_SLOTS * tt) for tt in range(TOKEN_TILES)]
-                now = steps[slot + 1] if slot + 1 < len(steps) else None
-                before = steps[slot] if 0 <= slot < len(steps) else None
-                for tt, age in ages:
-                    if age == -1:
-                        clamp(tt)
-                    if age == TILE_SLOTS + 6:
-                        store(tt)
+            last_slot = STRIDE * (BATCHES - 1) + LAST_PASS + 2
+            for slot in range(-1, last_slot + 1):
+                live = [(b, slot - STRIDE * b) for b in range(BATCHES)]
+                step = steps[slot + 1] if slot + 1 < len(steps) else None
+                step_before = steps[slot] if 0 <= slot < len(steps) else None
                 sums_of = [[], []]
                 for b, q in live:
                     for i in range(2):
-                        if q in SCALAR_SUMS:
-                            sums_of[i].append(scalar_member(b, SCALAR_SUMS[q][i]))
+                        if q in SUMS_OF_RISES:
+                            sums_of[i].append(rise_sum(b, SUMS_OF_RISES[q][i]))
                 for b, q in live:
                     for i in range(2):
-                        if q in VECTOR_SUMS:
-                            sums_of[i].append(vector_member(b, q, i))
-                squares = [(b, q + 1) for b, q in live if 0 <= q + 1 < STRIDE]
-                take_out(late)
-                if before:
-                    copy_spline(before, 1)
-                if slot in (16, 17, 18, 19):
-                    turn_base(slot - 16)
-                for tt, age in ages:
-                    if age in (9, 10):
-                        turn_silu(tt, 2 * (age - 9))
+                        if q in SUMS_OF_FALLS:
+                            sums_of[i].append(fall_sum(b, q, i))
+
+                for tt in range(TOKEN_TILES):
+                    if slot == STRIDE * batch_number(tt, CHUNKS - 1) + LAST_PASS + 2:
+                        store(tt)
                 for b, q in live:
-                    if 0 <= q < STRIDE:
+                    if q == -1:
+                        clamp(b)
+                finish_sums(late)
+                if step_before:
+                    copy_spline(step_before, 1)
+                if base_from <= slot < base_from + OUTPUT_TILES:
+                    turn_words(("base", slot - base_from), base_sb[slot - base_from], 0)
+                for tt in range(TOKEN_TILES):
+                    since = slot - tt // TILES_AT_ONCE * ROUND_SLOTS - tt % TILES_AT_ONCE * 8
+                    if since in (13, 14):
+                        turn_words(("silu", tt), unquantised[tt], since - 13)
+                for b, q in live:
+                    if 0 <= q < TENTS:
                         make_tile(b, q)
                         make_tile(b, q + TENTS)
-                for b, k in squares:
-                    fold(b, k)
-                    make_square(b, k + TENTS)
-                    make_square(b, k)
                 for b, q in live:
-                    for g in SCALAR_SUMS.get(q + 1, ()):
+                    if 0 <= q + 1 < TENTS:
+                        fold(b, q + 1)
+                        make_square(b, q + 1 + TENTS)
+                        make_square(b, q + 1)
+                for b, q in live:
+                    for g in SUMS_OF_RISES.get(q + 1, ()):
                         make_tail(b, "rise", g)
-                    if q + 1 in VECTOR_SUMS:
+                    if q + 1 in SUMS_OF_FALLS:
                         for e in range(PAIR):
-                            make_tail(b, "fall", VECTOR_SUMS[q + 1] + e)
+                            make_tail(b, "fall", SUMS_OF_FALLS[q + 1] + e)
                 sum_up(sums_of[0])
-                if now:
-                    turn_spline(now, 0)
-                take_out(sums_of[0])
-                if before:
-                    quantise_spline(before)
-                if now:
-                    copy_spline(now, 0)
+                if step:
+                    turn_spline(step, 0)
+                finish_sums(sums_of[0])
+                if base_from <= slot < base_from + OUTPUT_TILES:
+                    turn_words(("base", slot - base_from), base_sb[slot - base_from], 1)
+                if step_before:
+                    quantise_spline(step_before)
+                if step:
+                    copy_spline(step, 0)
                 if slot == -1:
-                    add_other_constants(nc, consts, consts_of)
+                    others = other_constants(nc, consts, constant)
+                    for name in others:
+                        constant[name] = others[name]
                 sum_up(sums_of[1])
                 late = sums_of[1]
-                if now:
-                    turn_spline(now, 1)
-                    if slot % 2 == 0:
-                        u = slot // 2 + 2
+                if step:
+                    turn_spline(step, 1)
+                    if (slot + 2) % PAIRS == 0:
+                        u = (slot + 2) // PAIRS + 1
                         if u < len(units):
                             load_spline(units[u])
                         else:
                             load_base(u - len(units))
-                if slot in (16, 17, 18, 19):
-                    quantise_base(slot - 16)
-                for tt, age in ages:
-                    if 4 <= age < 8:
-                        activate(tt, age - 4)
-                    if age == 8 and tt + 1 < TOKEN_TILES:
-                        load(tt + 1)
-                    if age == 11:
+                if base_from <= slot < base_from + OUTPUT_TILES:
+                    quantise_base(slot - base_from)
+                for tt in range(TOKEN_TILES):
+                    since = slot - tt // TILES_AT_ONCE * ROUND_SLOTS - tt % TILES_AT_ONCE * 8
+                    if 8 <= since < 8 + CHUNKS:
+                        activate(tt, since - 8)
+                    if since == 15:
                         quantise_silu(tt)
+                    if slot == STRIDE * batch_number(tt, CHUNKS - 1) and tt + TILES_AT_ONCE < TOKEN_TILES:
+                        load_h(tt + TILES_AT_ONCE)
                 for b, q in live:
-                    if q - 1 in VECTOR_SUMS:
+                    if q - 1 in SUMS_OF_FALLS:
                         quantise_bases(b, q - 1)
-                for tt, age in ages:
-                    if age == TILE_SLOTS + 5:
+                for tt in range(TOKEN_TILES):
+                    if slot == STRIDE * batch_number(tt, CHUNKS - 1) + LAST_PASS:
                         base_product(tt)
                 for b, q in live:
-                    if q - 2 in VECTOR_SUMS:
-                        multiply(b, q - 2)
+                    if q - MULTIPLY_AFTER in SUMS_OF_FALLS:
+                        multiply(b, q - MULTIPLY_AFTER)

@@ -248,6 +248,8 @@ def tile_kanblock_pb_kernel(tc, h, grid, w2_base, w2_spline, out):
             (c, half), q = step
             words = w_sb[c, 2 * half + part][:].bitcast(F32).rearrange("p (v i q) -> p v i q", v=PACK, q=PAIRS)
             bank["spline"] = turn_banks.tile([P, PACK, P], F32, name="turned", tag="turned")
+            if c == 0:
+                nc.tensor.matmul(out=bank["spline"][:, 0, :], lhsT=ident[:], rhs=ident[:], start=True, stop=True)
             for v in range(PACK):
                 nc.tensor.transpose(bank["spline"][:, v, :], words[:, v, :, q], ident[:])
 
@@ -311,9 +313,10 @@ def tile_kanblock_pb_kernel(tc, h, grid, w2_base, w2_spline, out):
                 in_=grouped["silu", tt][:].rearrange("p c n v -> p (c n v)"),
             )
 
-        def load_h(tt):
-            h_sb[tt] = rows.tile([P, FEATURES], BF16, name="h_sb", tag="h_sb", bufs=TILES_AT_ONCE)
-            nc.sync.dma_start(out=h_sb[tt][:], in_=h[tt * P : (tt + 1) * P, :])
+        def load_h(tt, start, stop):
+            if start == 0:
+                h_sb[tt] = rows.tile([P, FEATURES], BF16, name="h_sb", tag="h_sb", bufs=TILES_AT_ONCE)
+            nc.sync.dma_start(out=h_sb[tt][:, start:stop], in_=h[tt * P : (tt + 1) * P, start:stop])
 
         def base_product(tt):
             for c in range(CHUNKS):
@@ -454,10 +457,11 @@ def tile_kanblock_pb_kernel(tc, h, grid, w2_base, w2_spline, out):
 
         with tc.manual_schedule():
             constant = first_constants(nc, consts, grid)
-            load_h(0)
+            load_h(0, 0, CHUNK)
             load_spline(units[0])
+            load_h(0, CHUNK, FEATURES)
             load_spline(units[1])
-            load_h(1)
+            load_h(1, 0, FEATURES)
             late = []
             last_slot = STRIDE * (BATCHES - 1) + LAST_PASS + 2
             for slot in range(-1, last_slot + 1):
@@ -537,12 +541,12 @@ def tile_kanblock_pb_kernel(tc, h, grid, w2_base, w2_spline, out):
                     if since == 15:
                         quantise_silu(tt)
                     if slot == STRIDE * batch_number(tt, CHUNKS - 1) and tt + TILES_AT_ONCE < TOKEN_TILES:
-                        load_h(tt + TILES_AT_ONCE)
+                        load_h(tt + TILES_AT_ONCE, 0, FEATURES)
                 for b, q in live:
                     if q - 1 in SUMS_OF_FALLS:
                         quantise_bases(b, q - 1)
                 for tt in range(TOKEN_TILES):
-                    if slot == STRIDE * batch_number(tt, CHUNKS - 1) + LAST_PASS:
+                    if slot == STRIDE * batch_number(tt, CHUNKS - 1) + (LAST_PASS if tt < TILES_AT_ONCE else 0):
                         base_product(tt)
                 for b, q in live:
                     if q - MULTIPLY_AFTER in SUMS_OF_FALLS:

@@ -42,6 +42,7 @@ PAIR_ORDER = [SUMS_OF_FALLS[q] // PAIR for q in sorted(SUMS_OF_FALLS)]
 
 SHARED_BY_BOTH = ("rise", 0)
 SHARED_TAIL = {("fall", 6): SHARED_BY_BOTH}
+JOINED = ("rise", 5)
 TAILS_BY_SCALAR = (("rise", 0), ("rise", 1), ("rise", 2), ("rise", 3))
 
 FLOPS = 2 * TOKENS * OUTPUTS * (FEATURES + FEATURES * BASES)
@@ -138,13 +139,14 @@ def other_constants(nc, consts, first):
     def weigh(k, value, factor):
         nc.vector.tensor_mul(out=column(weight, k), in0=value, in1=factor)
 
-    for k in (0, 4, 6):
+    for k in (0, 4):
         nc.vector.memset(column(weight, k), 1.0)
     weigh(2, column(rise_ratio, 0), inv_fall_6[:])
     for k in (0, 2):
         weigh(k + 1, column(weight, k), column(step, k + 8 - 3))
-    for k in (4, 6):
-        weigh(k + 1, column(weight, k), column(step, k - 3))
+    weigh(5, column(weight, 4), column(step, 4 - 3))
+    weigh(6, column(weight, 5), column(rise_ratio, 5))
+    weigh(7, column(weight, 6), column(step, 6 - 3))
     nc.vector.tensor_copy(out=weight[:, TILES : 2 * TILES], in_=weight[:, 0:TILES])
 
     root_raw = consts.tile([P, TILES], F32)
@@ -181,7 +183,7 @@ def other_constants(nc, consts, first):
         return column(factor[kind] if positive else negative["factor", kind], g)
 
     def scale_of(kind, g):
-        return column(scale[kind] if lead_is_positive(kind, g) else negative["scale", kind], g)
+        return column(scale[kind] if lead_is_positive(kind, g) and (kind, g) != JOINED else negative["scale", kind], g)
 
     return {"root": root, "bias": bias, "factor_of": factor_of, "scale_of": scale_of}
 
@@ -248,8 +250,6 @@ def tile_kanblock_pb_kernel(tc, h, grid, w2_base, w2_spline, out):
             (c, half), q = step
             words = w_sb[c, 2 * half + part][:].bitcast(F32).rearrange("p (v i q) -> p v i q", v=PACK, q=PAIRS)
             bank["spline"] = turn_banks.tile([P, PACK, P], F32, name="turned", tag="turned")
-            if c == 0:
-                nc.tensor.matmul(out=bank["spline"][:, 0, :], lhsT=ident[:], rhs=ident[:], start=True, stop=True)
             for v in range(PACK):
                 nc.tensor.transpose(bank["spline"][:, v, :], words[:, v, :, q], ident[:])
 
@@ -373,7 +373,9 @@ def tile_kanblock_pb_kernel(tc, h, grid, w2_base, w2_spline, out):
             tail[b, kind, g] = work.tile([P, CHUNK], F32, name=tag, tag=tag, bufs=bufs)
             into, source = tail[b, kind, g][:], tile[b, tail_tile(kind, g)][:]
             factor = constant["factor_of"](kind, g)
-            if (kind, g) in TAILS_BY_SCALAR:
+            if (kind, g) == JOINED:
+                nc.vector.scalar_tensor_tensor(out=into, in0=source, scalar=0.0, in1=tile[b, 5][:], op0=ALU.max, op1=ALU.subtract)
+            elif (kind, g) in TAILS_BY_SCALAR:
                 nc.scalar.activation(out=into, in_=source, func=ACT.Relu, scale=factor)
             else:
                 nc.vector.tensor_scalar(
@@ -390,15 +392,19 @@ def tile_kanblock_pb_kernel(tc, h, grid, w2_base, w2_spline, out):
         def sum_up(members):
             for b, pool, key, quarters in members:
                 bank[key] = pool.tile([P, PACK, P], F32, name="bank", tag="bank")
-            for quarter in range(PACK):
-                for start in (True, False):
-                    for b, pool, key, quarters in members:
+            for b, pool, key, quarters in members:
+                for quarter in range(PACK):
+                    for start in (True, False):
                         kind, g, block = quarters[quarter]
                         operand = tile[b, lead_tile(kind, g)] if start else tail[(b,) + SHARED_TAIL.get((kind, g), (kind, g))]
-                        nc.tensor.matmul(
-                            out=bank[key][:, quarter, :], lhsT=operand[:, block * P : (block + 1) * P], rhs=ident[:],
-                            is_transpose=True, start=start, stop=not start,
-                        )
+                        if (kind, g) == JOINED:
+                            if start:
+                                nc.tensor.transpose(bank[key][:, quarter, :], tail[b, kind, g][:, block * P : (block + 1) * P], ident[:])
+                        else:
+                            nc.tensor.matmul(
+                                out=bank[key][:, quarter, :], lhsT=operand[:, block * P : (block + 1) * P], rhs=ident[:],
+                                is_transpose=True, start=start, stop=not start,
+                            )
 
         def finish_sums(members):
             for b, pool, key, quarters in members:
@@ -471,12 +477,12 @@ def tile_kanblock_pb_kernel(tc, h, grid, w2_base, w2_spline, out):
                 sums_of = [[], []]
                 for b, q in live:
                     for i in range(2):
-                        if q in SUMS_OF_RISES:
-                            sums_of[i].append(rise_sum(b, SUMS_OF_RISES[q][i]))
-                for b, q in live:
-                    for i in range(2):
                         if q in SUMS_OF_FALLS:
                             sums_of[i].append(fall_sum(b, q, i))
+                for b, q in live:
+                    for i in range(2):
+                        if q in SUMS_OF_RISES:
+                            sums_of[i].append(rise_sum(b, SUMS_OF_RISES[q][i]))
 
                 for tt in range(TOKEN_TILES):
                     if slot == STRIDE * batch_number(tt, CHUNKS - 1) + LAST_PASS + 2:
@@ -502,6 +508,9 @@ def tile_kanblock_pb_kernel(tc, h, grid, w2_base, w2_spline, out):
                         fold(b, q + 1)
                         make_square(b, q + 1 + TENTS)
                         make_square(b, q + 1)
+                for b, q in live:
+                    if q - 1 in SUMS_OF_FALLS:
+                        quantise_bases(b, q - 1)
                 for b, q in live:
                     for g in SUMS_OF_RISES.get(q + 1, ()):
                         make_tail(b, "rise", g)
@@ -542,9 +551,6 @@ def tile_kanblock_pb_kernel(tc, h, grid, w2_base, w2_spline, out):
                         quantise_silu(tt)
                     if slot == STRIDE * batch_number(tt, CHUNKS - 1) and tt + TILES_AT_ONCE < TOKEN_TILES:
                         load_h(tt + TILES_AT_ONCE, 0, FEATURES)
-                for b, q in live:
-                    if q - 1 in SUMS_OF_FALLS:
-                        quantise_bases(b, q - 1)
                 for tt in range(TOKEN_TILES):
                     if slot == STRIDE * batch_number(tt, CHUNKS - 1) + (LAST_PASS if tt < TILES_AT_ONCE else 0):
                         base_product(tt)

from contextlib import ExitStack

import concourse.masks as masks
import concourse.mybir as mybir

F32 = mybir.dt.float32
BF16 = mybir.dt.bfloat16
U32 = mybir.dt.uint32
U8 = mybir.dt.uint8
FP8X4 = mybir.dt.float8_e4m3fn_x4
ALU = mybir.AluOpType
ACT = mybir.ActivationFunctionType

P = 128
PACK = 4
TOKENS = 512
FEATURES = 2048
OUTPUTS = 512
BASES = 8
KNOTS = 12
PAIR = 2
PAIRS = BASES // PAIR
TOKEN_TILES = TOKENS // P
OUTPUT_TILES = OUTPUTS // P
CHUNK = P * PACK
CHUNKS = FEATURES // CHUNK
HALVES = 2
TILES = 8
TENTS = 4

TILES_AT_ONCE = 2
ROUND = TILES_AT_ONCE * CHUNKS
BATCHES = TOKEN_TILES * CHUNKS
STRIDE = 4
ROUND_SLOTS = STRIDE * ROUND
SUMS_OF_RISES = {2: (0, 4), 3: (1, 5), 4: (2, 6), 5: (3, 7)}
SUMS_OF_FALLS = {4: 0, 5: 4, 6: 2, 7: 6}
MULTIPLY_AFTER = 2
FIRST_PASS = min(SUMS_OF_FALLS) + MULTIPLY_AFTER
LAST_PASS = max(SUMS_OF_FALLS) + MULTIPLY_AFTER
PAIR_ORDER = [SUMS_OF_FALLS[q] // PAIR for q in sorted(SUMS_OF_FALLS)]

SHARED_BY_BOTH = ("rise", 0)
SHARED_TAIL = {("fall", 6): SHARED_BY_BOTH}
JOINED = ("rise", 5)
TAILS_BY_SCALAR = (("rise", 0), ("rise", 1), ("rise", 2), ("rise", 3))

FLOPS = 2 * TOKENS * OUTPUTS * (FEATURES + FEATURES * BASES)


def batch_place(b):
    within = b % ROUND
    return b // ROUND * TILES_AT_ONCE + within % TILES_AT_ONCE, within // TILES_AT_ONCE


def batch_number(tt, c):
    return tt // TILES_AT_ONCE * ROUND + c * TILES_AT_ONCE + tt % TILES_AT_ONCE


def lead_tile(kind, g):
    return g if kind == "rise" else (g + 4) % TILES


def tail_tile(kind, g):
    return (g + 1) % TILES if kind == "rise" else (g + 3) % TILES


def lead_is_positive(kind, g):
    return kind == "rise" and g >= TENTS


def tail_keeps_positive(kind, g):
    return g >= 3 if kind == "rise" else g == 0


def column(tile, j):
    return tile[:, j : j + 1]


def first_constants(nc, consts, grid):
    knots_bf = consts.tile([P, KNOTS], BF16)
    nc.sync.dma_start(out=knots_bf[:], in_=grid.partition_broadcast(P))
    knots = consts.tile([P, KNOTS], F32)
    nc.vector.tensor_copy(out=knots[:], in_=knots_bf[:])
    ends = consts.tile([P, TENTS], F32)
    nc.vector.tensor_add(out=ends[:], in0=knots[:, 0:TENTS], in1=knots[:, 8 : 8 + TENTS])
    width = consts.tile([P, TENTS], F32)
    nc.vector.tensor_sub(out=width[:], in0=knots[:, 8 : 8 + TENTS], in1=knots[:, 0:TENTS])
    neg_centre = consts.tile([P, TENTS], F32)
    nc.vector.tensor_scalar_mul(out=neg_centre[:], in0=ends[:], scalar1=-0.5)
    offset = consts.tile([P, TILES], F32)
    nc.vector.tensor_scalar_mul(out=offset[:, 0:TENTS], in0=width[:], scalar1=0.5)
    nc.vector.tensor_copy(out=offset[:, TENTS:TILES], in_=knots[:, TENTS:TILES])
    neg_offset = consts.tile([P, TILES], F32)
    nc.vector.tensor_scalar_mul(out=neg_offset[:], in0=offset[:], scalar1=-1.0)
    return {"knots": knots, "neg_centre": neg_centre, "offset": offset, "neg_offset": neg_offset}


def other_constants(nc, consts, first):
    knots = first["knots"]

    def product(name, *factors):
        value = factors[0]
        for i in range(1, len(factors)):
            out = consts.tile([P, BASES], F32, name="%s_%d" % (name, i))
            nc.vector.tensor_mul(out=out[:], in0=value, in1=factors[i])
            value = out[:]
        return value

    span = {}
    for width in range(1, 5):
        span[width] = consts.tile([P, KNOTS - width], F32, name="span%d" % width)
        nc.vector.tensor_sub(out=span[width][:], in0=knots[:, width:KNOTS], in1=knots[:, 0 : KNOTS - width])
    inv_span1 = consts.tile([P, KNOTS - 1], F32)
    nc.vector.reciprocal(out=inv_span1[:], in_=span[1][:])

    count = BASES + 1
    down_two = consts.tile([P, count], F32)
    nc.vector.tensor_mul(out=down_two[:], in0=span[1][:, 2 : 2 + count], in1=span[2][:, 1 : 1 + count])
    up_two = consts.tile([P, count], F32)
    nc.vector.tensor_mul(out=up_two[:], in0=span[1][:, 0:count], in1=span[2][:, 0:count])
    inv_down = consts.tile([P, count], F32)
    nc.vector.tensor_mul(out=inv_down[:], in0=down_two[:], in1=span[3][:, 0:count])
    inv_up = consts.tile([P, count], F32)
    nc.vector.tensor_mul(out=inv_up[:], in0=up_two[:], in1=span[3][:, 0:count])
    down = consts.tile([P, count], F32)
    nc.vector.reciprocal(out=down[:], in_=inv_down[:])
    up = consts.tile([P, count], F32)
    nc.vector.reciprocal(out=up[:], in_=inv_up[:])

    rise_ratio = product("rise_ratio", span[4][:], inv_span1[:, 0:BASES], inv_up[:, 0:BASES], up[:, 1 : 1 + BASES])
    fall_ratio = product("fall_ratio", span[4][:], inv_span1[:, 3 : 3 + BASES], inv_down[:, 1 : 1 + BASES], down[:, 0:BASES])

    weight = consts.tile([P, 2 * TILES], F32)
    step = product("step", down[:, 1 : 1 + BASES], inv_down[:, 0:BASES])
    inv_fall_6 = consts.tile([P, 1], F32)
    nc.vector.reciprocal(out=inv_fall_6[:], in_=column(fall_ratio, 6))

    def weigh(k, value, factor):
        nc.vector.tensor_mul(out=column(weight, k), in0=value, in1=factor)

    for k in (0, 4):
        nc.vector.memset(column(weight, k), 1.0)
    weigh(2, column(rise_ratio, 0), inv_fall_6[:])
    for k in (0, 2):
        weigh(k + 1, column(weight, k), column(step, k + 8 - 3))
    weigh(5, column(weight, 4), column(step, 4 - 3))
    weigh(6, column(weight, 5), column(rise_ratio, 5))
    weigh(7, column(weight, 6), column(step, 6 - 3))
    nc.vector.tensor_copy(out=weight[:, TILES : 2 * TILES], in_=weight[:, 0:TILES])

    root_raw = consts.tile([P, TILES], F32)
    nc.scalar.sqrt(out=root_raw[:], in_=weight[:, 0:TILES])
    inv_weight = consts.tile([P, 2 * TILES], F32)
    nc.vector.reciprocal(out=inv_weight[:], in_=weight[:])
    inv_root = consts.tile([P, TILES], F32)
    nc.vector.reciprocal(out=inv_root[:], in_=root_raw[:])
    root_other = consts.tile([P, TILES], F32)
    nc.vector.tensor_mul(out=root_other[:], in0=inv_root[:], in1=weight[:, 0:TILES])
    root_sum = consts.tile([P, TILES], F32)
    nc.vector.tensor_add(out=root_sum[:], in0=root_raw[:], in1=root_other[:])
    root = consts.tile([P, TILES], F32)
    nc.vector.tensor_scalar_mul(out=root[:], in0=root_sum[:], scalar1=0.5)
    bias = consts.tile([P, TILES], F32)
    nc.vector.tensor_mul(out=bias[:], in0=first["neg_offset"][:], in1=root[:])

    factor = {
        "rise": product("rise_factor", rise_ratio, weight[:, 0:BASES], inv_weight[:, 1 : 1 + BASES]),
        "fall": product("fall_factor", fall_ratio, weight[:, 4 : 4 + BASES], inv_weight[:, 3 : 3 + BASES]),
    }
    scale = {
        "rise": product("rise_scale", up[:, 0:BASES], inv_weight[:, 0:BASES]),
        "fall": product("fall_scale", down[:, 1 : 1 + BASES], inv_weight[:, 4 : 4 + BASES]),
    }
    negative = {}
    for kind in ("rise", "fall"):
        for name, value in (("factor", factor[kind]), ("scale", scale[kind])):
            negative[name, kind] = consts.tile([P, BASES], F32, name="neg_%s_%s" % (name, kind))
            nc.vector.tensor_scalar_mul(out=negative[name, kind][:], in0=value, scalar1=-1.0)

    def factor_of(kind, g):
        positive = tail_keeps_positive(kind, g) != lead_is_positive(kind, g)
        return column(factor[kind] if positive else negative["factor", kind], g)

    def scale_of(kind, g):
        return column(scale[kind] if lead_is_positive(kind, g) and (kind, g) != JOINED else negative["scale", kind], g)

    return {"root": root, "bias": bias, "factor_of": factor_of, "scale_of": scale_of}


def tile_kanblock_pb_kernel(tc, h, grid, w2_base, w2_spline, out):
    nc = tc.nc
    out_rows = out.flatten_outer_dims()
    spline_rows = w2_spline.rearrange("(dt p) i g -> p dt (i g)", p=P)

    with ExitStack() as ctx:
        consts = ctx.enter_context(tc.tile_pool(name="consts", bufs=1))
        keep = ctx.enter_context(tc.tile_pool(name="keep", bufs=1))
        w_rows = ctx.enter_context(tc.tile_pool(name="w_rows", bufs=4))
        rows = ctx.enter_context(tc.tile_pool(name="rows", bufs=1))
        work = ctx.enter_context(tc.tile_pool(name="work", bufs=1))
        operands = ctx.enter_context(tc.tile_pool(name="operands", bufs=4))
        sums = ctx.enter_context(tc.psum_pool(name="sums", bufs=TILES_AT_ONCE))
        rise_banks = ctx.enter_context(tc.psum_pool(name="rise_banks", bufs=2))
        fall_banks = ctx.enter_context(tc.psum_pool(name="fall_banks", bufs=2))
        turn_banks = ctx.enter_context(tc.psum_pool(name="turn_banks", bufs=2))

        ident = consts.tile([P, P], F32)
        masks.make_identity(nc, ident[:])
        base_codes = keep.tile([P, CHUNKS, OUTPUTS], U32, align_bytes=64)
        base_scales = keep.tile([P, CHUNKS, OUTPUTS], U8, align_bytes=64)
        w_codes = keep.tile([P, CHUNKS, HALVES, PAIRS, OUTPUTS], U32, align_bytes=64)
        w_scales = keep.tile([P, CHUNKS, HALVES, PAIRS, OUTPUTS], U8, align_bytes=64)

        constant = {}
        w_sb = {}
        w_grouped = {}
        base_sb = {}
        unquantised = {}
        grouped = {}
        silu_codes = {}
        silu_scales = {}
        h_sb = {}
        x = {}
        acc = {}
        folded = {}
        square = {}
        tile = {}
        tail = {}
        bank = {}
        risen = {}
        bases = {}
        b_codes = {}
        b_scales = {}

        def take_out(out, in_, by_vector):
            if by_vector:
                nc.vector.tensor_copy(out=out, in_=in_)
            else:
                nc.scalar.copy(out=out, in_=in_)

        def load_spline(unit):
            c, half = unit
            row_len = CHUNK * BASES
            for dt in (2 * half, 2 * half + 1):
                w_sb[c, dt] = w_rows.tile([P, row_len], BF16, name="w_sb", tag="w_sb")
                nc.sync.dma_start(out=w_sb[c, dt][:], in_=spline_rows[:, dt, c * row_len : (c + 1) * row_len])

        def turn_spline(step, part):
            (c, half), q = step
            words = w_sb[c, 2 * half + part][:].bitcast(F32).rearrange("p (v i q) -> p v i q", v=PACK, q=PAIRS)
            bank["spline"] = turn_banks.tile([P, PACK, P], F32, name="turned", tag="turned")
            for v in range(PACK):
                nc.tensor.transpose(bank["spline"][:, v, :], words[:, v, :, q], ident[:])

        def copy_spline(step, part):
            if part == 0:
                w_grouped[step] = w_rows.tile([P, HALVES, 2 * P, PACK], BF16, align_bytes=64, name="w_grouped", tag="w_grouped", bufs=2)
            take_out(
                w_grouped[step][:].bitcast(F32)[:, :, part * P : (part + 1) * P, :],
                bank["spline"][:].rearrange("p (m v) d -> p m d v", m=HALVES),
                by_vector=part == 1 and q % 2 == 0,
            )

        def quantise_spline(step):
            (c, half), q = step
            cols = slice(2 * half * P, 2 * (half + 1) * P)
            for m in range(HALVES):
                nc.vector.quantize_mx(
                    out=w_codes[:, c, m, q, cols].bitcast(FP8X4),
                    scales=w_scales[:, c, m, q, cols],
                    in_=w_grouped[step][:, m, :, :].rearrange("p d v -> p (d v)"),
                )

        def turn_words(key, rows_sb, part):
            if part == 0:
                grouped[key] = rows.tile([P, CHUNKS, P, PACK], BF16, align_bytes=64, name="grouped", tag="grouped")
            words = rows_sb[:].bitcast(F32)
            chunks = slice(2 * part, 2 * part + 2)
            turned = turn_banks.tile([P, 2, PAIR, P], F32, name="turned", tag="turned")
            for cc in range(2):
                for u in range(PAIR):
                    start = ((2 * part + cc) * PAIR + u) * P
                    nc.tensor.transpose(turned[:, cc, u, :], words[:, start : start + P], ident[:])
            take_out(grouped[key][:].bitcast(F32)[:, chunks, :, :], turned[:].rearrange("p c u r -> p c r u"), by_vector=part == 1)

        def load_base(half):
            for dt in (2 * half, 2 * half + 1):
                base_sb[dt] = w_rows.tile([P, FEATURES], BF16, name="w_sb", tag="w_sb")
                nc.sync.dma_start(out=base_sb[dt][:], in_=w2_base[dt * P : (dt + 1) * P, :])

        def quantise_base(dt):
            cols = slice(dt * P, (dt + 1) * P)
            for c in range(CHUNKS):
                nc.vector.quantize_mx(
                    out=base_codes[:, c, cols].bitcast(FP8X4),
                    scales=base_scales[:, c, cols],
                    in_=grouped["base", dt][:, c, :, :].rearrange("p d v -> p (d v)"),
                )

        def activate(tt, c):
            if c == 0:
                unquantised[tt] = rows.tile([P, FEATURES], BF16, name="unquantised", tag="unquantised")
            cols = slice(c * CHUNK, (c + 1) * CHUNK)
            nc.scalar.activation(out=unquantised[tt][:, cols], in_=h_sb[tt][:, cols], func=ACT.Silu)

        def quantise_silu(tt):
            silu_codes[tt] = rows.tile([P, CHUNKS, P], U32, align_bytes=64, name="silu_codes", tag="silu_codes", bufs=TILES_AT_ONCE)
            silu_scales[tt] = rows.tile([P, CHUNKS, P], U8, align_bytes=64, name="silu_scales", tag="silu_scales", bufs=TILES_AT_ONCE)
            nc.vector.quantize_mx(
                out=silu_codes[tt][:].rearrange("p c n -> p (c n)").bitcast(FP8X4),
                scales=silu_scales[tt][:].rearrange("p c n -> p (c n)"),
                in_=grouped["silu", tt][:].rearrange("p c n v -> p (c n v)"),
            )

        def load_h(tt, start, stop):
            if start == 0:
                h_sb[tt] = rows.tile([P, FEATURES], BF16, name="h_sb", tag="h_sb", bufs=TILES_AT_ONCE)
            nc.sync.dma_start(out=h_sb[tt][:, start:stop], in_=h[tt * P : (tt + 1) * P, start:stop])

        def base_product(tt):
            for c in range(CHUNKS):
                nc.tensor.matmul_mx(
                    out=acc[tt][:],
                    lhsT=silu_codes[tt][:, c, :].bitcast(FP8X4),
                    lhsT_scale=silu_scales[tt][:, c, :],
                    rhs=base_codes[:, c, :].bitcast(FP8X4),
                    rhs_scale=base_scales[:, c, :],
                    start=False,
                    stop=False,
                )

        def store(tt):
            result = rows.tile([P, OUTPUTS], F32, name="result", tag="result")
            nc.scalar.copy(out=result[:], in_=acc[tt][:])
            nc.sync.dma_start(out=out_rows[tt * P : (tt + 1) * P, :], in_=result[:])

        def clamp(b):
            tt, c = batch_place(b)
            x[b] = work.tile([P, CHUNK], BF16, name="x", tag="x", bufs=3)
            nc.vector.tensor_scalar(
                out=x[b][:], in0=h_sb[tt][:, c * CHUNK : (c + 1) * CHUNK], scalar1=column(constant["knots"], 0),
                scalar2=column(constant["knots"], KNOTS - 1), op0=ALU.max, op1=ALU.min,
            )

        def fold(b, k):
            folded[b, k] = work.tile([P, CHUNK], F32, name="folded", tag="folded", bufs=2)
            nc.scalar.activation(out=folded[b, k][:], in_=x[b][:], func=ACT.Abs, bias=column(constant["neg_centre"], k), scale=1.0)

        def argument(b, k):
            return folded[b, k][:] if k < TENTS else x[b][:]

        def make_square(b, k):
            tag, bufs = (("early_tent", 4) if k < 2 else ("late_tent", 4)) if k < TENTS else ("cube", 6)
            square[b, k] = work.tile([P, CHUNK], F32, name=tag, tag=tag, bufs=bufs)
            if k in (0, 4):
                bias, root = column(constant["neg_offset"], k), 1.0
            else:
                bias, root = column(constant["bias"], k), column(constant["root"], k)
            nc.scalar.activation(out=square[b, k][:], in_=argument(b, k), func=ACT.Square, bias=bias, scale=root)

        def make_tile(b, k):
            tile[b, k] = square[b, k]
            nc.vector.scalar_tensor_tensor(
                out=tile[b, k][:], in0=argument(b, k), scalar=column(constant["offset"], k), in1=square[b, k][:],
                op0=ALU.subtract, op1=ALU.mult,
            )

        def make_tail(b, kind, g):
            if (kind, g) in SHARED_TAIL:
                return
            tag, bufs = ("shared_tail", 3) if (kind, g) == SHARED_BY_BOTH else ("tail", 8)
            tail[b, kind, g] = work.tile([P, CHUNK], F32, name=tag, tag=tag, bufs=bufs)
            into, source = tail[b, kind, g][:], tile[b, tail_tile(kind, g)][:]
            factor = constant["factor_of"](kind, g)
            if (kind, g) == JOINED:
                nc.vector.scalar_tensor_tensor(out=into, in0=source, scalar=0.0, in1=tile[b, 5][:], op0=ALU.max, op1=ALU.subtract)
            elif (kind, g) in TAILS_BY_SCALAR:
                nc.scalar.activation(out=into, in_=source, func=ACT.Relu, scale=factor)
            else:
                nc.vector.tensor_scalar(
                    out=into, in0=source, scalar1=factor, scalar2=0.0, op0=ALU.mult, op1=ALU.min if lead_is_positive(kind, g) else ALU.max
                )

        def rise_sum(b, g):
            return (b, rise_banks, ("rise", b, g), [("rise", g, w) for w in range(PACK)])

        def fall_sum(b, q, m):
            g = SUMS_OF_FALLS[q]
            return (b, fall_banks, ("fall", b, q, m), [("fall", g + e, 2 * m + v) for v in range(2) for e in range(PAIR)])

        def sum_up(members):
            for b, pool, key, quarters in members:
                bank[key] = pool.tile([P, PACK, P], F32, name="bank", tag="bank")
            for b, pool, key, quarters in members:
                for quarter in range(PACK):
                    for start in (True, False):
                        kind, g, block = quarters[quarter]
                        operand = tile[b, lead_tile(kind, g)] if start else tail[(b,) + SHARED_TAIL.get((kind, g), (kind, g))]
                        if (kind, g) == JOINED:
                            if start:
                                nc.tensor.transpose(bank[key][:, quarter, :], tail[b, kind, g][:, block * P : (block + 1) * P], ident[:])
                        else:
                            nc.tensor.matmul(
                                out=bank[key][:, quarter, :], lhsT=operand[:, block * P : (block + 1) * P], rhs=ident[:],
                                is_transpose=True, start=start, stop=not start,
                            )

        def finish_sums(members):
            for b, pool, key, quarters in members:
                if key[0] == "rise":
                    round_rise(b, key[2])
                else:
                    finish_bases(b, key[2], key[3])

        def round_rise(b, g):
            if g % PAIR == 0:
                risen[b, g // PAIR] = work.tile([P, PACK, PAIR, P], BF16, name="risen", tag="risen", bufs=5)
            nc.scalar.activation(
                out=risen[b, g // PAIR][:, :, g % PAIR, :], in_=bank["rise", b, g][:], func=ACT.Relu, scale=constant["scale_of"]("rise", g)
            )

        def finish_bases(b, q, m):
            g = SUMS_OF_FALLS[q]
            if m == 0:
                bases[b, q] = operands.tile([P, HALVES, P, PACK], BF16, align_bytes=64, name="bases", tag="bases", bufs=2)
            nc.vector.scalar_tensor_tensor(
                out=bases[b, q][:, m, :, :],
                in0=bank["fall", b, q, m][:].rearrange("p w n -> p n w"),
                scalar=constant["scale_of"]("fall", g),
                in1=risen[b, g // PAIR][:, 2 * m : 2 * m + 2, :, :].rearrange("p v e n -> p n (v e)"),
                op0=ALU.mult, op1=ALU.max,
            )

        def quantise_bases(b, q):
            b_codes[b, q] = operands.tile([P, HALVES, P], U32, align_bytes=64, name="b_codes", tag="b_codes")
            b_scales[b, q] = operands.tile([P, HALVES, P], U8, align_bytes=64, name="b_scales", tag="b_scales")
            nc.vector.quantize_mx(
                out=b_codes[b, q][:].rearrange("p m n -> p (m n)").bitcast(FP8X4),
                scales=b_scales[b, q][:].rearrange("p m n -> p (m n)"),
                in_=bases[b, q][:].rearrange("p m n v -> p (m n v)"),
            )

        def multiply(b, q):
            tt, c = batch_place(b)
            for m in range(HALVES):
                first = c == 0 and q == min(SUMS_OF_FALLS) and m == 0
                if first:
                    acc[tt] = sums.tile([P, OUTPUTS], F32, name="acc", tag="acc")
                nc.tensor.matmul_mx(
                    out=acc[tt][:],
                    lhsT=b_codes[b, q][:, m, :].bitcast(FP8X4),
                    lhsT_scale=b_scales[b, q][:, m, :],
                    rhs=w_codes[:, c, m, SUMS_OF_FALLS[q] // PAIR, :].bitcast(FP8X4),
                    rhs_scale=w_scales[:, c, m, SUMS_OF_FALLS[q] // PAIR, :],
                    start=first,
                    stop=(c == CHUNKS - 1 and q == max(SUMS_OF_FALLS) and m == HALVES - 1),
                )

        units = [(c, half) for c in range(CHUNKS) for half in range(2)]
        steps = [(unit, q) for unit in units for q in PAIR_ORDER]
        base_from = len(steps) - 3

        with tc.manual_schedule():
            constant = first_constants(nc, consts, grid)
            load_h(0, 0, CHUNK)
            load_spline(units[0])
            load_h(0, CHUNK, FEATURES)
            load_spline(units[1])
            load_h(1, 0, FEATURES)
            late = []
            last_slot = STRIDE * (BATCHES - 1) + LAST_PASS + 2
            for slot in range(-1, last_slot + 1):
                live = [(b, slot - STRIDE * b) for b in range(BATCHES)]
                step = steps[slot + 1] if slot + 1 < len(steps) else None
                step_before = steps[slot] if 0 <= slot < len(steps) else None
                sums_of = [[], []]
                for b, q in live:
                    for i in range(2):
                        if q in SUMS_OF_FALLS:
                            sums_of[i].append(fall_sum(b, q, i))
                for b, q in live:
                    for i in range(2):
                        if q in SUMS_OF_RISES:
                            sums_of[i].append(rise_sum(b, SUMS_OF_RISES[q][i]))

                for tt in range(TOKEN_TILES):
                    if slot == STRIDE * batch_number(tt, CHUNKS - 1) + LAST_PASS + 2:
                        store(tt)
                for b, q in live:
                    if q == -1:
                        clamp(b)
                finish_sums(late)
                if step_before:
                    copy_spline(step_before, 1)
                if base_from <= slot < base_from + OUTPUT_TILES:
                    turn_words(("base", slot - base_from), base_sb[slot - base_from], 0)
                for tt in range(TOKEN_TILES):
                    since = slot - tt // TILES_AT_ONCE * ROUND_SLOTS - tt % TILES_AT_ONCE * 8
                    if since in (13, 14):
                        turn_words(("silu", tt), unquantised[tt], since - 13)
                for b, q in live:
                    if 0 <= q < TENTS:
                        make_tile(b, q)
                        make_tile(b, q + TENTS)
                for b, q in live:
                    if 0 <= q + 1 < TENTS:
                        fold(b, q + 1)
                        make_square(b, q + 1 + TENTS)
                        make_square(b, q + 1)
                for b, q in live:
                    if q - 1 in SUMS_OF_FALLS:
                        quantise_bases(b, q - 1)
                for b, q in live:
                    for g in SUMS_OF_RISES.get(q + 1, ()):
                        make_tail(b, "rise", g)
                    if q + 1 in SUMS_OF_FALLS:
                        for e in range(PAIR):
                            make_tail(b, "fall", SUMS_OF_FALLS[q + 1] + e)
                sum_up(sums_of[0])
                if step:
                    turn_spline(step, 0)
                finish_sums(sums_of[0])
                if base_from <= slot < base_from + OUTPUT_TILES:
                    turn_words(("base", slot - base_from), base_sb[slot - base_from], 1)
                if step_before:
                    quantise_spline(step_before)
                if step:
                    copy_spline(step, 0)
                if slot == -1:
                    others = other_constants(nc, consts, constant)
                    for name in others:
                        constant[name] = others[name]
                sum_up(sums_of[1])
                late = sums_of[1]
                if step:
                    turn_spline(step, 1)
                    if (slot + 2) % PAIRS == 0:
                        u = (slot + 2) // PAIRS + 1
                        if u < len(units):
                            load_spline(units[u])
                        else:
                            load_base(u - len(units))
                if base_from <= slot < base_from + OUTPUT_TILES:
                    quantise_base(slot - base_from)
                for tt in range(TOKEN_TILES):
                    since = slot - tt // TILES_AT_ONCE * ROUND_SLOTS - tt % TILES_AT_ONCE * 8
                    if 8 <= since < 8 + CHUNKS:
                        activate(tt, since - 8)
                    if since == 15:
                        quantise_silu(tt)
                    if slot == STRIDE * batch_number(tt, CHUNKS - 1) and tt + TILES_AT_ONCE < TOKEN_TILES:
                        load_h(tt + TILES_AT_ONCE, 0, FEATURES)
                for tt in range(TOKEN_TILES):
                    if slot == STRIDE * batch_number(tt, CHUNKS - 1) + (LAST_PASS if tt < TILES_AT_ONCE else 0):
                        base_product(tt)
                for b, q in live:
                    if q - MULTIPLY_AFTER in SUMS_OF_FALLS:
                        multiply(b, q - MULTIPLY_AFTER)
